import numpy as np
import ml_dtypes


def mxq(x, axis, fmt="e4m3"):
    dtype, down = {"e4m3": (ml_dtypes.float8_e4m3fn, 7), "e5m2": (ml_dtypes.float8_e5m2, 14)}[fmt]
    v = np.moveaxis(np.asarray(x, np.float32).astype(ml_dtypes.bfloat16).astype(np.float64), axis, -1)
    blocks = v.reshape(v.shape[:-1] + (-1, 32))
    amax = np.abs(blocks).max(-1, keepdims=True)
    byte = np.maximum(np.where(amax > 0, np.frexp(amax)[1] - 1 + 127, 0) - down, 1)
    scale = np.exp2(byte - 127.0)
    codes = (blocks / scale).astype(np.float32).astype(dtype).astype(np.float64)
    return np.moveaxis((codes * scale).reshape(v.shape), -1, axis)


WIDE = False


def mx_kscale(k):
    if not WIDE:
        return np.ones(k)
    levels = np.array([10, -10, 5, -5, 0])
    a = np.random.permutation(np.resize(levels, k // 512 * 4)).reshape(k // 512, 4)
    idx = np.arange(k)
    return np.exp2(a[idx // 512, idx % 128 // 32])


BF16 = ml_dtypes.bfloat16


def bf(x):
    return np.asarray(x, np.float32).astype(BF16)


def f64(x):
    return np.asarray(x).astype(np.float64)


E2M1 = np.array([0.0, 0.5, 1.0, 1.5, 2.0, 3.0, 4.0, 6.0, -0.0, -0.5, -1.0, -1.5, -2.0, -3.0, -4.0, -6.0])


def pack_weight(w, fmt):
    k, n = w.shape
    w = f64(bf(w)).reshape(k // 32, 32, n)
    amax = np.abs(w).max(1)
    if fmt == "e4m3":
        byte = np.frexp(amax)[1] - 1 + 127 - 7
    else:
        mant, ex = np.frexp(amax / 6.0)
        byte = np.where(mant > 0.5, ex, ex - 1) + 127
    byte = np.clip(np.where(amax > 0, byte, 1), 1, 254)
    scaled = (w * np.exp2(127.0 - byte)[:, None, :]).reshape(k, n).astype(np.float32)
    by_word = np.ascontiguousarray(scaled.reshape(k // 512, 128, 4, n).transpose(0, 1, 3, 2))
    if fmt == "e4m3":
        words = by_word.astype(ml_dtypes.float8_e4m3fn).view(np.uint8)
    else:
        c = by_word.astype(ml_dtypes.float4_e2m1fn).view(np.uint8) & 0xF
        words = c[..., 0::2] | (c[..., 1::2] << 4)
    return np.ascontiguousarray(words), np.ascontiguousarray(byte.astype(np.uint8).reshape(k // 512, 16, n))


def unpack_weight(words, scales, fmt):
    g, p, n, _ = words.shape
    if fmt == "e4m3":
        vals = np.ascontiguousarray(words).view(ml_dtypes.float8_e4m3fn).astype(np.float64)
    else:
        nib = np.empty((g, p, n, 4), np.uint8)
        nib[..., 0::2] = words & 0xF
        nib[..., 1::2] = words >> 4
        vals = E2M1[nib]
    vals = vals * np.repeat(np.exp2(scales.astype(np.float64) - 127.0), 8, axis=1)[..., None]
    return vals.transpose(0, 1, 3, 2).reshape(g * 512, n)


B, P, D, NL, T, E, G = 8, 512, 512, 8, 2, 1, 2
WG = NL * NL * T * G
CLIP = 1.0
LOG_2PI = np.log(2.0 * np.pi)
FMT = "e4m3"


def clip(v):
    return np.clip(v, -CLIP, CLIP)


def gaussian_multi(m1, v1, m2, v2):
    v1s = np.exp(2.0 * v1)
    v2s = np.exp(2.0 * v2)
    add = v1s + v2s
    log_add = np.log(add)
    scale = (-0.5 * (LOG_2PI + log_add + (m1 - m2) ** 2 / add)).sum(-1)
    mu = (m1 * v2s + m2 * v1s) / add
    var = v1 + v2 - 0.5 * log_add
    return scale, mu, var


def setup_inputs():
    s = mx_kscale(D)
    x = bf(np.random.standard_normal((B, P, D)) * s)
    s_weight = bf(np.random.standard_normal((B, P, NL, E)))
    s_mu = bf(clip(np.random.standard_normal((B, P, NL, E, G))))
    s_var = bf(clip(np.random.standard_normal((B, P, NL, E, G))))
    tcm_w_words, tcm_w_scales = pack_weight(np.random.standard_normal((D, WG)) / np.sqrt(D) / s[:, None], FMT)
    tcm_b = bf(np.random.standard_normal(WG) * 0.3)
    tcv_w_words, tcv_w_scales = pack_weight(np.random.standard_normal((D, WG)) / np.sqrt(D) / s[:, None], FMT)
    tcv_b = bf(np.random.standard_normal(WG) * 0.3)
    return {"x": x,
            "s_weight": s_weight,
            "s_mu": s_mu,
            "s_var": s_var,
            "tcm_w_words": tcm_w_words,
            "tcm_w_scales": tcm_w_scales,
            "tcm_b": tcm_b,
            "tcv_w_words": tcv_w_words,
            "tcv_w_scales": tcv_w_scales,
            "tcv_b": tcv_b}


def reference(x, s_weight, s_mu, s_var, tcm_w_words, tcm_w_scales, tcm_b, tcv_w_words, tcv_w_scales, tcv_b):
    xq = mxq(f64(x).reshape(B * P, D), 1, "e4m3")
    t_c_mu = clip(((xq @ unpack_weight(tcm_w_words, tcm_w_scales, FMT)) + f64(tcm_b)).reshape(B, P, NL, NL, T, G))[:, :, :, :, :, None, :]
    t_c_var = clip(((xq @ unpack_weight(tcv_w_words, tcv_w_scales, FMT)) + f64(tcv_b)).reshape(B, P, NL, NL, T, G))[:, :, :, :, :, None, :]
    m1 = f64(s_mu)[:, :, None, :, None, :, :]
    v1 = f64(s_var)[:, :, None, :, None, :, :]
    cs_scale, cs_mu, cs_var = gaussian_multi(m1, v1, t_c_mu, t_c_var)
    cs_scale = cs_scale + f64(s_weight)[:, :, None, :, None, :]
    return cs_scale, cs_mu, cs_var

@@ -1,0 +1,319 @@
+import math
+from contextlib import ExitStack
+
+import concourse.mybir as mybir
+from concourse.masks import make_identity
+
+F32 = mybir.dt.float32
+BF16 = mybir.dt.bfloat16
+I32 = mybir.dt.int32
+U32 = mybir.dt.uint32
+U8 = mybir.dt.uint8
+FP8X4 = mybir.dt.float8_e4m3fn_x4
+ALU = mybir.AluOpType
+ACT = mybir.ActivationFunctionType
+
+P = 128
+K = 512
+ROWS = 4096
+SLOTS = ROWS // P
+GROUP = 4
+GROUP_ROWS = GROUP * P
+N_GROUPS = SLOTS // GROUP
+PAIR = 2
+N_PAIRS = N_GROUPS // PAIR
+NL = 8
+JTG = 32
+JT = 16
+WG = NL * JTG
+CHUNKS = 2 * WG // P
+LOG_2PI = math.log(2.0 * math.pi)
+
+FLOPS = 2 * ROWS * K * 2 * WG
+
+
+def tile_chainlveg_pa_t_kernel(
+    tc,
+    x,
+    s_weight,
+    s_mu,
+    s_var,
+    tcm_w_words,
+    tcm_w_scales,
+    tcm_b,
+    tcv_w_words,
+    tcv_w_scales,
+    tcv_b,
+    out_0,
+    out_1,
+    out_2,
+):
+    nc = tc.nc
+
+    x_v = x.flatten_outer_dims().rearrange("(p s) k -> p s k", s=SLOTS)
+    sw_v = s_weight.rearrange("b q j e -> (b q) (j e)").rearrange("(p s) c -> p s c", s=SLOTS)
+    smu_v = s_mu.rearrange("b q j e g -> (b q) (j e g)").rearrange("(p s) c -> p s c", s=SLOTS)
+    svar_v = s_var.rearrange("b q j e g -> (b q) (j e g)").rearrange("(p s) c -> p s c", s=SLOTS)
+    scale_v = out_0.rearrange("b q i j t e -> (b q) (i j t e)").rearrange("(p s) c -> p s c", s=SLOTS)
+    mu_v = out_1.rearrange("b q i j t e g -> (b q) (i j t e g)").rearrange("(p s) c -> p s c", s=SLOTS)
+    var_v = out_2.rearrange("b q i j t e g -> (b q) (i j t e g)").rearrange("(p s) c -> p s c", s=SLOTS)
+
+    with ExitStack() as stack:
+        keep = stack.enter_context(tc.tile_pool(name="keep", bufs=1))
+        x_pool = stack.enter_context(tc.tile_pool(name="x_pool", bufs=N_GROUPS))
+        two = stack.enter_context(tc.tile_pool(name="two", bufs=2))
+        three = stack.enter_context(tc.tile_pool(name="three", bufs=3))
+        four = stack.enter_context(tc.tile_pool(name="four", bufs=4))
+        xt_banks = stack.enter_context(tc.psum_pool(name="xt_banks", bufs=2))
+        acc_banks = stack.enter_context(tc.psum_pool(name="acc_banks", bufs=2))
+        a_banks = stack.enter_context(tc.psum_pool(name="a_banks", bufs=4))
+        stack.enter_context(tc.manual_schedule())
+
+        w_codes = keep.tile([P, 2 * WG], U32, align_bytes=64)
+        w_scales = keep.tile([P, 2 * WG], U8, align_bytes=64)
+        bias_rows = keep.tile([P, P], BF16)
+        half = keep.tile([P, 1], F32)
+        nc.vector.memset(w_scales[:].bitcast(I32), 0)
+        nc.vector.memset(bias_rows[:], 0.0)
+        nc.vector.memset(half[:], 0.5)
+
+        x_sb = []
+        for g in range(N_GROUPS):
+            x_tile = x_pool.tile([P, GROUP, K], BF16, name="x_tile")
+            x_sb.append(x_tile)
+
+        def load_x(g):
+            nc.sync.dma_start(out=x_sb[g][:], in_=x_v[:, GROUP * g : GROUP * (g + 1), :])
+
+        load_x(0)
+        for w, (words, scales) in enumerate(((tcm_w_words, tcm_w_scales), (tcv_w_words, tcv_w_scales))):
+            cols = slice(WG * w, WG * (w + 1))
+            nc.sync.dma_start(
+                out=w_codes[:, cols].bitcast(I32),
+                in_=words[0].rearrange("p n t -> p (n t)").bitcast(I32),
+            )
+            for quad in range(4):
+                nc.sync.dma_start(
+                    out=w_scales[32 * quad : 32 * quad + 4, cols].bitcast(I32),
+                    in_=scales[0][4 * quad : 4 * quad + 4, :].bitcast(I32),
+                )
+        for g in range(1, N_GROUPS):
+            load_x(g)
+
+        smu_raw = keep.tile([P, SLOTS, NL * 2], BF16)
+        svar_raw = keep.tile([P, SLOTS, NL * 2], BF16)
+        sw_raw = keep.tile([P, SLOTS, NL], BF16)
+        nc.scalar.dma_start(out=bias_rows[0:2, :], in_=tcm_b.rearrange("(c n) -> c n", c=2))
+        nc.scalar.dma_start(out=bias_rows[2:4, :], in_=tcv_b.rearrange("(c n) -> c n", c=2))
+        nc.scalar.dma_start(out=svar_raw[:], in_=svar_v)
+        nc.scalar.dma_start(out=smu_raw[:], in_=smu_v)
+        nc.scalar.dma_start(out=sw_raw[:], in_=sw_v)
+
+        ident = keep.tile([P, P], F32)
+        make_identity(nc, ident[:])
+
+        bias_f32 = keep.tile([P, P], F32)
+        nc.vector.tensor_copy(out=bias_f32[:], in_=bias_rows[:])
+        bias_bank = acc_banks.tile([P, GROUP_ROWS], F32, name="acc")
+        nc.tensor.transpose(bias_bank[:, 0:P], bias_f32[:], ident[:])
+        bias_plus1 = keep.tile([P, CHUNKS], F32)
+        nc.vector.tensor_scalar_add(out=bias_plus1[:], in0=bias_bank[:, 0:CHUNKS], scalar1=1.0)
+
+        def spread_over_t(dst, src):
+            nc.vector.tensor_copy(
+                out=dst[:].rearrange("p s (j t g) -> p (s j) t g", t=2, g=2),
+                in_=src[:].rearrange("p s (j g) -> p (s j) g", g=2).unsqueeze(2).to_broadcast([P, SLOTS * NL, 2, 2]),
+            )
+
+        v1 = keep.tile([P, SLOTS, JTG], F32)
+        v1_plus1 = keep.tile([P, SLOTS, JTG], F32)
+        m1 = keep.tile([P, SLOTS, JTG], F32)
+        m1_plus1 = keep.tile([P, SLOTS, JTG], F32)
+        inv_e1 = keep.tile([P, SLOTS, JTG], F32)
+        quarter_inv_e1 = keep.tile([P, SLOTS, JTG], F32)
+        spread_over_t(v1, svar_raw)
+        nc.scalar.activation(out=inv_e1[:], in_=v1[:], func=ACT.Exp, scale=-2.0)
+        nc.vector.tensor_scalar_add(out=v1_plus1[:], in0=v1[:], scalar1=1.0)
+        spread_over_t(m1, smu_raw)
+        nc.vector.tensor_scalar_add(out=m1_plus1[:], in0=m1[:], scalar1=1.0)
+        nc.vector.tensor_scalar_mul(out=quarter_inv_e1[:], in0=inv_e1[:], scalar1=0.25)
+
+        v1_sum = keep.tile([P, SLOTS * NL], F32)
+        base_j = keep.tile([P, SLOTS * NL], F32)
+        base = keep.tile([P, SLOTS, JT], F32)
+        svar_pairs = svar_raw[:].rearrange("p s (j g) -> p (s j) g", g=2)
+        nc.vector.tensor_tensor(out=v1_sum[:], in0=svar_pairs[:, :, 0], in1=svar_pairs[:, :, 1], op=ALU.add)
+        nc.vector.scalar_tensor_tensor(
+            out=base_j[:],
+            in0=sw_raw[:].rearrange("p s j -> p (s j)"),
+            scalar=-LOG_2PI,
+            in1=v1_sum[:],
+            op0=ALU.add,
+            op1=ALU.subtract,
+        )
+        nc.vector.tensor_copy(
+            out=base[:].rearrange("p s (j t) -> p (s j) t", t=2),
+            in_=base_j[:].unsqueeze(2).to_broadcast([P, SLOTS * NL, 2]),
+        )
+
+        grouped = {}
+        x_codes = {}
+        x_scales = {}
+        a_t = {}
+        dm = {}
+        dw = {}
+        th = {}
+        zz = {}
+        ln_rho = {}
+        ln_rho2 = {}
+
+        def over_i(ap):
+            return ap.rearrange("p (i c) -> p i c", i=NL)
+
+        def flat(t):
+            return t[:].rearrange("p s c -> p (s c)")
+
+        def transpose_x(g):
+            grouped[g] = two.tile([P, GROUP_ROWS, 4], BF16, align_bytes=64, name="grouped")
+            words_out = (
+                grouped[g][:].rearrange("p r t -> p (r t)").bitcast(F32).rearrange("p (r u) -> p r u", u=2)
+            )
+            x_words = x_sb[g][:].bitcast(F32)
+            for h in range(2):
+                xt = xt_banks.tile([P, 2, 2 * P], F32, name="xt")
+                for j in range(2):
+                    for u in range(2):
+                        nc.tensor.transpose(
+                            xt[:, u, P * j : P * (j + 1)], x_words[:, 2 * h + j, u : K // 2 : 2], ident[:]
+                        )
+                nc.scalar.copy(
+                    out=words_out[:, 2 * P * h : 2 * P * (h + 1), :], in_=xt[:].rearrange("p u r -> p r u")
+                )
+
+        def quantise_x(g):
+            x_codes[g] = two.tile([P, GROUP_ROWS], U32, align_bytes=64, name="x_codes")
+            x_scales[g] = two.tile([P, GROUP_ROWS], U8, align_bytes=64, name="x_scales")
+            nc.vector.quantize_mx(
+                out=x_codes[g][:].bitcast(FP8X4),
+                scales=x_scales[g][:],
+                in_=grouped[g][:].rearrange("p r t -> p (r t)"),
+            )
+
+        def project(g):
+            a_t[g] = two.tile([P, CHUNKS, GROUP_ROWS], F32, name="a_t")
+            for c in range(CHUNKS):
+                acc = acc_banks.tile([P, GROUP_ROWS], F32, name="acc")
+                nc.tensor.matmul_mx(
+                    out=acc[:],
+                    lhsT=w_codes[:, P * c : P * (c + 1)].bitcast(FP8X4),
+                    lhsT_scale=w_scales[:, P * c : P * (c + 1)],
+                    rhs=x_codes[g][:].bitcast(FP8X4),
+                    rhs_scale=x_scales[g][:],
+                    start=True,
+                    stop=True,
+                )
+                nc.scalar.activation(
+                    out=a_t[g][:, c, :], in_=acc[:], func=ACT.Relu, bias=bias_plus1[:, c : c + 1], scale=1.0
+                )
+
+        def differences(g):
+            dm[g] = two.tile([P, GROUP, WG], F32, name="dm")
+            th[g] = four.tile([P, GROUP, WG], F32, name="th")
+            dw[g] = two.tile([P, GROUP, WG], F32, name="dw")
+            for s in range(GROUP):
+                slot = GROUP * g + s
+                a_rows = a_banks.tile([P, 2 * WG], F32, name="a_rows")
+                for c in range(CHUNKS):
+                    nc.tensor.transpose(
+                        a_rows[:, P * c : P * (c + 1)], a_t[g][:, c, P * s : P * (s + 1)], ident[:]
+                    )
+                for dst, first, state in ((dm[g], 0, m1_plus1), (th[g], WG, v1_plus1)):
+                    nc.vector.scalar_tensor_tensor(
+                        out=over_i(dst[:, s, :]),
+                        in0=over_i(a_rows[:, first : first + WG]),
+                        scalar=2.0,
+                        in1=state[:, slot, :].unsqueeze(1).to_broadcast([P, NL, JTG]),
+                        op0=ALU.min,
+                        op1=ALU.subtract,
+                    )
+            slots = slice(GROUP * g, GROUP * (g + 1))
+            nc.vector.tensor_tensor(
+                out=dw[g][:].rearrange("p s (i c) -> p s i c", i=NL),
+                in0=dm[g][:].rearrange("p s (i c) -> p s i c", i=NL),
+                in1=quarter_inv_e1[:, slots, :].unsqueeze(2).to_broadcast([P, GROUP, NL, JTG]),
+                op=ALU.mult,
+            )
+
+        def tanh(g):
+            nc.scalar.activation(out=flat(th[g]), in_=flat(th[g]), func=ACT.Tanh)
+
+        def mean(g):
+            y2 = two.tile([P, GROUP, WG], F32, name="y2")
+            mu = three.tile([P, GROUP, WG], F32, name="mu")
+            zz[g] = two.tile([P, GROUP, WG], F32, name="zz")
+            nc.vector.scalar_tensor_tensor(
+                out=flat(y2), in0=flat(th[g]), scalar=1.0, in1=flat(dm[g]), op0=ALU.subtract, op1=ALU.mult
+            )
+            for s in range(GROUP):
+                nc.vector.scalar_tensor_tensor(
+                    out=over_i(mu[:, s, :]),
+                    in0=over_i(y2[:, s, :]),
+                    scalar=-0.5,
+                    in1=m1[:, GROUP * g + s, :].unsqueeze(1).to_broadcast([P, NL, JTG]),
+                    op0=ALU.mult,
+                    op1=ALU.add,
+                )
+            nc.sync.dma_start(out=mu_v[:, GROUP * g : GROUP * (g + 1), :], in_=mu[:])
+            nc.vector.tensor_tensor(out=flat(zz[g]), in0=flat(y2), in1=flat(dw[g]), op=ALU.mult)
+
+        def logs(g):
+            ln_rho2[g] = two.tile([P, GROUP, WG], F32, name="ln_rho2")
+            ln_rho[g] = two.tile([P, GROUP, WG], F32, name="ln_rho")
+            nc.scalar.activation(out=flat(ln_rho2[g]), in_=flat(th[g]), func=ACT.Ln, bias=half[:], scale=0.5)
+            nc.scalar.activation(out=flat(ln_rho[g]), in_=flat(th[g]), func=ACT.Ln, bias=half[:], scale=-0.5)
+
+        def deviation_and_weight(g):
+            slots = slice(GROUP * g, GROUP * (g + 1))
+            var = three.tile([P, GROUP, WG], F32, name="var")
+            for s in range(GROUP):
+                nc.vector.scalar_tensor_tensor(
+                    out=over_i(var[:, s, :]),
+                    in0=over_i(ln_rho2[g][:, s, :]),
+                    scalar=0.5,
+                    in1=v1[:, GROUP * g + s, :].unsqueeze(1).to_broadcast([P, NL, JTG]),
+                    op0=ALU.mult,
+                    op1=ALU.add,
+                )
+            nc.sync.dma_start(out=var_v[:, slots, :], in_=var[:])
+            term = two.tile([P, GROUP, WG], F32, name="term")
+            nc.vector.scalar_tensor_tensor(
+                out=flat(term), in0=flat(ln_rho[g]), scalar=0.5, in1=flat(zz[g]), op0=ALU.mult, op1=ALU.add
+            )
+            term_pairs = term[:].rearrange("p s (m g) -> p (s m) g", g=2)
+            term_sum = two.tile([P, GROUP, WG // 2], F32, name="term_sum")
+            nc.vector.tensor_tensor(
+                out=flat(term_sum), in0=term_pairs[:, :, 0], in1=term_pairs[:, :, 1], op=ALU.add
+            )
+            weight = three.tile([P, GROUP, WG // 2], F32, name="weight")
+            nc.vector.tensor_tensor(
+                out=weight[:].rearrange("p s (i c) -> p s i c", i=NL),
+                in0=term_sum[:].rearrange("p s (i c) -> p s i c", i=NL),
+                in1=base[:, slots, :].unsqueeze(2).to_broadcast([P, GROUP, NL, JT]),
+                op=ALU.add,
+            )
+            nc.sync.dma_start(out=scale_v[:, slots, :], in_=weight[:])
+
+        def for_pair(pair, stage):
+            if 0 <= pair < N_PAIRS:
+                for g in range(PAIR * pair, PAIR * (pair + 1)):
+                    stage(g)
+
+        for k in range(-2, N_PAIRS):
+            for_pair(k + 1, project)
+            for_pair(k, mean)
+            for_pair(k + 1, differences)
+            for_pair(k, logs)
+            for_pair(k + 2, transpose_x)
+            for_pair(k + 1, tanh)
+            for_pair(k, deviation_and_weight)
+            for_pair(k + 2, quantise_x)

@@ -164,6 +164,9 @@ def tile_chainlveg_pa_t_kernel(
         dw = {}
         th = {}
         zz = {}
+        y2 = {}
+        term = {}
+        term_sum = {}
         ln_rho = {}
         ln_rho2 = {}
 
@@ -236,35 +239,36 @@ def tile_chainlveg_pa_t_kernel(
                         op0=ALU.min,
                         op1=ALU.subtract,
                     )
-            slots = slice(GROUP * g, GROUP * (g + 1))
-            nc.vector.tensor_tensor(
-                out=dw[g][:].rearrange("p s (i c) -> p s i c", i=NL),
-                in0=dm[g][:].rearrange("p s (i c) -> p s i c", i=NL),
-                in1=quarter_inv_e1[:, slots, :].unsqueeze(2).to_broadcast([P, GROUP, NL, JTG]),
-                op=ALU.mult,
-            )
+                nc.gpsimd.tensor_tensor(
+                    out=over_i(dw[g][:, s, :]),
+                    in0=over_i(dm[g][:, s, :]),
+                    in1=quarter_inv_e1[:, slot, :].unsqueeze(1).to_broadcast([P, NL, JTG]),
+                    op=ALU.mult,
+                )
 
         def tanh(g):
             nc.scalar.activation(out=flat(th[g]), in_=flat(th[g]), func=ACT.Tanh)
 
+        def shift(g):
+            y2[g] = two.tile([P, GROUP, WG], F32, name="y2")
+            nc.vector.scalar_tensor_tensor(
+                out=flat(y2[g]), in0=flat(th[g]), scalar=1.0, in1=flat(dm[g]), op0=ALU.subtract, op1=ALU.mult
+            )
+
         def mean(g):
-            y2 = two.tile([P, GROUP, WG], F32, name="y2")
             mu = three.tile([P, GROUP, WG], F32, name="mu")
             zz[g] = two.tile([P, GROUP, WG], F32, name="zz")
-            nc.vector.scalar_tensor_tensor(
-                out=flat(y2), in0=flat(th[g]), scalar=1.0, in1=flat(dm[g]), op0=ALU.subtract, op1=ALU.mult
-            )
             for s in range(GROUP):
                 nc.vector.scalar_tensor_tensor(
                     out=over_i(mu[:, s, :]),
-                    in0=over_i(y2[:, s, :]),
+                    in0=over_i(y2[g][:, s, :]),
                     scalar=-0.5,
                     in1=m1[:, GROUP * g + s, :].unsqueeze(1).to_broadcast([P, NL, JTG]),
                     op0=ALU.mult,
                     op1=ALU.add,
                 )
             nc.sync.dma_start(out=mu_v[:, GROUP * g : GROUP * (g + 1), :], in_=mu[:])
-            nc.vector.tensor_tensor(out=flat(zz[g]), in0=flat(y2), in1=flat(dw[g]), op=ALU.mult)
+            nc.vector.tensor_tensor(out=flat(zz[g]), in0=flat(y2[g]), in1=flat(dw[g]), op=ALU.mult)
 
         def logs(g):
             ln_rho2[g] = two.tile([P, GROUP, WG], F32, name="ln_rho2")
@@ -272,7 +276,7 @@ def tile_chainlveg_pa_t_kernel(
             nc.scalar.activation(out=flat(ln_rho2[g]), in_=flat(th[g]), func=ACT.Ln, bias=half[:], scale=0.5)
             nc.scalar.activation(out=flat(ln_rho[g]), in_=flat(th[g]), func=ACT.Ln, bias=half[:], scale=-0.5)
 
-        def deviation_and_weight(g):
+        def deviation(g):
             slots = slice(GROUP * g, GROUP * (g + 1))
             var = three.tile([P, GROUP, WG], F32, name="var")
             for s in range(GROUP):
@@ -285,19 +289,24 @@ def tile_chainlveg_pa_t_kernel(
                     op1=ALU.add,
                 )
             nc.sync.dma_start(out=var_v[:, slots, :], in_=var[:])
-            term = two.tile([P, GROUP, WG], F32, name="term")
+            term[g] = two.tile([P, GROUP, WG], F32, name="term")
             nc.vector.scalar_tensor_tensor(
-                out=flat(term), in0=flat(ln_rho[g]), scalar=0.5, in1=flat(zz[g]), op0=ALU.mult, op1=ALU.add
+                out=flat(term[g]), in0=flat(ln_rho[g]), scalar=0.5, in1=flat(zz[g]), op0=ALU.mult, op1=ALU.add
             )
-            term_pairs = term[:].rearrange("p s (m g) -> p (s m) g", g=2)
-            term_sum = two.tile([P, GROUP, WG // 2], F32, name="term_sum")
+
+        def sum_over_g(g):
+            term_pairs = term[g][:].rearrange("p s (m g) -> p (s m) g", g=2)
+            term_sum[g] = two.tile([P, GROUP, WG // 2], F32, name="term_sum")
             nc.vector.tensor_tensor(
-                out=flat(term_sum), in0=term_pairs[:, :, 0], in1=term_pairs[:, :, 1], op=ALU.add
+                out=flat(term_sum[g]), in0=term_pairs[:, :, 0], in1=term_pairs[:, :, 1], op=ALU.add
             )
+
+        def weight_out(g):
+            slots = slice(GROUP * g, GROUP * (g + 1))
             weight = three.tile([P, GROUP, WG // 2], F32, name="weight")
             nc.vector.tensor_tensor(
                 out=weight[:].rearrange("p s (i c) -> p s i c", i=NL),
-                in0=term_sum[:].rearrange("p s (i c) -> p s i c", i=NL),
+                in0=term_sum[g][:].rearrange("p s (i c) -> p s i c", i=NL),
                 in1=base[:, slots, :].unsqueeze(2).to_broadcast([P, GROUP, NL, JT]),
                 op=ALU.add,
             )
@@ -310,10 +319,13 @@ def tile_chainlveg_pa_t_kernel(
 
         for k in range(-2, N_PAIRS):
             for_pair(k + 1, project)
+            for_pair(k, shift)
             for_pair(k, mean)
             for_pair(k + 1, differences)
             for_pair(k, logs)
             for_pair(k + 2, transpose_x)
             for_pair(k + 1, tanh)
-            for_pair(k, deviation_and_weight)
+            for_pair(k, deviation)
+            for_pair(k, sum_over_g)
+            for_pair(k, weight_out)
             for_pair(k + 2, quantise_x)

@@ -64,9 +64,7 @@ def tile_chainlveg_pa_t_kernel(
         two = stack.enter_context(tc.tile_pool(name="two", bufs=2))
         three = stack.enter_context(tc.tile_pool(name="three", bufs=3))
         four = stack.enter_context(tc.tile_pool(name="four", bufs=4))
-        xt_banks = stack.enter_context(tc.psum_pool(name="xt_banks", bufs=2))
-        acc_banks = stack.enter_context(tc.psum_pool(name="acc_banks", bufs=2))
-        a_banks = stack.enter_context(tc.psum_pool(name="a_banks", bufs=4))
+        banks = stack.enter_context(tc.psum_pool(name="banks", bufs=8))
         stack.enter_context(tc.manual_schedule())
 
         w_codes = keep.tile([P, 2 * WG], U32, align_bytes=64)
@@ -76,6 +74,8 @@ def tile_chainlveg_pa_t_kernel(
         nc.vector.memset(w_scales[:].bitcast(I32), 0)
         nc.vector.memset(bias_rows[:], 0.0)
         nc.vector.memset(half[:], 0.5)
+        warm = keep.tile([P, 1], F32)
+        nc.scalar.activation(out=warm[:], in_=half[:], func=ACT.Exp)
 
         x_sb = []
         for g in range(N_GROUPS):
@@ -103,9 +103,9 @@ def tile_chainlveg_pa_t_kernel(
         smu_raw = keep.tile([P, SLOTS, NL * 2], BF16)
         svar_raw = keep.tile([P, SLOTS, NL * 2], BF16)
         sw_raw = keep.tile([P, SLOTS, NL], BF16)
+        nc.scalar.dma_start(out=svar_raw[:], in_=svar_v)
         nc.scalar.dma_start(out=bias_rows[0:2, :], in_=tcm_b.rearrange("(c n) -> c n", c=2))
         nc.scalar.dma_start(out=bias_rows[2:4, :], in_=tcv_b.rearrange("(c n) -> c n", c=2))
-        nc.scalar.dma_start(out=svar_raw[:], in_=svar_v)
         nc.scalar.dma_start(out=smu_raw[:], in_=smu_v)
         nc.scalar.dma_start(out=sw_raw[:], in_=sw_v)
 
@@ -114,7 +114,7 @@ def tile_chainlveg_pa_t_kernel(
 
         bias_f32 = keep.tile([P, P], F32)
         nc.vector.tensor_copy(out=bias_f32[:], in_=bias_rows[:])
-        bias_bank = acc_banks.tile([P, GROUP_ROWS], F32, name="acc")
+        bias_bank = banks.tile([P, GROUP_ROWS], F32, name="bias_bank", tag="bank")
         nc.tensor.transpose(bias_bank[:, 0:P], bias_f32[:], ident[:])
         bias_plus1 = keep.tile([P, CHUNKS], F32)
         nc.vector.tensor_scalar_add(out=bias_plus1[:], in0=bias_bank[:, 0:CHUNKS], scalar1=1.0)
@@ -183,7 +183,7 @@ def tile_chainlveg_pa_t_kernel(
             )
             x_words = x_sb[g][:].bitcast(F32)
             for h in range(2):
-                xt = xt_banks.tile([P, 2, 2 * P], F32, name="xt")
+                xt = banks.tile([P, 2, 2 * P], F32, name="xt", tag="bank")
                 for j in range(2):
                     for u in range(2):
                         nc.tensor.transpose(
@@ -205,7 +205,7 @@ def tile_chainlveg_pa_t_kernel(
         def project(g):
             a_t[g] = two.tile([P, CHUNKS, GROUP_ROWS], F32, name="a_t")
             for c in range(CHUNKS):
-                acc = acc_banks.tile([P, GROUP_ROWS], F32, name="acc")
+                acc = banks.tile([P, GROUP_ROWS], F32, name="acc", tag="bank")
                 nc.tensor.matmul_mx(
                     out=acc[:],
                     lhsT=w_codes[:, P * c : P * (c + 1)].bitcast(FP8X4),
@@ -225,7 +225,7 @@ def tile_chainlveg_pa_t_kernel(
             dw[g] = two.tile([P, GROUP, WG], F32, name="dw")
             for s in range(GROUP):
                 slot = GROUP * g + s
-                a_rows = a_banks.tile([P, 2 * WG], F32, name="a_rows")
+                a_rows = banks.tile([P, 2 * WG], F32, name="a_rows", tag="bank")
                 for c in range(CHUNKS):
                     nc.tensor.transpose(
                         a_rows[:, P * c : P * (c + 1)], a_t[g][:, c, P * s : P * (s + 1)], ident[:]

@@ -71,43 +71,43 @@ def tile_chainlveg_pa_t_kernel(
         w_scales = keep.tile([P, 2 * WG], U8, align_bytes=64)
         bias_rows = keep.tile([P, P], BF16)
         half = keep.tile([P, 1], F32)
-        nc.vector.memset(w_scales[:].bitcast(I32), 0)
         nc.vector.memset(bias_rows[:], 0.0)
+        nc.vector.memset(w_scales[:].bitcast(I32), 0)
         nc.vector.memset(half[:], 0.5)
-        warm = keep.tile([P, 1], F32)
-        nc.scalar.activation(out=warm[:], in_=half[:], func=ACT.Exp)
 
         x_sb = []
         for g in range(N_GROUPS):
             x_tile = x_pool.tile([P, GROUP, K], BF16, name="x_tile")
             x_sb.append(x_tile)
-
-        def load_x(g):
-            nc.sync.dma_start(out=x_sb[g][:], in_=x_v[:, GROUP * g : GROUP * (g + 1), :])
-
-        load_x(0)
-        for w, (words, scales) in enumerate(((tcm_w_words, tcm_w_scales), (tcv_w_words, tcv_w_scales))):
-            cols = slice(WG * w, WG * (w + 1))
-            nc.sync.dma_start(
-                out=w_codes[:, cols].bitcast(I32),
-                in_=words[0].rearrange("p n t -> p (n t)").bitcast(I32),
-            )
-            for quad in range(4):
-                nc.sync.dma_start(
-                    out=w_scales[32 * quad : 32 * quad + 4, cols].bitcast(I32),
-                    in_=scales[0][4 * quad : 4 * quad + 4, :].bitcast(I32),
-                )
-        for g in range(1, N_GROUPS):
-            load_x(g)
-
         smu_raw = keep.tile([P, SLOTS, NL * 2], BF16)
         svar_raw = keep.tile([P, SLOTS, NL * 2], BF16)
         sw_raw = keep.tile([P, SLOTS, NL], BF16)
-        nc.scalar.dma_start(out=svar_raw[:], in_=svar_v)
+
+        def load_x(queue, g):
+            queue.dma_start(out=x_sb[g][:], in_=x_v[:, GROUP * g : GROUP * (g + 1), :])
+
         nc.scalar.dma_start(out=bias_rows[0:2, :], in_=tcm_b.rearrange("(c n) -> c n", c=2))
         nc.scalar.dma_start(out=bias_rows[2:4, :], in_=tcv_b.rearrange("(c n) -> c n", c=2))
+        nc.scalar.dma_start(out=svar_raw[:], in_=svar_v)
         nc.scalar.dma_start(out=smu_raw[:], in_=smu_v)
-        nc.scalar.dma_start(out=sw_raw[:], in_=sw_v)
+        warm = keep.tile([P, 1], F32)
+        nc.scalar.activation(out=warm[:], in_=half[:], func=ACT.Exp)
+        load_x(nc.sync, 0)
+        for w, words in enumerate((tcm_w_words, tcv_w_words)):
+            nc.sync.dma_start(
+                out=w_codes[:, WG * w : WG * (w + 1)].bitcast(I32),
+                in_=words[0].rearrange("p n t -> p (n t)").bitcast(I32),
+            )
+        for w, scales in enumerate((tcm_w_scales, tcv_w_scales)):
+            for quad in range(4):
+                nc.sync.dma_start(
+                    out=w_scales[32 * quad : 32 * quad + 4, WG * w : WG * (w + 1)].bitcast(I32),
+                    in_=scales[0][4 * quad : 4 * quad + 4, :].bitcast(I32),
+                )
+        load_x(nc.scalar, 1)
+        nc.sync.dma_start(out=sw_raw[:], in_=sw_v)
+        for g in range(2, N_GROUPS):
+            load_x(nc.sync, g)
 
         ident = keep.tile([P, P], F32)
         make_identity(nc, ident[:])
@@ -133,27 +133,28 @@ def tile_chainlveg_pa_t_kernel(
         quarter_inv_e1 = keep.tile([P, SLOTS, JTG], F32)
         spread_over_t(v1, svar_raw)
         nc.scalar.activation(out=inv_e1[:], in_=v1[:], func=ACT.Exp, scale=-2.0)
+        nc.gpsimd.tensor_scalar(
+            out=quarter_inv_e1[:], in0=inv_e1[:], scalar1=0.25, scalar2=0.0, op0=ALU.mult, op1=ALU.add
+        )
         nc.vector.tensor_scalar_add(out=v1_plus1[:], in0=v1[:], scalar1=1.0)
         spread_over_t(m1, smu_raw)
         nc.vector.tensor_scalar_add(out=m1_plus1[:], in0=m1[:], scalar1=1.0)
-        nc.vector.tensor_scalar_mul(out=quarter_inv_e1[:], in0=inv_e1[:], scalar1=0.25)
 
         v1_sum = keep.tile([P, SLOTS * NL], F32)
         base_j = keep.tile([P, SLOTS * NL], F32)
         base = keep.tile([P, SLOTS, JT], F32)
         svar_pairs = svar_raw[:].rearrange("p s (j g) -> p (s j) g", g=2)
-        nc.vector.tensor_tensor(out=v1_sum[:], in0=svar_pairs[:, :, 0], in1=svar_pairs[:, :, 1], op=ALU.add)
-        nc.vector.scalar_tensor_tensor(
-            out=base_j[:],
-            in0=sw_raw[:].rearrange("p s j -> p (s j)"),
-            scalar=-LOG_2PI,
-            in1=v1_sum[:],
-            op0=ALU.add,
-            op1=ALU.subtract,
+        nc.gpsimd.tensor_tensor(out=v1_sum[:], in0=svar_pairs[:, :, 0], in1=svar_pairs[:, :, 1], op=ALU.add)
+        nc.gpsimd.tensor_tensor(
+            out=base_j[:], in0=sw_raw[:].rearrange("p s j -> p (s j)"), in1=v1_sum[:], op=ALU.subtract
         )
-        nc.vector.tensor_copy(
+        nc.gpsimd.tensor_scalar(
             out=base[:].rearrange("p s (j t) -> p (s j) t", t=2),
-            in_=base_j[:].unsqueeze(2).to_broadcast([P, SLOTS * NL, 2]),
+            in0=base_j[:].unsqueeze(2).to_broadcast([P, SLOTS * NL, 2]),
+            scalar1=1.0,
+            scalar2=-LOG_2PI,
+            op0=ALU.mult,
+            op1=ALU.add,
         )
 
         grouped = {}

@@ -116,8 +116,11 @@ def tile_chainlveg_pa_t_kernel(
         nc.vector.tensor_copy(out=bias_f32[:], in_=bias_rows[:])
         bias_bank = banks.tile([P, GROUP_ROWS], F32, name="bias_bank", tag="bank")
         nc.tensor.transpose(bias_bank[:, 0:P], bias_f32[:], ident[:])
-        bias_plus1 = keep.tile([P, CHUNKS], F32)
-        nc.vector.tensor_scalar_add(out=bias_plus1[:], in0=bias_bank[:, 0:CHUNKS], scalar1=1.0)
+        relu_bias = keep.tile([P, CHUNKS], F32)
+        nc.vector.tensor_scalar_add(out=relu_bias[:, 0:2], in0=bias_bank[:, 0:2], scalar1=1.0)
+        nc.vector.tensor_scalar(
+            out=relu_bias[:, 2:4], in0=bias_bank[:, 2:4], scalar1=-2.0, scalar2=2.0, op0=ALU.mult, op1=ALU.add
+        )
 
         def spread_over_t(dst, src):
             nc.vector.tensor_copy(
@@ -126,17 +129,19 @@ def tile_chainlveg_pa_t_kernel(
             )
 
         v1 = keep.tile([P, SLOTS, JTG], F32)
-        v1_plus1 = keep.tile([P, SLOTS, JTG], F32)
+        two_less_2v1 = keep.tile([P, SLOTS, JTG], F32)
         m1 = keep.tile([P, SLOTS, JTG], F32)
         m1_plus1 = keep.tile([P, SLOTS, JTG], F32)
         inv_e1 = keep.tile([P, SLOTS, JTG], F32)
-        quarter_inv_e1 = keep.tile([P, SLOTS, JTG], F32)
+        half_inv_e1 = keep.tile([P, SLOTS, JTG], F32)
         spread_over_t(v1, svar_raw)
         nc.scalar.activation(out=inv_e1[:], in_=v1[:], func=ACT.Exp, scale=-2.0)
         nc.gpsimd.tensor_scalar(
-            out=quarter_inv_e1[:], in0=inv_e1[:], scalar1=0.25, scalar2=0.0, op0=ALU.mult, op1=ALU.add
+            out=half_inv_e1[:], in0=inv_e1[:], scalar1=0.5, scalar2=0.0, op0=ALU.mult, op1=ALU.add
         )
-        nc.vector.tensor_scalar_add(out=v1_plus1[:], in0=v1[:], scalar1=1.0)
+        nc.vector.tensor_scalar(
+            out=two_less_2v1[:], in0=v1[:], scalar1=-2.0, scalar2=2.0, op0=ALU.mult, op1=ALU.add
+        )
         spread_over_t(m1, smu_raw)
         nc.vector.tensor_scalar_add(out=m1_plus1[:], in0=m1[:], scalar1=1.0)
 
@@ -166,10 +171,11 @@ def tile_chainlveg_pa_t_kernel(
         th = {}
         zz = {}
         y2 = {}
-        term = {}
-        term_sum = {}
-        ln_rho = {}
+        nd = {}
         ln_rho2 = {}
+        sum_t_bank = {}
+        sum_t = {}
+        sum_bank = {}
 
         def over_i(ap):
             return ap.rearrange("p (i c) -> p i c", i=NL)
@@ -217,12 +223,16 @@ def tile_chainlveg_pa_t_kernel(
                     stop=True,
                 )
                 nc.scalar.activation(
-                    out=a_t[g][:, c, :], in_=acc[:], func=ACT.Relu, bias=bias_plus1[:, c : c + 1], scale=1.0
+                    out=a_t[g][:, c, :],
+                    in_=acc[:],
+                    func=ACT.Relu,
+                    bias=relu_bias[:, c : c + 1],
+                    scale=1.0 if c < 2 else -2.0,
                 )
 
         def differences(g):
             dm[g] = two.tile([P, GROUP, WG], F32, name="dm")
-            th[g] = four.tile([P, GROUP, WG], F32, name="th")
+            nd[g] = four.tile([P, GROUP, WG], F32, name="nd")
             dw[g] = two.tile([P, GROUP, WG], F32, name="dw")
             for s in range(GROUP):
                 slot = GROUP * g + s
@@ -231,11 +241,11 @@ def tile_chainlveg_pa_t_kernel(
                     nc.tensor.transpose(
                         a_rows[:, P * c : P * (c + 1)], a_t[g][:, c, P * s : P * (s + 1)], ident[:]
                     )
-                for dst, first, state in ((dm[g], 0, m1_plus1), (th[g], WG, v1_plus1)):
+                for dst, first, top, state in ((dm[g], 0, 2.0, m1_plus1), (nd[g], WG, 4.0, two_less_2v1)):
                     nc.vector.scalar_tensor_tensor(
                         out=over_i(dst[:, s, :]),
                         in0=over_i(a_rows[:, first : first + WG]),
-                        scalar=2.0,
+                        scalar=top,
                         in1=state[:, slot, :].unsqueeze(1).to_broadcast([P, NL, JTG]),
                         op0=ALU.min,
                         op1=ALU.subtract,
@@ -243,12 +253,13 @@ def tile_chainlveg_pa_t_kernel(
                 nc.gpsimd.tensor_tensor(
                     out=over_i(dw[g][:, s, :]),
                     in0=over_i(dm[g][:, s, :]),
-                    in1=quarter_inv_e1[:, slot, :].unsqueeze(1).to_broadcast([P, NL, JTG]),
+                    in1=half_inv_e1[:, slot, :].unsqueeze(1).to_broadcast([P, NL, JTG]),
                     op=ALU.mult,
                 )
 
         def tanh(g):
-            nc.scalar.activation(out=flat(th[g]), in_=flat(th[g]), func=ACT.Tanh)
+            th[g] = two.tile([P, GROUP, WG], F32, name="th")
+            nc.scalar.activation(out=flat(th[g]), in_=flat(nd[g]), func=ACT.Tanh, scale=-0.5)
 
         def shift(g):
             y2[g] = two.tile([P, GROUP, WG], F32, name="y2")
@@ -273,9 +284,7 @@ def tile_chainlveg_pa_t_kernel(
 
         def logs(g):
             ln_rho2[g] = two.tile([P, GROUP, WG], F32, name="ln_rho2")
-            ln_rho[g] = two.tile([P, GROUP, WG], F32, name="ln_rho")
             nc.scalar.activation(out=flat(ln_rho2[g]), in_=flat(th[g]), func=ACT.Ln, bias=half[:], scale=0.5)
-            nc.scalar.activation(out=flat(ln_rho[g]), in_=flat(th[g]), func=ACT.Ln, bias=half[:], scale=-0.5)
 
         def deviation(g):
             slots = slice(GROUP * g, GROUP * (g + 1))
@@ -290,24 +299,38 @@ def tile_chainlveg_pa_t_kernel(
                     op1=ALU.add,
                 )
             nc.sync.dma_start(out=var_v[:, slots, :], in_=var[:])
-            term[g] = two.tile([P, GROUP, WG], F32, name="term")
-            nc.vector.scalar_tensor_tensor(
-                out=flat(term[g]), in0=flat(ln_rho[g]), scalar=0.5, in1=flat(zz[g]), op0=ALU.mult, op1=ALU.add
-            )
 
-        def sum_over_g(g):
-            term_pairs = term[g][:].rearrange("p s (m g) -> p (s m) g", g=2)
-            term_sum[g] = two.tile([P, GROUP, WG // 2], F32, name="term_sum")
-            nc.vector.tensor_tensor(
-                out=flat(term_sum[g]), in0=term_pairs[:, :, 0], in1=term_pairs[:, :, 1], op=ALU.add
-            )
+        def sum_transposed(g):
+            sum_t_bank[g] = banks.tile([P, GROUP_ROWS], F32, name="sum_t_bank", tag="bank")
+            for s in range(GROUP):
+                parts = [t[g][:, s, e:WG:2] for t in (nd, zz, ln_rho2) for e in range(2)]
+                for n, part in enumerate(parts):
+                    nc.tensor.matmul(
+                        out=sum_t_bank[g][:, P * s : P * (s + 1)],
+                        lhsT=part,
+                        rhs=ident[:],
+                        is_transpose=True,
+                        start=(n == 0),
+                        stop=(n == len(parts) - 1),
+                    )
+
+        def sum_copy(g):
+            sum_t[g] = two.tile([P, GROUP_ROWS], F32, name="sum_t")
+            nc.scalar.mul(out=sum_t[g][:], in_=sum_t_bank[g][:], mul=0.5)
+
+        def sum_back(g):
+            sum_bank[g] = banks.tile([P, GROUP_ROWS], F32, name="sum_bank", tag="bank")
+            for s in range(GROUP):
+                nc.tensor.transpose(
+                    sum_bank[g][:, P * s : P * (s + 1)], sum_t[g][:, P * s : P * (s + 1)], ident[:]
+                )
 
         def weight_out(g):
             slots = slice(GROUP * g, GROUP * (g + 1))
             weight = three.tile([P, GROUP, WG // 2], F32, name="weight")
             nc.vector.tensor_tensor(
                 out=weight[:].rearrange("p s (i c) -> p s i c", i=NL),
-                in0=term_sum[g][:].rearrange("p s (i c) -> p s i c", i=NL),
+                in0=sum_bank[g][:].rearrange("p (s i c) -> p s i c", s=GROUP, i=NL),
                 in1=base[:, slots, :].unsqueeze(2).to_broadcast([P, GROUP, NL, JT]),
                 op=ALU.add,
             )
@@ -318,15 +341,17 @@ def tile_chainlveg_pa_t_kernel(
                 for g in range(PAIR * pair, PAIR * (pair + 1)):
                     stage(g)
 
-        for k in range(-2, N_PAIRS):
+        for k in range(-2, N_PAIRS + 1):
             for_pair(k + 1, project)
+            for_pair(k - 1, sum_back)
             for_pair(k, shift)
             for_pair(k, mean)
+            for_pair(k - 1, weight_out)
             for_pair(k + 1, differences)
             for_pair(k, logs)
             for_pair(k + 2, transpose_x)
             for_pair(k + 1, tanh)
+            for_pair(k, sum_transposed)
             for_pair(k, deviation)
-            for_pair(k, sum_over_g)
-            for_pair(k, weight_out)
+            for_pair(k, sum_copy)
             for_pair(k + 2, quantise_x)

@@ -177,8 +177,14 @@ def tile_chainlveg_pa_t_kernel(
         sum_t = {}
         sum_bank = {}
 
-        def over_i(ap):
-            return ap.rearrange("p (i c) -> p i c", i=NL)
+        def natural(ap):
+            return ap.rearrange("p (i c e) -> p i c e", i=NL, e=2)
+
+        def split(ap):
+            return ap.rearrange("p (e i c) -> p i c e", i=NL, e=2)
+
+        def state_of(tile_, slot):
+            return tile_[:, slot, :].rearrange("p (c e) -> p c e", e=2).unsqueeze(1).to_broadcast([P, NL, JT, 2])
 
         def flat(t):
             return t[:].rearrange("p s c -> p (s c)")
@@ -243,17 +249,20 @@ def tile_chainlveg_pa_t_kernel(
                     )
                 for dst, first, top, state in ((dm[g], 0, 2.0, m1_plus1), (nd[g], WG, 4.0, two_less_2v1)):
                     nc.vector.scalar_tensor_tensor(
-                        out=over_i(dst[:, s, :]),
-                        in0=over_i(a_rows[:, first : first + WG]),
+                        out=split(dst[:, s, :]),
+                        in0=natural(a_rows[:, first : first + WG]),
                         scalar=top,
-                        in1=state[:, slot, :].unsqueeze(1).to_broadcast([P, NL, JTG]),
+                        in1=state_of(state, slot),
                         op0=ALU.min,
                         op1=ALU.subtract,
                     )
                 nc.gpsimd.tensor_tensor(
-                    out=over_i(dw[g][:, s, :]),
-                    in0=over_i(dm[g][:, s, :]),
-                    in1=half_inv_e1[:, slot, :].unsqueeze(1).to_broadcast([P, NL, JTG]),
+                    out=dw[g][:, s, :].rearrange("p (e i c) -> p e i c", e=2, i=NL),
+                    in0=dm[g][:, s, :].rearrange("p (e i c) -> p e i c", e=2, i=NL),
+                    in1=half_inv_e1[:, slot, :]
+                    .rearrange("p (c e) -> p e c", e=2)
+                    .unsqueeze(2)
+                    .to_broadcast([P, 2, NL, JT]),
                     op=ALU.mult,
                 )
 
@@ -272,10 +281,10 @@ def tile_chainlveg_pa_t_kernel(
             zz[g] = two.tile([P, GROUP, WG], F32, name="zz")
             for s in range(GROUP):
                 nc.vector.scalar_tensor_tensor(
-                    out=over_i(mu[:, s, :]),
-                    in0=over_i(y2[g][:, s, :]),
+                    out=natural(mu[:, s, :]),
+                    in0=split(y2[g][:, s, :]),
                     scalar=-0.5,
-                    in1=m1[:, GROUP * g + s, :].unsqueeze(1).to_broadcast([P, NL, JTG]),
+                    in1=state_of(m1, GROUP * g + s),
                     op0=ALU.mult,
                     op1=ALU.add,
                 )
@@ -291,10 +300,10 @@ def tile_chainlveg_pa_t_kernel(
             var = three.tile([P, GROUP, WG], F32, name="var")
             for s in range(GROUP):
                 nc.vector.scalar_tensor_tensor(
-                    out=over_i(var[:, s, :]),
-                    in0=over_i(ln_rho2[g][:, s, :]),
+                    out=natural(var[:, s, :]),
+                    in0=split(ln_rho2[g][:, s, :]),
                     scalar=0.5,
-                    in1=v1[:, GROUP * g + s, :].unsqueeze(1).to_broadcast([P, NL, JTG]),
+                    in1=state_of(v1, GROUP * g + s),
                     op0=ALU.mult,
                     op1=ALU.add,
                 )
@@ -303,7 +312,7 @@ def tile_chainlveg_pa_t_kernel(
         def sum_transposed(g):
             sum_t_bank[g] = banks.tile([P, GROUP_ROWS], F32, name="sum_t_bank", tag="bank")
             for s in range(GROUP):
-                parts = [t[g][:, s, e:WG:2] for t in (nd, zz, ln_rho2) for e in range(2)]
+                parts = [t[g][:, s, P * e : P * (e + 1)] for t in (nd, zz, ln_rho2) for e in range(2)]
                 for n, part in enumerate(parts):
                     nc.tensor.matmul(
                         out=sum_t_bank[g][:, P * s : P * (s + 1)],

@@ -17,11 +17,18 @@ P = 128
 K = 512
 ROWS = 4096
 SLOTS = ROWS // P
-GROUP = 4
-GROUP_ROWS = GROUP * P
-N_GROUPS = SLOTS // GROUP
-PAIR = 2
-N_PAIRS = N_GROUPS // PAIR
+UNIT_SLOTS = (4, 4, 4, 4, 4, 4, 4, 4)
+ROUNDS = ((0, 1), (2, 3), (4, 5), (6, 7))
+X_LOADS = ((0, 4), (4, 4), (8, 4), (12, 4), (16, 4), (20, 4), (24, 4), (28, 4))
+ORDER_EVEN = (("project",1),("sum_back",-1),("shift",0),("mean",0),("differences",1),("weight_out",-1),("logs",0),("transpose_x",2),("tanh",1),("sum_transposed",0),("deviation",0),("sum_copy",0),("quantise_x",2),)
+ORDER_ODD = ORDER_EVEN
+DEPTH = {}
+PROLOGUE = (("state_v",0),("state_exp",0),("transpose_x",0),("quantise_x",0),("transpose_x",1),("project",0),("quantise_x",1),("state_rest",0),("state_base",0),("differences",0),("project",1),("transpose_x",2),("tanh",0),("differences",1),("quantise_x",2),("transpose_x",3),("tanh",1),("quantise_x",3),)
+X_ON_VECTOR = (0, 1)
+DW_ON_VECTOR = False
+W_ON_SCALAR = ()
+BASE_ON_VECTOR = True
+LOAD_ORDER = ("bias",0,"state","sw","warm","codes",1,"scales",2,3,4,5,6,7)
 NL = 8
 JTG = 32
 JT = 16
@@ -60,10 +67,16 @@ def tile_chainlveg_pa_t_kernel(
 
     with ExitStack() as stack:
         keep = stack.enter_context(tc.tile_pool(name="keep", bufs=1))
-        x_pool = stack.enter_context(tc.tile_pool(name="x_pool", bufs=N_GROUPS))
-        two = stack.enter_context(tc.tile_pool(name="two", bufs=2))
-        three = stack.enter_context(tc.tile_pool(name="three", bufs=3))
-        four = stack.enter_context(tc.tile_pool(name="four", bufs=4))
+        pools = {}
+        for depth in (2, 3, 4, 6, 8):
+            pools[depth] = stack.enter_context(tc.tile_pool(name="ring%d" % depth, bufs=depth))
+        default_depth = {"grouped": 2, "x_codes": 2, "x_scales": 2, "a_t": 2, "dm": 2, "dw": 2, "y2": 2, "zz": 2,
+                         "ln_rho2": 2, "sum_t": 2, "mu": 3, "var": 3, "weight": 3, "nd": 4, "th": 2}
+
+        def ring(name, shape, dtype, align=32):
+            return pools[DEPTH.get(name, default_depth[name])].tile(shape, dtype, name=name, align_bytes=align)
+
+        first = [sum(UNIT_SLOTS[:u]) for u in range(len(UNIT_SLOTS))]
         banks = stack.enter_context(tc.psum_pool(name="banks", bufs=8))
         stack.enter_context(tc.manual_schedule())
 
@@ -74,47 +87,68 @@ def tile_chainlveg_pa_t_kernel(
         nc.vector.memset(bias_rows[:], 0.0)
         nc.vector.memset(w_scales[:].bitcast(I32), 0)
         nc.vector.memset(half[:], 0.5)
+        ln_half = keep.tile([P, 1], F32)
+        nc.vector.tensor_scalar(out=ln_half[:], in0=half[:], scalar1=0.0, scalar2=math.log(0.5), op0=ALU.mult, op1=ALU.add)
 
-        x_sb = []
-        for g in range(N_GROUPS):
-            x_tile = x_pool.tile([P, GROUP, K], BF16, name="x_tile")
-            x_sb.append(x_tile)
+        x_all = keep.tile([P, SLOTS, K], BF16)
         smu_raw = keep.tile([P, SLOTS, NL * 2], BF16)
         svar_raw = keep.tile([P, SLOTS, NL * 2], BF16)
         sw_raw = keep.tile([P, SLOTS, NL], BF16)
 
         def load_x(queue, g):
-            queue.dma_start(out=x_sb[g][:], in_=x_v[:, GROUP * g : GROUP * (g + 1), :])
+            s0, n = X_LOADS[g]
+            queue.dma_start(out=x_all[:, s0 : s0 + n, :], in_=x_v[:, s0 : s0 + n, :])
 
-        nc.scalar.dma_start(out=bias_rows[0:2, :], in_=tcm_b.rearrange("(c n) -> c n", c=2))
-        nc.scalar.dma_start(out=bias_rows[2:4, :], in_=tcv_b.rearrange("(c n) -> c n", c=2))
-        nc.scalar.dma_start(out=svar_raw[:], in_=svar_v)
-        nc.scalar.dma_start(out=smu_raw[:], in_=smu_v)
-        warm = keep.tile([P, 1], F32)
-        nc.scalar.activation(out=warm[:], in_=half[:], func=ACT.Exp)
-        load_x(nc.sync, 0)
-        for w, words in enumerate((tcm_w_words, tcv_w_words)):
-            nc.sync.dma_start(
-                out=w_codes[:, WG * w : WG * (w + 1)].bitcast(I32),
-                in_=words[0].rearrange("p n t -> p (n t)").bitcast(I32),
-            )
-        for w, scales in enumerate((tcm_w_scales, tcv_w_scales)):
-            for quad in range(4):
+        def load_bias():
+            nc.scalar.dma_start(out=bias_rows[0:2, :], in_=tcm_b.rearrange("(c n) -> c n", c=2))
+            nc.scalar.dma_start(out=bias_rows[2:4, :], in_=tcv_b.rearrange("(c n) -> c n", c=2))
+
+        def load_state():
+            nc.scalar.dma_start(out=svar_raw[:], in_=svar_v)
+            nc.scalar.dma_start(out=smu_raw[:], in_=smu_v)
+
+        def load_codes():
+            for w, words in enumerate((tcm_w_words, tcv_w_words)):
                 nc.sync.dma_start(
-                    out=w_scales[32 * quad : 32 * quad + 4, WG * w : WG * (w + 1)].bitcast(I32),
-                    in_=scales[0][4 * quad : 4 * quad + 4, :].bitcast(I32),
+                    out=w_codes[:, WG * w : WG * (w + 1)].bitcast(I32),
+                    in_=words[0].rearrange("p n t -> p (n t)").bitcast(I32),
                 )
-        load_x(nc.scalar, 1)
-        nc.sync.dma_start(out=sw_raw[:], in_=sw_v)
-        for g in range(2, N_GROUPS):
-            load_x(nc.sync, g)
+
+        def load_scales(which):
+            for w, scales in which:
+                for quad in range(4):
+                    nc.sync.dma_start(
+                        out=w_scales[32 * quad : 32 * quad + 4, WG * w : WG * (w + 1)].bitcast(I32),
+                        in_=scales[0][4 * quad : 4 * quad + 4, :].bitcast(I32),
+                    )
+
+        warm = keep.tile([P, 1], F32)
+        for what in LOAD_ORDER:
+            if what == "bias":
+                load_bias()
+            elif what == "state":
+                load_state()
+            elif what == "warm":
+                nc.scalar.activation(out=warm[:], in_=half[:], func=ACT.Exp)
+            elif what == "codes":
+                load_codes()
+            elif what == "scales":
+                load_scales(((0, tcm_w_scales), (1, tcv_w_scales)))
+            elif what == "scales_m":
+                load_scales(((0, tcm_w_scales),))
+            elif what == "scales_v":
+                load_scales(((1, tcv_w_scales),))
+            elif what == "sw":
+                nc.sync.dma_start(out=sw_raw[:], in_=sw_v)
+            else:
+                load_x(nc.sync, what)
 
         ident = keep.tile([P, P], F32)
         make_identity(nc, ident[:])
 
         bias_f32 = keep.tile([P, P], F32)
         nc.vector.tensor_copy(out=bias_f32[:], in_=bias_rows[:])
-        bias_bank = banks.tile([P, GROUP_ROWS], F32, name="bias_bank", tag="bank")
+        bias_bank = banks.tile([P, 4 * P], F32, name="bias_bank", tag="bank")
         nc.tensor.transpose(bias_bank[:, 0:P], bias_f32[:], ident[:])
         relu_bias = keep.tile([P, CHUNKS], F32)
         nc.vector.tensor_scalar_add(out=relu_bias[:, 0:2], in0=bias_bank[:, 0:2], scalar1=1.0)
@@ -132,35 +166,61 @@ def tile_chainlveg_pa_t_kernel(
         two_less_2v1 = keep.tile([P, SLOTS, JTG], F32)
         m1 = keep.tile([P, SLOTS, JTG], F32)
         m1_plus1 = keep.tile([P, SLOTS, JTG], F32)
-        inv_e1 = keep.tile([P, SLOTS, JTG], F32)
         half_inv_e1 = keep.tile([P, SLOTS, JTG], F32)
-        spread_over_t(v1, svar_raw)
-        nc.scalar.activation(out=inv_e1[:], in_=v1[:], func=ACT.Exp, scale=-2.0)
-        nc.gpsimd.tensor_scalar(
-            out=half_inv_e1[:], in0=inv_e1[:], scalar1=0.5, scalar2=0.0, op0=ALU.mult, op1=ALU.add
-        )
-        nc.vector.tensor_scalar(
-            out=two_less_2v1[:], in0=v1[:], scalar1=-2.0, scalar2=2.0, op0=ALU.mult, op1=ALU.add
-        )
-        spread_over_t(m1, smu_raw)
-        nc.vector.tensor_scalar_add(out=m1_plus1[:], in0=m1[:], scalar1=1.0)
+        def state_v(u):
+            spread_over_t(v1, svar_raw)
+
+        def state_rest(u):
+            nc.vector.tensor_scalar(
+                out=two_less_2v1[:], in0=v1[:], scalar1=-2.0, scalar2=2.0, op0=ALU.mult, op1=ALU.add
+            )
+            spread_over_t(m1, smu_raw)
+            nc.vector.tensor_scalar_add(out=m1_plus1[:], in0=m1[:], scalar1=1.0)
+
+        if not any(name == "state_v" for name, u in PROLOGUE):
+            state_v(0)
+        def state_exp(u):
+            nc.scalar.activation(out=half_inv_e1[:], in_=v1[:], func=ACT.Exp, scale=-2.0, bias=ln_half[:])
+
+        if not any(name == "state_exp" for name, u in PROLOGUE):
+            state_exp(0)
+        if not any(name == "state_rest" for name, u in PROLOGUE):
+            state_rest(0)
 
         v1_sum = keep.tile([P, SLOTS * NL], F32)
         base_j = keep.tile([P, SLOTS * NL], F32)
         base = keep.tile([P, SLOTS, JT], F32)
         svar_pairs = svar_raw[:].rearrange("p s (j g) -> p (s j) g", g=2)
-        nc.gpsimd.tensor_tensor(out=v1_sum[:], in0=svar_pairs[:, :, 0], in1=svar_pairs[:, :, 1], op=ALU.add)
-        nc.gpsimd.tensor_tensor(
-            out=base_j[:], in0=sw_raw[:].rearrange("p s j -> p (s j)"), in1=v1_sum[:], op=ALU.subtract
-        )
-        nc.gpsimd.tensor_scalar(
-            out=base[:].rearrange("p s (j t) -> p (s j) t", t=2),
-            in0=base_j[:].unsqueeze(2).to_broadcast([P, SLOTS * NL, 2]),
-            scalar1=1.0,
-            scalar2=-LOG_2PI,
-            op0=ALU.mult,
-            op1=ALU.add,
-        )
+
+        def state_base(u):
+            eng = nc.vector if BASE_ON_VECTOR else nc.gpsimd
+            eng.tensor_tensor(out=v1_sum[:], in0=svar_pairs[:, :, 0], in1=svar_pairs[:, :, 1], op=ALU.add)
+            eng.tensor_tensor(
+                out=base_j[:], in0=sw_raw[:].rearrange("p s j -> p (s j)"), in1=v1_sum[:], op=ALU.subtract
+            )
+            eng.tensor_scalar(
+                out=base[:].rearrange("p s (j t) -> p (s j) t", t=2),
+                in0=base_j[:].unsqueeze(2).to_broadcast([P, SLOTS * NL, 2]),
+                scalar1=1.0,
+                scalar2=-LOG_2PI,
+                op0=ALU.mult,
+                op1=ALU.add,
+            )
+
+        if not any(name == "state_base" for name, u in PROLOGUE):
+            state_base(0)
+
+        base_twice = keep.tile([P, SLOTS, WG // 2], F32)
+        for u in W_ON_SCALAR:
+            s0, n = first[u], UNIT_SLOTS[u]
+            nc.gpsimd.tensor_scalar(
+                out=base_twice[:, s0 : s0 + n, :].rearrange("p s (i c) -> p s i c", i=NL),
+                in0=base[:, s0 : s0 + n, :].unsqueeze(2).to_broadcast([P, n, NL, JT]),
+                scalar1=2.0,
+                scalar2=0.0,
+                op0=ALU.mult,
+                op1=ALU.add,
+            )
 
         grouped = {}
         x_codes = {}
@@ -189,76 +249,86 @@ def tile_chainlveg_pa_t_kernel(
         def flat(t):
             return t[:].rearrange("p s c -> p (s c)")
 
-        def transpose_x(g):
-            grouped[g] = two.tile([P, GROUP_ROWS, 4], BF16, align_bytes=64, name="grouped")
+        def transpose_x(u):
+            s0, n = first[u], UNIT_SLOTS[u]
+            grouped[u] = ring("grouped", [P, n * P, 4], BF16, 64)
             words_out = (
-                grouped[g][:].rearrange("p r t -> p (r t)").bitcast(F32).rearrange("p (r u) -> p r u", u=2)
+                grouped[u][:].rearrange("p r t -> p (r t)").bitcast(F32).rearrange("p (r h) -> p r h", h=2)
             )
-            x_words = x_sb[g][:].bitcast(F32)
-            for h in range(2):
-                xt = banks.tile([P, 2, 2 * P], F32, name="xt", tag="bank")
-                for j in range(2):
-                    for u in range(2):
+            x_words = x_all[:, s0 : s0 + n, :].bitcast(F32)
+            for b in range(0, n, 2):
+                m = min(2, n - b)
+                xt = banks.tile([P, 2, m * P], F32, name="xt", tag="bank")
+                for j in range(m):
+                    for h in range(2):
                         nc.tensor.transpose(
-                            xt[:, u, P * j : P * (j + 1)], x_words[:, 2 * h + j, u : K // 2 : 2], ident[:]
+                            xt[:, h, P * j : P * (j + 1)], x_words[:, b + j, h : K // 2 : 2], ident[:]
                         )
-                nc.scalar.copy(
-                    out=words_out[:, 2 * P * h : 2 * P * (h + 1), :], in_=xt[:].rearrange("p u r -> p r u")
-                )
+                if u in X_ON_VECTOR:
+                    nc.vector.tensor_copy(
+                        out=words_out[:, P * b : P * (b + m), :], in_=xt[:].rearrange("p h r -> p r h")
+                    )
+                else:
+                    nc.scalar.copy(
+                        out=words_out[:, P * b : P * (b + m), :], in_=xt[:].rearrange("p h r -> p r h")
+                    )
 
-        def quantise_x(g):
-            x_codes[g] = two.tile([P, GROUP_ROWS], U32, align_bytes=64, name="x_codes")
-            x_scales[g] = two.tile([P, GROUP_ROWS], U8, align_bytes=64, name="x_scales")
+        def quantise_x(u):
+            rows = UNIT_SLOTS[u] * P
+            x_codes[u] = ring("x_codes", [P, rows], U32, 64)
+            x_scales[u] = ring("x_scales", [P, rows], U8, 64)
             nc.vector.quantize_mx(
-                out=x_codes[g][:].bitcast(FP8X4),
-                scales=x_scales[g][:],
-                in_=grouped[g][:].rearrange("p r t -> p (r t)"),
+                out=x_codes[u][:].bitcast(FP8X4),
+                scales=x_scales[u][:],
+                in_=grouped[u][:].rearrange("p r t -> p (r t)"),
             )
 
-        def project(g):
-            a_t[g] = two.tile([P, CHUNKS, GROUP_ROWS], F32, name="a_t")
+        def project(u):
+            rows = UNIT_SLOTS[u] * P
+            a_t[u] = ring("a_t", [P, CHUNKS, rows], F32)
             for c in range(CHUNKS):
-                acc = banks.tile([P, GROUP_ROWS], F32, name="acc", tag="bank")
+                acc = banks.tile([P, rows], F32, name="acc", tag="bank")
                 nc.tensor.matmul_mx(
                     out=acc[:],
                     lhsT=w_codes[:, P * c : P * (c + 1)].bitcast(FP8X4),
                     lhsT_scale=w_scales[:, P * c : P * (c + 1)],
-                    rhs=x_codes[g][:].bitcast(FP8X4),
-                    rhs_scale=x_scales[g][:],
+                    rhs=x_codes[u][:].bitcast(FP8X4),
+                    rhs_scale=x_scales[u][:],
                     start=True,
                     stop=True,
                 )
                 nc.scalar.activation(
-                    out=a_t[g][:, c, :],
+                    out=a_t[u][:, c, :],
                     in_=acc[:],
                     func=ACT.Relu,
                     bias=relu_bias[:, c : c + 1],
                     scale=1.0 if c < 2 else -2.0,
                 )
 
-        def differences(g):
-            dm[g] = two.tile([P, GROUP, WG], F32, name="dm")
-            nd[g] = four.tile([P, GROUP, WG], F32, name="nd")
-            dw[g] = two.tile([P, GROUP, WG], F32, name="dw")
-            for s in range(GROUP):
-                slot = GROUP * g + s
+        def differences(u):
+            s0, n = first[u], UNIT_SLOTS[u]
+            dm[u] = ring("dm", [P, n, WG], F32)
+            nd[u] = ring("nd", [P, n, WG], F32)
+            dw[u] = ring("dw", [P, n, WG], F32)
+            for s in range(n):
+                slot = s0 + s
                 a_rows = banks.tile([P, 2 * WG], F32, name="a_rows", tag="bank")
                 for c in range(CHUNKS):
                     nc.tensor.transpose(
-                        a_rows[:, P * c : P * (c + 1)], a_t[g][:, c, P * s : P * (s + 1)], ident[:]
+                        a_rows[:, P * c : P * (c + 1)], a_t[u][:, c, P * s : P * (s + 1)], ident[:]
                     )
-                for dst, first, top, state in ((dm[g], 0, 2.0, m1_plus1), (nd[g], WG, 4.0, two_less_2v1)):
+                for dst, start_col, top, state in ((dm[u], 0, 2.0, m1_plus1), (nd[u], WG, 4.0, two_less_2v1)):
                     nc.vector.scalar_tensor_tensor(
                         out=split(dst[:, s, :]),
-                        in0=natural(a_rows[:, first : first + WG]),
+                        in0=natural(a_rows[:, start_col : start_col + WG]),
                         scalar=top,
                         in1=state_of(state, slot),
                         op0=ALU.min,
                         op1=ALU.subtract,
                     )
-                nc.gpsimd.tensor_tensor(
-                    out=dw[g][:, s, :].rearrange("p (e i c) -> p e i c", e=2, i=NL),
-                    in0=dm[g][:, s, :].rearrange("p (e i c) -> p e i c", e=2, i=NL),
+                (nc.vector if DW_ON_VECTOR else nc.gpsimd).tensor_tensor(
+                    out=dw[u][:, s, :].rearrange("p (e i c) -> p e i c", e=2, i=NL),
+                    in0=dm[u][:, s, :].rearrange("p (e i c) -> p e i c", e=2, i=NL),
                     in1=half_inv_e1[:, slot, :]
                     .rearrange("p (c e) -> p e c", e=2)
                     .unsqueeze(2)
@@ -266,101 +336,107 @@ def tile_chainlveg_pa_t_kernel(
                     op=ALU.mult,
                 )
 
-        def tanh(g):
-            th[g] = two.tile([P, GROUP, WG], F32, name="th")
-            nc.scalar.activation(out=flat(th[g]), in_=flat(nd[g]), func=ACT.Tanh, scale=-0.5)
+        def tanh(u):
+            th[u] = ring("th", [P, UNIT_SLOTS[u], WG], F32)
+            nc.scalar.activation(out=flat(th[u]), in_=flat(nd[u]), func=ACT.Tanh, scale=-0.5)
 
-        def shift(g):
-            y2[g] = two.tile([P, GROUP, WG], F32, name="y2")
+        def shift(u):
+            y2[u] = ring("y2", [P, UNIT_SLOTS[u], WG], F32)
             nc.vector.scalar_tensor_tensor(
-                out=flat(y2[g]), in0=flat(th[g]), scalar=1.0, in1=flat(dm[g]), op0=ALU.subtract, op1=ALU.mult
+                out=flat(y2[u]), in0=flat(th[u]), scalar=1.0, in1=flat(dm[u]), op0=ALU.subtract, op1=ALU.mult
             )
 
-        def mean(g):
-            mu = three.tile([P, GROUP, WG], F32, name="mu")
-            zz[g] = two.tile([P, GROUP, WG], F32, name="zz")
-            for s in range(GROUP):
+        def mean(u):
+            s0, n = first[u], UNIT_SLOTS[u]
+            mu = ring("mu", [P, n, WG], F32)
+            zz[u] = ring("zz", [P, n, WG], F32)
+            for s in range(n):
                 nc.vector.scalar_tensor_tensor(
                     out=natural(mu[:, s, :]),
-                    in0=split(y2[g][:, s, :]),
+                    in0=split(y2[u][:, s, :]),
                     scalar=-0.5,
-                    in1=state_of(m1, GROUP * g + s),
+                    in1=state_of(m1, s0 + s),
                     op0=ALU.mult,
                     op1=ALU.add,
                 )
-            nc.sync.dma_start(out=mu_v[:, GROUP * g : GROUP * (g + 1), :], in_=mu[:])
-            nc.vector.tensor_tensor(out=flat(zz[g]), in0=flat(y2[g]), in1=flat(dw[g]), op=ALU.mult)
+            nc.sync.dma_start(out=mu_v[:, s0 : s0 + n, :], in_=mu[:])
+            nc.vector.tensor_tensor(out=flat(zz[u]), in0=flat(y2[u]), in1=flat(dw[u]), op=ALU.mult)
 
-        def logs(g):
-            ln_rho2[g] = two.tile([P, GROUP, WG], F32, name="ln_rho2")
-            nc.scalar.activation(out=flat(ln_rho2[g]), in_=flat(th[g]), func=ACT.Ln, bias=half[:], scale=0.5)
+        def logs(u):
+            ln_rho2[u] = ring("ln_rho2", [P, UNIT_SLOTS[u], WG], F32)
+            nc.scalar.activation(out=flat(ln_rho2[u]), in_=flat(th[u]), func=ACT.Ln, bias=half[:], scale=0.5)
 
-        def deviation(g):
-            slots = slice(GROUP * g, GROUP * (g + 1))
-            var = three.tile([P, GROUP, WG], F32, name="var")
-            for s in range(GROUP):
+        def deviation(u):
+            s0, n = first[u], UNIT_SLOTS[u]
+            var = ring("var", [P, n, WG], F32)
+            for s in range(n):
                 nc.vector.scalar_tensor_tensor(
                     out=natural(var[:, s, :]),
-                    in0=split(ln_rho2[g][:, s, :]),
+                    in0=split(ln_rho2[u][:, s, :]),
                     scalar=0.5,
-                    in1=state_of(v1, GROUP * g + s),
+                    in1=state_of(v1, s0 + s),
                     op0=ALU.mult,
                     op1=ALU.add,
                 )
-            nc.sync.dma_start(out=var_v[:, slots, :], in_=var[:])
+            nc.sync.dma_start(out=var_v[:, s0 : s0 + n, :], in_=var[:])
 
-        def sum_transposed(g):
-            sum_t_bank[g] = banks.tile([P, GROUP_ROWS], F32, name="sum_t_bank", tag="bank")
-            for s in range(GROUP):
-                parts = [t[g][:, s, P * e : P * (e + 1)] for t in (nd, zz, ln_rho2) for e in range(2)]
-                for n, part in enumerate(parts):
+        def sum_transposed(u):
+            n = UNIT_SLOTS[u]
+            sum_t_bank[u] = banks.tile([P, n * P], F32, name="sum_t_bank", tag="bank")
+            for s in range(n):
+                parts = [t[u][:, s, P * e : P * (e + 1)] for t in (nd, zz, ln_rho2) for e in range(2)]
+                if u in W_ON_SCALAR:
+                    parts.insert(0, base_twice[:, first[u] + s, :])
+                for k, part in enumerate(parts):
                     nc.tensor.matmul(
-                        out=sum_t_bank[g][:, P * s : P * (s + 1)],
+                        out=sum_t_bank[u][:, P * s : P * (s + 1)],
                         lhsT=part,
                         rhs=ident[:],
                         is_transpose=True,
-                        start=(n == 0),
-                        stop=(n == len(parts) - 1),
+                        start=(k == 0),
+                        stop=(k == len(parts) - 1),
                     )
 
-        def sum_copy(g):
-            sum_t[g] = two.tile([P, GROUP_ROWS], F32, name="sum_t")
-            nc.scalar.mul(out=sum_t[g][:], in_=sum_t_bank[g][:], mul=0.5)
+        def sum_copy(u):
+            sum_t[u] = ring("sum_t", [P, UNIT_SLOTS[u] * P], F32)
+            nc.scalar.mul(out=sum_t[u][:], in_=sum_t_bank[u][:], mul=0.5)
 
-        def sum_back(g):
-            sum_bank[g] = banks.tile([P, GROUP_ROWS], F32, name="sum_bank", tag="bank")
-            for s in range(GROUP):
+        def sum_back(u):
+            n = UNIT_SLOTS[u]
+            sum_bank[u] = banks.tile([P, n * P], F32, name="sum_bank", tag="bank")
+            for s in range(n):
                 nc.tensor.transpose(
-                    sum_bank[g][:, P * s : P * (s + 1)], sum_t[g][:, P * s : P * (s + 1)], ident[:]
+                    sum_bank[u][:, P * s : P * (s + 1)], sum_t[u][:, P * s : P * (s + 1)], ident[:]
                 )
 
-        def weight_out(g):
-            slots = slice(GROUP * g, GROUP * (g + 1))
-            weight = three.tile([P, GROUP, WG // 2], F32, name="weight")
-            nc.vector.tensor_tensor(
+        def weight_out(u):
+            s0, n = first[u], UNIT_SLOTS[u]
+            weight = ring("weight", [P, n, WG // 2], F32)
+            if u in W_ON_SCALAR:
+                nc.scalar.copy(out=flat(weight), in_=sum_bank[u][:])
+            else:
+              nc.vector.tensor_tensor(
                 out=weight[:].rearrange("p s (i c) -> p s i c", i=NL),
-                in0=sum_bank[g][:].rearrange("p (s i c) -> p s i c", s=GROUP, i=NL),
-                in1=base[:, slots, :].unsqueeze(2).to_broadcast([P, GROUP, NL, JT]),
+                in0=sum_bank[u][:].rearrange("p (s i c) -> p s i c", s=n, i=NL),
+                in1=base[:, s0 : s0 + n, :].unsqueeze(2).to_broadcast([P, n, NL, JT]),
                 op=ALU.add,
             )
-            nc.sync.dma_start(out=scale_v[:, slots, :], in_=weight[:])
+            nc.sync.dma_start(out=scale_v[:, s0 : s0 + n, :], in_=weight[:])
 
-        def for_pair(pair, stage):
-            if 0 <= pair < N_PAIRS:
-                for g in range(PAIR * pair, PAIR * (pair + 1)):
-                    stage(g)
+        stage_of = {
+            "state_base": state_base, "state_exp": state_exp, "state_v": state_v, "state_rest": state_rest,
+            "transpose_x": transpose_x, "quantise_x": quantise_x, "project": project, "differences": differences,
+            "tanh": tanh, "shift": shift, "mean": mean, "logs": logs, "deviation": deviation,
+            "sum_transposed": sum_transposed, "sum_copy": sum_copy, "sum_back": sum_back, "weight_out": weight_out,
+        }
 
-        for k in range(-2, N_PAIRS + 1):
-            for_pair(k + 1, project)
-            for_pair(k - 1, sum_back)
-            for_pair(k, shift)
-            for_pair(k, mean)
-            for_pair(k - 1, weight_out)
-            for_pair(k + 1, differences)
-            for_pair(k, logs)
-            for_pair(k + 2, transpose_x)
-            for_pair(k + 1, tanh)
-            for_pair(k, sum_transposed)
-            for_pair(k, deviation)
-            for_pair(k, sum_copy)
-            for_pair(k + 2, quantise_x)
+        done = set()
+        for name, u in PROLOGUE:
+            stage_of[name](u)
+            done.add((name, u))
+        for r in range(-3, len(ROUNDS) + 3):
+            for name, offset in ORDER_EVEN if r % 2 == 0 else ORDER_ODD:
+                if 0 <= r + offset < len(ROUNDS):
+                    for u in ROUNDS[r + offset]:
+                        if (name, u) not in done:
+                            stage_of[name](u)

@@ -180,7 +180,13 @@ def tile_chainlveg_pa_t_kernel(
         if not any(name == "state_v" for name, u in PROLOGUE):
             state_v(0)
         def state_exp(u):
-            nc.scalar.activation(out=half_inv_e1[:], in_=v1[:], func=ACT.Exp, scale=-2.0, bias=ln_half[:])
+            nc.scalar.activation(
+                out=half_inv_e1[:].rearrange("p s (e c) -> p s c e", e=2),
+                in_=v1[:].rearrange("p s (c e) -> p s c e", e=2),
+                func=ACT.Exp,
+                scale=-2.0,
+                bias=ln_half[:],
+            )
 
         if not any(name == "state_exp" for name, u in PROLOGUE):
             state_exp(0)
@@ -309,7 +315,6 @@ def tile_chainlveg_pa_t_kernel(
             s0, n = first[u], UNIT_SLOTS[u]
             dm[u] = ring("dm", [P, n, WG], F32)
             nd[u] = ring("nd", [P, n, WG], F32)
-            dw[u] = ring("dw", [P, n, WG], F32)
             for s in range(n):
                 slot = s0 + s
                 a_rows = banks.tile([P, 2 * WG], F32, name="a_rows", tag="bank")
@@ -326,22 +331,24 @@ def tile_chainlveg_pa_t_kernel(
                         op0=ALU.min,
                         op1=ALU.subtract,
                     )
-                (nc.vector if DW_ON_VECTOR else nc.gpsimd).tensor_tensor(
-                    out=dw[u][:, s, :].rearrange("p (e i c) -> p e i c", e=2, i=NL),
-                    in0=dm[u][:, s, :].rearrange("p (e i c) -> p e i c", e=2, i=NL),
-                    in1=half_inv_e1[:, slot, :]
-                    .rearrange("p (c e) -> p e c", e=2)
-                    .unsqueeze(2)
-                    .to_broadcast([P, 2, NL, JT]),
-                    op=ALU.mult,
-                )
 
         def tanh(u):
             th[u] = ring("th", [P, UNIT_SLOTS[u], WG], F32)
             nc.scalar.activation(out=flat(th[u]), in_=flat(nd[u]), func=ACT.Tanh, scale=-0.5)
 
         def shift(u):
-            y2[u] = ring("y2", [P, UNIT_SLOTS[u], WG], F32)
+            s0, n = first[u], UNIT_SLOTS[u]
+            y2[u] = ring("y2", [P, n, WG], F32)
+            dw[u] = ring("dw", [P, n, WG], F32)
+            nc.vector.tensor_tensor(
+                out=dw[u][:].rearrange("p s (e i c) -> p (s e) i c", e=2, i=NL),
+                in0=dm[u][:].rearrange("p s (e i c) -> p (s e) i c", e=2, i=NL),
+                in1=half_inv_e1[:, s0 : s0 + n, :]
+                .rearrange("p s (e c) -> p (s e) c", e=2)
+                .unsqueeze(2)
+                .to_broadcast([P, 2 * n, NL, JT]),
+                op=ALU.mult,
+            )
             nc.vector.scalar_tensor_tensor(
                 out=flat(y2[u]), in0=flat(th[u]), scalar=1.0, in1=flat(dm[u]), op0=ALU.subtract, op1=ALU.mult
             )

@@ -25,7 +25,7 @@ ORDER_ODD = ORDER_EVEN
 DEPTH = {}
 PROLOGUE = (("state_v",0),("state_exp",0),("transpose_x",0),("quantise_x",0),("transpose_x",1),("project",0),("quantise_x",1),("state_rest",0),("state_base",0),("differences",0),("project",1),("transpose_x",2),("tanh",0),("differences",1),("quantise_x",2),("transpose_x",3),("tanh",1),("quantise_x",3),)
 X_ON_VECTOR = (0, 1)
-DW_ON_VECTOR = False
+DW_ON_GPSIMD = (0, 2, 4, 6)
 W_ON_SCALAR = ()
 BASE_ON_VECTOR = True
 LOAD_ORDER = ("bias",0,"state","sw","warm","codes",1,"scales",2,3,4,5,6,7)
@@ -315,6 +315,7 @@ def tile_chainlveg_pa_t_kernel(
             s0, n = first[u], UNIT_SLOTS[u]
             dm[u] = ring("dm", [P, n, WG], F32)
             nd[u] = ring("nd", [P, n, WG], F32)
+            dw[u] = ring("dw", [P, n, WG], F32)
             for s in range(n):
                 slot = s0 + s
                 a_rows = banks.tile([P, 2 * WG], F32, name="a_rows", tag="bank")
@@ -331,6 +332,16 @@ def tile_chainlveg_pa_t_kernel(
                         op0=ALU.min,
                         op1=ALU.subtract,
                     )
+                if u in DW_ON_GPSIMD:
+                    nc.gpsimd.tensor_tensor(
+                        out=dw[u][:, s, :].rearrange("p (e i c) -> p e i c", e=2, i=NL),
+                        in0=dm[u][:, s, :].rearrange("p (e i c) -> p e i c", e=2, i=NL),
+                        in1=half_inv_e1[:, slot, :]
+                        .rearrange("p (e c) -> p e c", e=2)
+                        .unsqueeze(2)
+                        .to_broadcast([P, 2, NL, JT]),
+                        op=ALU.mult,
+                    )
 
         def tanh(u):
             th[u] = ring("th", [P, UNIT_SLOTS[u], WG], F32)
@@ -339,16 +350,16 @@ def tile_chainlveg_pa_t_kernel(
         def shift(u):
             s0, n = first[u], UNIT_SLOTS[u]
             y2[u] = ring("y2", [P, n, WG], F32)
-            dw[u] = ring("dw", [P, n, WG], F32)
-            nc.vector.tensor_tensor(
-                out=dw[u][:].rearrange("p s (e i c) -> p (s e) i c", e=2, i=NL),
-                in0=dm[u][:].rearrange("p s (e i c) -> p (s e) i c", e=2, i=NL),
-                in1=half_inv_e1[:, s0 : s0 + n, :]
-                .rearrange("p s (e c) -> p (s e) c", e=2)
-                .unsqueeze(2)
-                .to_broadcast([P, 2 * n, NL, JT]),
-                op=ALU.mult,
-            )
+            if u not in DW_ON_GPSIMD:
+                nc.vector.tensor_tensor(
+                    out=dw[u][:].rearrange("p s (e i c) -> p (s e) i c", e=2, i=NL),
+                    in0=dm[u][:].rearrange("p s (e i c) -> p (s e) i c", e=2, i=NL),
+                    in1=half_inv_e1[:, s0 : s0 + n, :]
+                    .rearrange("p s (e c) -> p (s e) c", e=2)
+                    .unsqueeze(2)
+                    .to_broadcast([P, 2 * n, NL, JT]),
+                    op=ALU.mult,
+                )
             nc.vector.scalar_tensor_tensor(
                 out=flat(y2[u]), in0=flat(th[u]), scalar=1.0, in1=flat(dm[u]), op0=ALU.subtract, op1=ALU.mult
             )

@@ -88,7 +88,7 @@ def tile_chainlveg_pa_t_kernel(
         nc.vector.memset(w_scales[:].bitcast(I32), 0)
         nc.vector.memset(half[:], 0.5)
         ln_half = keep.tile([P, 1], F32)
-        nc.vector.tensor_scalar(out=ln_half[:], in0=half[:], scalar1=0.0, scalar2=math.log(0.5), op0=ALU.mult, op1=ALU.add)
+        nc.vector.tensor_scalar(out=ln_half[:], in0=half[:], scalar1=0.0, scalar2=math.log(2.0), op0=ALU.mult, op1=ALU.add)
 
         x_all = keep.tile([P, SLOTS, K], BF16)
         smu_raw = keep.tile([P, SLOTS, NL * 2], BF16)
@@ -151,7 +151,9 @@ def tile_chainlveg_pa_t_kernel(
         bias_bank = banks.tile([P, 4 * P], F32, name="bias_bank", tag="bank")
         nc.tensor.transpose(bias_bank[:, 0:P], bias_f32[:], ident[:])
         relu_bias = keep.tile([P, CHUNKS], F32)
-        nc.vector.tensor_scalar_add(out=relu_bias[:, 0:2], in0=bias_bank[:, 0:2], scalar1=1.0)
+        nc.vector.tensor_scalar(
+            out=relu_bias[:, 0:2], in0=bias_bank[:, 0:2], scalar1=-0.5, scalar2=0.5, op0=ALU.mult, op1=ALU.add
+        )
         nc.vector.tensor_scalar(
             out=relu_bias[:, 2:4], in0=bias_bank[:, 2:4], scalar1=-2.0, scalar2=2.0, op0=ALU.mult, op1=ALU.add
         )
@@ -175,7 +177,9 @@ def tile_chainlveg_pa_t_kernel(
                 out=two_less_2v1[:], in0=v1[:], scalar1=-2.0, scalar2=2.0, op0=ALU.mult, op1=ALU.add
             )
             spread_over_t(m1, smu_raw)
-            nc.vector.tensor_scalar_add(out=m1_plus1[:], in0=m1[:], scalar1=1.0)
+            nc.vector.tensor_scalar(
+                out=m1_plus1[:], in0=m1[:], scalar1=-0.5, scalar2=0.5, op0=ALU.mult, op1=ALU.add
+            )
 
         if not any(name == "state_v" for name, u in PROLOGUE):
             state_v(0)
@@ -308,7 +312,7 @@ def tile_chainlveg_pa_t_kernel(
                     in_=acc[:],
                     func=ACT.Relu,
                     bias=relu_bias[:, c : c + 1],
-                    scale=1.0 if c < 2 else -2.0,
+                    scale=-0.5 if c < 2 else -2.0,
                 )
 
         def differences(u):
@@ -323,7 +327,7 @@ def tile_chainlveg_pa_t_kernel(
                     nc.tensor.transpose(
                         a_rows[:, P * c : P * (c + 1)], a_t[u][:, c, P * s : P * (s + 1)], ident[:]
                     )
-                for dst, start_col, top, state in ((dm[u], 0, 2.0, m1_plus1), (nd[u], WG, 4.0, two_less_2v1)):
+                for dst, start_col, top, state in ((dm[u], 0, 1.0, m1_plus1), (nd[u], WG, 4.0, two_less_2v1)):
                     nc.vector.scalar_tensor_tensor(
                         out=split(dst[:, s, :]),
                         in0=natural(a_rows[:, start_col : start_col + WG]),
@@ -368,15 +372,15 @@ def tile_chainlveg_pa_t_kernel(
             s0, n = first[u], UNIT_SLOTS[u]
             mu = ring("mu", [P, n, WG], F32)
             zz[u] = ring("zz", [P, n, WG], F32)
-            for s in range(n):
-                nc.vector.scalar_tensor_tensor(
-                    out=natural(mu[:, s, :]),
-                    in0=split(y2[u][:, s, :]),
-                    scalar=-0.5,
-                    in1=state_of(m1, s0 + s),
-                    op0=ALU.mult,
-                    op1=ALU.add,
-                )
+            nc.vector.tensor_tensor(
+                out=mu[:].rearrange("p s (i c e) -> p s i c e", i=NL, e=2),
+                in0=y2[u][:].rearrange("p s (e i c) -> p s i c e", i=NL, e=2),
+                in1=m1[:, s0 : s0 + n, :]
+                .rearrange("p s (c e) -> p s c e", e=2)
+                .unsqueeze(2)
+                .to_broadcast([P, n, NL, JT, 2]),
+                op=ALU.add,
+            )
             nc.sync.dma_start(out=mu_v[:, s0 : s0 + n, :], in_=mu[:])
             nc.vector.tensor_tensor(out=flat(zz[u]), in0=flat(y2[u]), in1=flat(dw[u]), op=ALU.mult)
 

@@ -372,6 +372,7 @@ def tile_chainlveg_pa_t_kernel(
             s0, n = first[u], UNIT_SLOTS[u]
             mu = ring("mu", [P, n, WG], F32)
             zz[u] = ring("zz", [P, n, WG], F32)
+            nc.vector.tensor_tensor(out=flat(zz[u]), in0=flat(y2[u]), in1=flat(dw[u]), op=ALU.mult)
             nc.vector.tensor_tensor(
                 out=mu[:].rearrange("p s (i c e) -> p s i c e", i=NL, e=2),
                 in0=y2[u][:].rearrange("p s (e i c) -> p s i c e", i=NL, e=2),
@@ -382,7 +383,6 @@ def tile_chainlveg_pa_t_kernel(
                 op=ALU.add,
             )
             nc.sync.dma_start(out=mu_v[:, s0 : s0 + n, :], in_=mu[:])
-            nc.vector.tensor_tensor(out=flat(zz[u]), in0=flat(y2[u]), in1=flat(dw[u]), op=ALU.mult)
 
         def logs(u):
             ln_rho2[u] = ring("ln_rho2", [P, UNIT_SLOTS[u], WG], F32)
@@ -406,7 +406,7 @@ def tile_chainlveg_pa_t_kernel(
             n = UNIT_SLOTS[u]
             sum_t_bank[u] = banks.tile([P, n * P], F32, name="sum_t_bank", tag="bank")
             for s in range(n):
-                parts = [t[u][:, s, P * e : P * (e + 1)] for t in (nd, zz, ln_rho2) for e in range(2)]
+                parts = [t[u][:, s, P * e : P * (e + 1)] for t in (nd, ln_rho2, zz) for e in range(2)]
                 if u in W_ON_SCALAR:
                     parts.insert(0, base_twice[:, first[u] + s, :])
                 for k, part in enumerate(parts):
@@ -457,8 +457,12 @@ def tile_chainlveg_pa_t_kernel(
             stage_of[name](u)
             done.add((name, u))
         for r in range(-3, len(ROUNDS) + 3):
-            for name, offset in ORDER_EVEN if r % 2 == 0 else ORDER_ODD:
+            for entry in ORDER_EVEN if r % 2 == 0 else ORDER_ODD:
+                name, offset = entry[0], entry[1]
                 if 0 <= r + offset < len(ROUNDS):
-                    for u in ROUNDS[r + offset]:
+                    units = ROUNDS[r + offset]
+                    if len(entry) > 2:
+                        units = units[entry[2] : entry[2] + 1]
+                    for u in units:
                         if (name, u) not in done:
                             stage_of[name](u)

@@ -27,6 +27,7 @@ PROLOGUE = (("state_v",0),("state_exp",0),("transpose_x",0),("quantise_x",0),("t
 X_ON_VECTOR = (0, 1)
 DW_ON_GPSIMD = (0, 2, 4, 6)
 W_ON_SCALAR = ()
+LN_RHO_ON_SCALAR = (1, 3, 5, 7)
 BASE_ON_VECTOR = True
 LOAD_ORDER = ("bias",0,"state","sw","warm","codes",1,"scales",2,3,4,5,6,7)
 NL = 8
@@ -71,7 +72,7 @@ def tile_chainlveg_pa_t_kernel(
         for depth in (2, 3, 4, 6, 8):
             pools[depth] = stack.enter_context(tc.tile_pool(name="ring%d" % depth, bufs=depth))
         default_depth = {"grouped": 2, "x_codes": 2, "x_scales": 2, "a_t": 2, "dm": 2, "dw": 2, "y2": 2, "zz": 2,
-                         "ln_rho2": 2, "sum_t": 2, "mu": 3, "var": 3, "weight": 3, "nd": 4, "th": 2}
+                         "ln_rho2": 2, "ln_rho": 2, "sum_t": 2, "mu": 3, "var": 3, "weight": 3, "nd": 4, "th": 2}
 
         def ring(name, shape, dtype, align=32):
             return pools[DEPTH.get(name, default_depth[name])].tile(shape, dtype, name=name, align_bytes=align)
@@ -243,6 +244,7 @@ def tile_chainlveg_pa_t_kernel(
         y2 = {}
         nd = {}
         ln_rho2 = {}
+        ln_rho = {}
         sum_t_bank = {}
         sum_t = {}
         sum_bank = {}
@@ -387,6 +389,9 @@ def tile_chainlveg_pa_t_kernel(
         def logs(u):
             ln_rho2[u] = ring("ln_rho2", [P, UNIT_SLOTS[u], WG], F32)
             nc.scalar.activation(out=flat(ln_rho2[u]), in_=flat(th[u]), func=ACT.Ln, bias=half[:], scale=0.5)
+            if u in LN_RHO_ON_SCALAR:
+                ln_rho[u] = ring("ln_rho", [P, UNIT_SLOTS[u], WG], F32)
+                nc.scalar.activation(out=flat(ln_rho[u]), in_=flat(th[u]), func=ACT.Ln, bias=half[:], scale=-0.5)
 
         def deviation(u):
             s0, n = first[u], UNIT_SLOTS[u]
@@ -406,7 +411,8 @@ def tile_chainlveg_pa_t_kernel(
             n = UNIT_SLOTS[u]
             sum_t_bank[u] = banks.tile([P, n * P], F32, name="sum_t_bank", tag="bank")
             for s in range(n):
-                parts = [t[u][:, s, P * e : P * (e + 1)] for t in (nd, ln_rho2, zz) for e in range(2)]
+                terms = (ln_rho, zz) if u in LN_RHO_ON_SCALAR else (nd, ln_rho2, zz)
+                parts = [t[u][:, s, P * e : P * (e + 1)] for t in terms for e in range(2)]
                 if u in W_ON_SCALAR:
                     parts.insert(0, base_twice[:, first[u] + s, :])
                 for k, part in enumerate(parts):

@@ -25,9 +25,13 @@ ORDER_ODD = ORDER_EVEN
 DEPTH = {}
 PROLOGUE = (("state_v",0),("state_exp",0),("transpose_x",0),("quantise_x",0),("transpose_x",1),("project",0),("quantise_x",1),("state_rest",0),("state_base",0),("differences",0),("project",1),("transpose_x",2),("tanh",0),("differences",1),("quantise_x",2),("transpose_x",3),("tanh",1),("quantise_x",3),)
 X_ON_VECTOR = (0, 1)
-DW_ON_GPSIMD = (0, 2, 4, 6)
+GPSIMD_SLOTS = (4, 1)
 W_ON_SCALAR = ()
-LN_RHO_ON_SCALAR = (1, 3, 5, 7)
+PLAIN_IN_DIFFERENCES = ()
+PLAIN_IN_SUMS = False
+PLAIN_EVERY = 1
+N_WARM = 0
+LN_RHO_ON_SCALAR = (1, 3, 5, 6, 7)
 BASE_ON_VECTOR = True
 LOAD_ORDER = ("bias",0,"state","sw","warm","codes",1,"scales",2,3,4,5,6,7)
 NL = 8
@@ -146,6 +150,11 @@ def tile_chainlveg_pa_t_kernel(
 
         ident = keep.tile([P, P], F32)
         make_identity(nc, ident[:])
+
+        if N_WARM:
+            warm_bank = banks.tile([P, P], F32, name="warm_bank", tag="bank")
+            for w in range(N_WARM):
+                nc.tensor.matmul(out=warm_bank[:], lhsT=ident[:], rhs=ident[:], start=True, stop=True)
 
         bias_f32 = keep.tile([P, P], F32)
         nc.vector.tensor_copy(out=bias_f32[:], in_=bias_rows[:])
@@ -326,9 +335,18 @@ def tile_chainlveg_pa_t_kernel(
                 slot = s0 + s
                 a_rows = banks.tile([P, 2 * WG], F32, name="a_rows", tag="bank")
                 for c in range(CHUNKS):
-                    nc.tensor.transpose(
-                        a_rows[:, P * c : P * (c + 1)], a_t[u][:, c, P * s : P * (s + 1)], ident[:]
-                    )
+                    if c in PLAIN_IN_DIFFERENCES and s % PLAIN_EVERY == 0:
+                        nc.tensor.matmul(
+                            out=a_rows[:, P * c : P * (c + 1)],
+                            lhsT=a_t[u][:, c, P * s : P * (s + 1)],
+                            rhs=ident[:],
+                            start=True,
+                            stop=True,
+                        )
+                    else:
+                        nc.tensor.transpose(
+                            a_rows[:, P * c : P * (c + 1)], a_t[u][:, c, P * s : P * (s + 1)], ident[:]
+                        )
                 for dst, start_col, top, state in ((dm[u], 0, 1.0, m1_plus1), (nd[u], WG, 4.0, two_less_2v1)):
                     nc.vector.scalar_tensor_tensor(
                         out=split(dst[:, s, :]),
@@ -338,7 +356,7 @@ def tile_chainlveg_pa_t_kernel(
                         op0=ALU.min,
                         op1=ALU.subtract,
                     )
-                if u in DW_ON_GPSIMD:
+                if s < GPSIMD_SLOTS[u % 2]:
                     nc.gpsimd.tensor_tensor(
                         out=dw[u][:, s, :].rearrange("p (e i c) -> p e i c", e=2, i=NL),
                         in0=dm[u][:, s, :].rearrange("p (e i c) -> p e i c", e=2, i=NL),
@@ -356,14 +374,15 @@ def tile_chainlveg_pa_t_kernel(
         def shift(u):
             s0, n = first[u], UNIT_SLOTS[u]
             y2[u] = ring("y2", [P, n, WG], F32)
-            if u not in DW_ON_GPSIMD:
+            g = GPSIMD_SLOTS[u % 2]
+            if g < n:
                 nc.vector.tensor_tensor(
-                    out=dw[u][:].rearrange("p s (e i c) -> p (s e) i c", e=2, i=NL),
-                    in0=dm[u][:].rearrange("p s (e i c) -> p (s e) i c", e=2, i=NL),
-                    in1=half_inv_e1[:, s0 : s0 + n, :]
+                    out=dw[u][:, g:n, :].rearrange("p s (e i c) -> p (s e) i c", e=2, i=NL),
+                    in0=dm[u][:, g:n, :].rearrange("p s (e i c) -> p (s e) i c", e=2, i=NL),
+                    in1=half_inv_e1[:, s0 + g : s0 + n, :]
                     .rearrange("p s (e c) -> p (s e) c", e=2)
                     .unsqueeze(2)
-                    .to_broadcast([P, 2 * n, NL, JT]),
+                    .to_broadcast([P, 2 * (n - g), NL, JT]),
                     op=ALU.mult,
                 )
             nc.vector.scalar_tensor_tensor(
@@ -420,7 +439,7 @@ def tile_chainlveg_pa_t_kernel(
                         out=sum_t_bank[u][:, P * s : P * (s + 1)],
                         lhsT=part,
                         rhs=ident[:],
-                        is_transpose=True,
+                        is_transpose=not (k == 0 and s % 2 == 0 and PLAIN_IN_SUMS),
                         start=(k == 0),
                         stop=(k == len(parts) - 1),
                     )

@@ -17,23 +17,11 @@ P = 128
 K = 512
 ROWS = 4096
 SLOTS = ROWS // P
-UNIT_SLOTS = (4, 4, 4, 4, 4, 4, 4, 4)
-ROUNDS = ((0, 1), (2, 3), (4, 5), (6, 7))
-X_LOADS = ((0, 4), (4, 4), (8, 4), (12, 4), (16, 4), (20, 4), (24, 4), (28, 4))
-ORDER_EVEN = (("project",1),("sum_back",-1),("shift",0),("mean",0),("differences",1),("weight_out",-1),("logs",0),("transpose_x",2),("tanh",1),("sum_transposed",0),("deviation",0),("sum_copy",0),("quantise_x",2),)
-ORDER_ODD = ORDER_EVEN
-DEPTH = {}
-PROLOGUE = (("state_v",0),("state_exp",0),("transpose_x",0),("quantise_x",0),("transpose_x",1),("project",0),("quantise_x",1),("state_rest",0),("state_base",0),("differences",0),("project",1),("transpose_x",2),("tanh",0),("differences",1),("quantise_x",2),("transpose_x",3),("tanh",1),("quantise_x",3),)
-X_ON_VECTOR = (0, 1)
-GPSIMD_SLOTS = (4, 1)
-W_ON_SCALAR = ()
-PLAIN_IN_DIFFERENCES = ()
-PLAIN_IN_SUMS = False
-PLAIN_EVERY = 1
-N_WARM = 0
-LN_RHO_ON_SCALAR = (1, 3, 5, 6, 7)
-BASE_ON_VECTOR = True
-LOAD_ORDER = ("bias",0,"state","sw","warm","codes",1,"scales",2,3,4,5,6,7)
+GROUP = 4
+GROUP_ROWS = GROUP * P
+N_GROUPS = SLOTS // GROUP
+PAIR = 2
+N_PAIRS = N_GROUPS // PAIR
 NL = 8
 JTG = 32
 JT = 16
@@ -41,7 +29,13 @@ WG = NL * JTG
 CHUNKS = 2 * WG // P
 LOG_2PI = math.log(2.0 * math.pi)
 
+GPSIMD_SLOTS = (4, 1)
+
 FLOPS = 2 * ROWS * K * 2 * WG
+
+
+def scalar_makes_ln_rho(grp):
+    return grp % PAIR == 1 or grp // PAIR == N_PAIRS - 1
 
 
 def tile_chainlveg_pa_t_kernel(
@@ -63,25 +57,18 @@ def tile_chainlveg_pa_t_kernel(
     nc = tc.nc
 
     x_v = x.flatten_outer_dims().rearrange("(p s) k -> p s k", s=SLOTS)
-    sw_v = s_weight.rearrange("b q j e -> (b q) (j e)").rearrange("(p s) c -> p s c", s=SLOTS)
-    smu_v = s_mu.rearrange("b q j e g -> (b q) (j e g)").rearrange("(p s) c -> p s c", s=SLOTS)
-    svar_v = s_var.rearrange("b q j e g -> (b q) (j e g)").rearrange("(p s) c -> p s c", s=SLOTS)
-    scale_v = out_0.rearrange("b q i j t e -> (b q) (i j t e)").rearrange("(p s) c -> p s c", s=SLOTS)
-    mu_v = out_1.rearrange("b q i j t e g -> (b q) (i j t e g)").rearrange("(p s) c -> p s c", s=SLOTS)
-    var_v = out_2.rearrange("b q i j t e g -> (b q) (i j t e g)").rearrange("(p s) c -> p s c", s=SLOTS)
+    sw_v = s_weight.rearrange("b q j e -> (b q) (j e)").rearrange("(p s) n -> p s n", s=SLOTS)
+    smu_v = s_mu.rearrange("b q j e g -> (b q) (j e g)").rearrange("(p s) n -> p s n", s=SLOTS)
+    svar_v = s_var.rearrange("b q j e g -> (b q) (j e g)").rearrange("(p s) n -> p s n", s=SLOTS)
+    scale_v = out_0.rearrange("b q i j t e -> (b q) (i j t e)").rearrange("(p s) n -> p s n", s=SLOTS)
+    mu_v = out_1.rearrange("b q i j t e g -> (b q) (i j t e g)").rearrange("(p s) n -> p s n", s=SLOTS)
+    var_v = out_2.rearrange("b q i j t e g -> (b q) (i j t e g)").rearrange("(p s) n -> p s n", s=SLOTS)
 
     with ExitStack() as stack:
         keep = stack.enter_context(tc.tile_pool(name="keep", bufs=1))
-        pools = {}
-        for depth in (2, 3, 4, 6, 8):
-            pools[depth] = stack.enter_context(tc.tile_pool(name="ring%d" % depth, bufs=depth))
-        default_depth = {"grouped": 2, "x_codes": 2, "x_scales": 2, "a_t": 2, "dm": 2, "dw": 2, "y2": 2, "zz": 2,
-                         "ln_rho2": 2, "ln_rho": 2, "sum_t": 2, "mu": 3, "var": 3, "weight": 3, "nd": 4, "th": 2}
-
-        def ring(name, shape, dtype, align=32):
-            return pools[DEPTH.get(name, default_depth[name])].tile(shape, dtype, name=name, align_bytes=align)
-
-        first = [sum(UNIT_SLOTS[:u]) for u in range(len(UNIT_SLOTS))]
+        two = stack.enter_context(tc.tile_pool(name="two", bufs=PAIR))
+        three = stack.enter_context(tc.tile_pool(name="three", bufs=3))
+        four = stack.enter_context(tc.tile_pool(name="four", bufs=2 * PAIR))
         banks = stack.enter_context(tc.psum_pool(name="banks", bufs=8))
         stack.enter_context(tc.manual_schedule())
 
@@ -89,77 +76,54 @@ def tile_chainlveg_pa_t_kernel(
         w_scales = keep.tile([P, 2 * WG], U8, align_bytes=64)
         bias_rows = keep.tile([P, P], BF16)
         half = keep.tile([P, 1], F32)
+        ln_2 = keep.tile([P, 1], F32)
         nc.vector.memset(bias_rows[:], 0.0)
         nc.vector.memset(w_scales[:].bitcast(I32), 0)
         nc.vector.memset(half[:], 0.5)
-        ln_half = keep.tile([P, 1], F32)
-        nc.vector.tensor_scalar(out=ln_half[:], in0=half[:], scalar1=0.0, scalar2=math.log(2.0), op0=ALU.mult, op1=ALU.add)
+        nc.vector.tensor_scalar(
+            out=ln_2[:], in0=half[:], scalar1=0.0, scalar2=math.log(2.0), op0=ALU.mult, op1=ALU.add
+        )
 
-        x_all = keep.tile([P, SLOTS, K], BF16)
+        x_sb = keep.tile([P, SLOTS, K], BF16)
         smu_raw = keep.tile([P, SLOTS, NL * 2], BF16)
         svar_raw = keep.tile([P, SLOTS, NL * 2], BF16)
         sw_raw = keep.tile([P, SLOTS, NL], BF16)
 
-        def load_x(queue, g):
-            s0, n = X_LOADS[g]
-            queue.dma_start(out=x_all[:, s0 : s0 + n, :], in_=x_v[:, s0 : s0 + n, :])
+        def load_x(grp):
+            slots = slice(GROUP * grp, GROUP * (grp + 1))
+            nc.sync.dma_start(out=x_sb[:, slots, :], in_=x_v[:, slots, :])
 
-        def load_bias():
-            nc.scalar.dma_start(out=bias_rows[0:2, :], in_=tcm_b.rearrange("(c n) -> c n", c=2))
-            nc.scalar.dma_start(out=bias_rows[2:4, :], in_=tcv_b.rearrange("(c n) -> c n", c=2))
-
-        def load_state():
-            nc.scalar.dma_start(out=svar_raw[:], in_=svar_v)
-            nc.scalar.dma_start(out=smu_raw[:], in_=smu_v)
-
-        def load_codes():
-            for w, words in enumerate((tcm_w_words, tcv_w_words)):
-                nc.sync.dma_start(
-                    out=w_codes[:, WG * w : WG * (w + 1)].bitcast(I32),
-                    in_=words[0].rearrange("p n t -> p (n t)").bitcast(I32),
-                )
-
-        def load_scales(which):
-            for w, scales in which:
-                for quad in range(4):
-                    nc.sync.dma_start(
-                        out=w_scales[32 * quad : 32 * quad + 4, WG * w : WG * (w + 1)].bitcast(I32),
-                        in_=scales[0][4 * quad : 4 * quad + 4, :].bitcast(I32),
-                    )
-
+        nc.scalar.dma_start(out=bias_rows[0:2, :], in_=tcm_b.rearrange("(c n) -> c n", c=2))
+        nc.scalar.dma_start(out=bias_rows[2:4, :], in_=tcv_b.rearrange("(c n) -> c n", c=2))
+        load_x(0)
+        nc.scalar.dma_start(out=svar_raw[:], in_=svar_v)
+        nc.scalar.dma_start(out=smu_raw[:], in_=smu_v)
+        nc.sync.dma_start(out=sw_raw[:], in_=sw_v)
         warm = keep.tile([P, 1], F32)
-        for what in LOAD_ORDER:
-            if what == "bias":
-                load_bias()
-            elif what == "state":
-                load_state()
-            elif what == "warm":
-                nc.scalar.activation(out=warm[:], in_=half[:], func=ACT.Exp)
-            elif what == "codes":
-                load_codes()
-            elif what == "scales":
-                load_scales(((0, tcm_w_scales), (1, tcv_w_scales)))
-            elif what == "scales_m":
-                load_scales(((0, tcm_w_scales),))
-            elif what == "scales_v":
-                load_scales(((1, tcv_w_scales),))
-            elif what == "sw":
-                nc.sync.dma_start(out=sw_raw[:], in_=sw_v)
-            else:
-                load_x(nc.sync, what)
+        nc.scalar.activation(out=warm[:], in_=half[:], func=ACT.Exp)
+        for which, words in enumerate((tcm_w_words, tcv_w_words)):
+            nc.sync.dma_start(
+                out=w_codes[:, WG * which : WG * (which + 1)].bitcast(I32),
+                in_=words[0].rearrange("p n z -> p (n z)").bitcast(I32),
+            )
+        load_x(1)
+        for which, scales in enumerate((tcm_w_scales, tcv_w_scales)):
+            for quad in range(4):
+                nc.sync.dma_start(
+                    out=w_scales[32 * quad : 32 * quad + 4, WG * which : WG * (which + 1)].bitcast(I32),
+                    in_=scales[0][4 * quad : 4 * quad + 4, :].bitcast(I32),
+                )
+        for grp in range(2, N_GROUPS):
+            load_x(grp)
 
         ident = keep.tile([P, P], F32)
         make_identity(nc, ident[:])
 
-        if N_WARM:
-            warm_bank = banks.tile([P, P], F32, name="warm_bank", tag="bank")
-            for w in range(N_WARM):
-                nc.tensor.matmul(out=warm_bank[:], lhsT=ident[:], rhs=ident[:], start=True, stop=True)
-
         bias_f32 = keep.tile([P, P], F32)
         nc.vector.tensor_copy(out=bias_f32[:], in_=bias_rows[:])
-        bias_bank = banks.tile([P, 4 * P], F32, name="bias_bank", tag="bank")
+        bias_bank = banks.tile([P, GROUP_ROWS], F32, name="bias_bank", tag="bank")
         nc.tensor.transpose(bias_bank[:, 0:P], bias_f32[:], ident[:])
+        relu_scale = (-0.5, -0.5, -2.0, -2.0)
         relu_bias = keep.tile([P, CHUNKS], F32)
         nc.vector.tensor_scalar(
             out=relu_bias[:, 0:2], in0=bias_bank[:, 0:2], scalar1=-0.5, scalar2=0.5, op0=ALU.mult, op1=ALU.add
@@ -168,76 +132,62 @@ def tile_chainlveg_pa_t_kernel(
             out=relu_bias[:, 2:4], in0=bias_bank[:, 2:4], scalar1=-2.0, scalar2=2.0, op0=ALU.mult, op1=ALU.add
         )
 
+        def natural(ap):
+            return ap.rearrange("p (i u g) -> p i u g", i=NL, g=2)
+
+        def split(ap):
+            return ap.rearrange("p (g i u) -> p i u g", i=NL, g=2)
+
+        def flat(t):
+            return t[:].rearrange("p s n -> p (s n)")
+
         def spread_over_t(dst, src):
             nc.vector.tensor_copy(
                 out=dst[:].rearrange("p s (j t g) -> p (s j) t g", t=2, g=2),
                 in_=src[:].rearrange("p s (j g) -> p (s j) g", g=2).unsqueeze(2).to_broadcast([P, SLOTS * NL, 2, 2]),
             )
 
+        def state_of(tile_, slot):
+            return tile_[:, slot, :].rearrange("p (u g) -> p u g", g=2).unsqueeze(1).to_broadcast([P, NL, JT, 2])
+
         v1 = keep.tile([P, SLOTS, JTG], F32)
         two_less_2v1 = keep.tile([P, SLOTS, JTG], F32)
         m1 = keep.tile([P, SLOTS, JTG], F32)
-        m1_plus1 = keep.tile([P, SLOTS, JTG], F32)
-        half_inv_e1 = keep.tile([P, SLOTS, JTG], F32)
-        def state_v(u):
-            spread_over_t(v1, svar_raw)
+        half_less_half_m1 = keep.tile([P, SLOTS, JTG], F32)
+        two_inv_e1 = keep.tile([P, SLOTS, JTG], F32)
+        v1_sum = keep.tile([P, SLOTS * NL], F32)
+        base_j = keep.tile([P, SLOTS * NL], F32)
+        base = keep.tile([P, SLOTS, JT], F32)
 
-        def state_rest(u):
+        def state_exp():
+            nc.scalar.activation(
+                out=two_inv_e1[:].rearrange("p s (g u) -> p s u g", g=2),
+                in_=v1[:].rearrange("p s (u g) -> p s u g", g=2),
+                func=ACT.Exp,
+                scale=-2.0,
+                bias=ln_2[:],
+            )
+
+        def state_offsets():
             nc.vector.tensor_scalar(
                 out=two_less_2v1[:], in0=v1[:], scalar1=-2.0, scalar2=2.0, op0=ALU.mult, op1=ALU.add
             )
             spread_over_t(m1, smu_raw)
             nc.vector.tensor_scalar(
-                out=m1_plus1[:], in0=m1[:], scalar1=-0.5, scalar2=0.5, op0=ALU.mult, op1=ALU.add
+                out=half_less_half_m1[:], in0=m1[:], scalar1=-0.5, scalar2=0.5, op0=ALU.mult, op1=ALU.add
             )
 
-        if not any(name == "state_v" for name, u in PROLOGUE):
-            state_v(0)
-        def state_exp(u):
-            nc.scalar.activation(
-                out=half_inv_e1[:].rearrange("p s (e c) -> p s c e", e=2),
-                in_=v1[:].rearrange("p s (c e) -> p s c e", e=2),
-                func=ACT.Exp,
-                scale=-2.0,
-                bias=ln_half[:],
-            )
-
-        if not any(name == "state_exp" for name, u in PROLOGUE):
-            state_exp(0)
-        if not any(name == "state_rest" for name, u in PROLOGUE):
-            state_rest(0)
-
-        v1_sum = keep.tile([P, SLOTS * NL], F32)
-        base_j = keep.tile([P, SLOTS * NL], F32)
-        base = keep.tile([P, SLOTS, JT], F32)
-        svar_pairs = svar_raw[:].rearrange("p s (j g) -> p (s j) g", g=2)
-
-        def state_base(u):
-            eng = nc.vector if BASE_ON_VECTOR else nc.gpsimd
-            eng.tensor_tensor(out=v1_sum[:], in0=svar_pairs[:, :, 0], in1=svar_pairs[:, :, 1], op=ALU.add)
-            eng.tensor_tensor(
+        def state_base():
+            svar_pairs = svar_raw[:].rearrange("p s (j g) -> p (s j) g", g=2)
+            nc.vector.tensor_tensor(out=v1_sum[:], in0=svar_pairs[:, :, 0], in1=svar_pairs[:, :, 1], op=ALU.add)
+            nc.vector.tensor_tensor(
                 out=base_j[:], in0=sw_raw[:].rearrange("p s j -> p (s j)"), in1=v1_sum[:], op=ALU.subtract
             )
-            eng.tensor_scalar(
+            nc.vector.tensor_scalar(
                 out=base[:].rearrange("p s (j t) -> p (s j) t", t=2),
                 in0=base_j[:].unsqueeze(2).to_broadcast([P, SLOTS * NL, 2]),
                 scalar1=1.0,
                 scalar2=-LOG_2PI,
-                op0=ALU.mult,
-                op1=ALU.add,
-            )
-
-        if not any(name == "state_base" for name, u in PROLOGUE):
-            state_base(0)
-
-        base_twice = keep.tile([P, SLOTS, WG // 2], F32)
-        for u in W_ON_SCALAR:
-            s0, n = first[u], UNIT_SLOTS[u]
-            nc.gpsimd.tensor_scalar(
-                out=base_twice[:, s0 : s0 + n, :].rearrange("p s (i c) -> p s i c", i=NL),
-                in0=base[:, s0 : s0 + n, :].unsqueeze(2).to_broadcast([P, n, NL, JT]),
-                scalar1=2.0,
-                scalar2=0.0,
                 op0=ALU.mult,
                 op1=ALU.add,
             )
@@ -247,107 +197,84 @@ def tile_chainlveg_pa_t_kernel(
         x_scales = {}
         a_t = {}
         dm = {}
+        nd = {}
         dw = {}
         th = {}
+        y = {}
         zz = {}
-        y2 = {}
-        nd = {}
-        ln_rho2 = {}
+        ln_rest = {}
         ln_rho = {}
         sum_t_bank = {}
         sum_t = {}
         sum_bank = {}
 
-        def natural(ap):
-            return ap.rearrange("p (i c e) -> p i c e", i=NL, e=2)
-
-        def split(ap):
-            return ap.rearrange("p (e i c) -> p i c e", i=NL, e=2)
-
-        def state_of(tile_, slot):
-            return tile_[:, slot, :].rearrange("p (c e) -> p c e", e=2).unsqueeze(1).to_broadcast([P, NL, JT, 2])
-
-        def flat(t):
-            return t[:].rearrange("p s c -> p (s c)")
-
-        def transpose_x(u):
-            s0, n = first[u], UNIT_SLOTS[u]
-            grouped[u] = ring("grouped", [P, n * P, 4], BF16, 64)
+        def transpose_x(grp, copy):
+            grouped[grp] = two.tile([P, GROUP_ROWS, 4], BF16, align_bytes=64, name="grouped")
             words_out = (
-                grouped[u][:].rearrange("p r t -> p (r t)").bitcast(F32).rearrange("p (r h) -> p r h", h=2)
+                grouped[grp][:].rearrange("p r z -> p (r z)").bitcast(F32).rearrange("p (r h) -> p r h", h=2)
             )
-            x_words = x_all[:, s0 : s0 + n, :].bitcast(F32)
-            for b in range(0, n, 2):
-                m = min(2, n - b)
-                xt = banks.tile([P, 2, m * P], F32, name="xt", tag="bank")
-                for j in range(m):
+            x_words = x_sb[:, GROUP * grp : GROUP * (grp + 1), :].bitcast(F32)
+            for first in range(0, GROUP, 2):
+                xt = banks.tile([P, 2, 2 * P], F32, name="xt", tag="bank")
+                for s in range(2):
                     for h in range(2):
                         nc.tensor.transpose(
-                            xt[:, h, P * j : P * (j + 1)], x_words[:, b + j, h : K // 2 : 2], ident[:]
+                            xt[:, h, P * s : P * (s + 1)], x_words[:, first + s, h : K // 2 : 2], ident[:]
                         )
-                if u in X_ON_VECTOR:
-                    nc.vector.tensor_copy(
-                        out=words_out[:, P * b : P * (b + m), :], in_=xt[:].rearrange("p h r -> p r h")
-                    )
-                else:
-                    nc.scalar.copy(
-                        out=words_out[:, P * b : P * (b + m), :], in_=xt[:].rearrange("p h r -> p r h")
-                    )
+                copy(out=words_out[:, P * first : P * (first + 2), :], in_=xt[:].rearrange("p h r -> p r h"))
 
-        def quantise_x(u):
-            rows = UNIT_SLOTS[u] * P
-            x_codes[u] = ring("x_codes", [P, rows], U32, 64)
-            x_scales[u] = ring("x_scales", [P, rows], U8, 64)
+        def quantise_x(grp):
+            x_codes[grp] = two.tile([P, GROUP_ROWS], U32, align_bytes=64, name="x_codes")
+            x_scales[grp] = two.tile([P, GROUP_ROWS], U8, align_bytes=64, name="x_scales")
             nc.vector.quantize_mx(
-                out=x_codes[u][:].bitcast(FP8X4),
-                scales=x_scales[u][:],
-                in_=grouped[u][:].rearrange("p r t -> p (r t)"),
+                out=x_codes[grp][:].bitcast(FP8X4),
+                scales=x_scales[grp][:],
+                in_=grouped[grp][:].rearrange("p r z -> p (r z)"),
             )
 
-        def project(u):
-            rows = UNIT_SLOTS[u] * P
-            a_t[u] = ring("a_t", [P, CHUNKS, rows], F32)
+        def project(grp):
+            a_t[grp] = two.tile([P, CHUNKS, GROUP_ROWS], F32, name="a_t")
             for c in range(CHUNKS):
-                acc = banks.tile([P, rows], F32, name="acc", tag="bank")
+                acc = banks.tile([P, GROUP_ROWS], F32, name="acc", tag="bank")
                 nc.tensor.matmul_mx(
                     out=acc[:],
                     lhsT=w_codes[:, P * c : P * (c + 1)].bitcast(FP8X4),
                     lhsT_scale=w_scales[:, P * c : P * (c + 1)],
-                    rhs=x_codes[u][:].bitcast(FP8X4),
-                    rhs_scale=x_scales[u][:],
+                    rhs=x_codes[grp][:].bitcast(FP8X4),
+                    rhs_scale=x_scales[grp][:],
                     start=True,
                     stop=True,
                 )
                 nc.scalar.activation(
-                    out=a_t[u][:, c, :],
-                    in_=acc[:],
-                    func=ACT.Relu,
-                    bias=relu_bias[:, c : c + 1],
-                    scale=-0.5 if c < 2 else -2.0,
+                    out=a_t[grp][:, c, :], in_=acc[:], func=ACT.Relu, bias=relu_bias[:, c : c + 1], scale=relu_scale[c]
                 )
 
-        def differences(u):
-            s0, n = first[u], UNIT_SLOTS[u]
-            dm[u] = ring("dm", [P, n, WG], F32)
-            nd[u] = ring("nd", [P, n, WG], F32)
-            dw[u] = ring("dw", [P, n, WG], F32)
-            for s in range(n):
-                slot = s0 + s
+        def times_two_inv_e1(engine, grp, first, last):
+            engine.tensor_tensor(
+                out=dw[grp][:, first:last, :].rearrange("p s (g i u) -> p (s g) i u", g=2, i=NL),
+                in0=dm[grp][:, first:last, :].rearrange("p s (g i u) -> p (s g) i u", g=2, i=NL),
+                in1=two_inv_e1[:, GROUP * grp + first : GROUP * grp + last, :]
+                .rearrange("p s (g u) -> p (s g) u", g=2)
+                .unsqueeze(2)
+                .to_broadcast([P, 2 * (last - first), NL, JT]),
+                op=ALU.mult,
+            )
+
+        def differences(grp):
+            dm[grp] = two.tile([P, GROUP, WG], F32, name="dm")
+            nd[grp] = four.tile([P, GROUP, WG], F32, name="nd")
+            dw[grp] = two.tile([P, GROUP, WG], F32, name="dw")
+            for s in range(GROUP):
+                slot = GROUP * grp + s
                 a_rows = banks.tile([P, 2 * WG], F32, name="a_rows", tag="bank")
                 for c in range(CHUNKS):
-                    if c in PLAIN_IN_DIFFERENCES and s % PLAIN_EVERY == 0:
-                        nc.tensor.matmul(
-                            out=a_rows[:, P * c : P * (c + 1)],
-                            lhsT=a_t[u][:, c, P * s : P * (s + 1)],
-                            rhs=ident[:],
-                            start=True,
-                            stop=True,
-                        )
-                    else:
-                        nc.tensor.transpose(
-                            a_rows[:, P * c : P * (c + 1)], a_t[u][:, c, P * s : P * (s + 1)], ident[:]
-                        )
-                for dst, start_col, top, state in ((dm[u], 0, 1.0, m1_plus1), (nd[u], WG, 4.0, two_less_2v1)):
+                    nc.tensor.transpose(
+                        a_rows[:, P * c : P * (c + 1)], a_t[grp][:, c, P * s : P * (s + 1)], ident[:]
+                    )
+                for dst, start_col, top, state in (
+                    (dm[grp], 0, 1.0, half_less_half_m1),
+                    (nd[grp], WG, 4.0, two_less_2v1),
+                ):
                     nc.vector.scalar_tensor_tensor(
                         out=split(dst[:, s, :]),
                         in0=natural(a_rows[:, start_col : start_col + WG]),
@@ -356,138 +283,130 @@ def tile_chainlveg_pa_t_kernel(
                         op0=ALU.min,
                         op1=ALU.subtract,
                     )
-                if s < GPSIMD_SLOTS[u % 2]:
-                    nc.gpsimd.tensor_tensor(
-                        out=dw[u][:, s, :].rearrange("p (e i c) -> p e i c", e=2, i=NL),
-                        in0=dm[u][:, s, :].rearrange("p (e i c) -> p e i c", e=2, i=NL),
-                        in1=half_inv_e1[:, slot, :]
-                        .rearrange("p (e c) -> p e c", e=2)
-                        .unsqueeze(2)
-                        .to_broadcast([P, 2, NL, JT]),
-                        op=ALU.mult,
-                    )
+                if s < GPSIMD_SLOTS[grp % PAIR]:
+                    times_two_inv_e1(nc.gpsimd, grp, s, s + 1)
 
-        def tanh(u):
-            th[u] = ring("th", [P, UNIT_SLOTS[u], WG], F32)
-            nc.scalar.activation(out=flat(th[u]), in_=flat(nd[u]), func=ACT.Tanh, scale=-0.5)
+        def tanh(grp):
+            th[grp] = two.tile([P, GROUP, WG], F32, name="th")
+            nc.scalar.activation(out=flat(th[grp]), in_=flat(nd[grp]), func=ACT.Tanh, scale=-0.5)
 
-        def shift(u):
-            s0, n = first[u], UNIT_SLOTS[u]
-            y2[u] = ring("y2", [P, n, WG], F32)
-            g = GPSIMD_SLOTS[u % 2]
-            if g < n:
-                nc.vector.tensor_tensor(
-                    out=dw[u][:, g:n, :].rearrange("p s (e i c) -> p (s e) i c", e=2, i=NL),
-                    in0=dm[u][:, g:n, :].rearrange("p s (e i c) -> p (s e) i c", e=2, i=NL),
-                    in1=half_inv_e1[:, s0 + g : s0 + n, :]
-                    .rearrange("p s (e c) -> p (s e) c", e=2)
-                    .unsqueeze(2)
-                    .to_broadcast([P, 2 * (n - g), NL, JT]),
-                    op=ALU.mult,
-                )
+        def shift(grp):
+            y[grp] = two.tile([P, GROUP, WG], F32, name="y")
+            if GPSIMD_SLOTS[grp % PAIR] < GROUP:
+                times_two_inv_e1(nc.vector, grp, GPSIMD_SLOTS[grp % PAIR], GROUP)
             nc.vector.scalar_tensor_tensor(
-                out=flat(y2[u]), in0=flat(th[u]), scalar=1.0, in1=flat(dm[u]), op0=ALU.subtract, op1=ALU.mult
+                out=flat(y[grp]), in0=flat(th[grp]), scalar=1.0, in1=flat(dm[grp]), op0=ALU.subtract, op1=ALU.mult
             )
 
-        def mean(u):
-            s0, n = first[u], UNIT_SLOTS[u]
-            mu = ring("mu", [P, n, WG], F32)
-            zz[u] = ring("zz", [P, n, WG], F32)
-            nc.vector.tensor_tensor(out=flat(zz[u]), in0=flat(y2[u]), in1=flat(dw[u]), op=ALU.mult)
+        def mean(grp):
+            slots = slice(GROUP * grp, GROUP * (grp + 1))
+            mu = three.tile([P, GROUP, WG], F32, name="mu")
+            zz[grp] = two.tile([P, GROUP, WG], F32, name="zz")
+            nc.vector.tensor_tensor(out=flat(zz[grp]), in0=flat(y[grp]), in1=flat(dw[grp]), op=ALU.mult)
             nc.vector.tensor_tensor(
-                out=mu[:].rearrange("p s (i c e) -> p s i c e", i=NL, e=2),
-                in0=y2[u][:].rearrange("p s (e i c) -> p s i c e", i=NL, e=2),
-                in1=m1[:, s0 : s0 + n, :]
-                .rearrange("p s (c e) -> p s c e", e=2)
-                .unsqueeze(2)
-                .to_broadcast([P, n, NL, JT, 2]),
+                out=mu[:].rearrange("p s (i u g) -> p s i u g", i=NL, g=2),
+                in0=y[grp][:].rearrange("p s (g i u) -> p s i u g", i=NL, g=2),
+                in1=m1[:, slots, :].rearrange("p s (u g) -> p s u g", g=2).unsqueeze(2).to_broadcast([P, GROUP, NL, JT, 2]),
                 op=ALU.add,
             )
-            nc.sync.dma_start(out=mu_v[:, s0 : s0 + n, :], in_=mu[:])
+            nc.sync.dma_start(out=mu_v[:, slots, :], in_=mu[:])
 
-        def logs(u):
-            ln_rho2[u] = ring("ln_rho2", [P, UNIT_SLOTS[u], WG], F32)
-            nc.scalar.activation(out=flat(ln_rho2[u]), in_=flat(th[u]), func=ACT.Ln, bias=half[:], scale=0.5)
-            if u in LN_RHO_ON_SCALAR:
-                ln_rho[u] = ring("ln_rho", [P, UNIT_SLOTS[u], WG], F32)
-                nc.scalar.activation(out=flat(ln_rho[u]), in_=flat(th[u]), func=ACT.Ln, bias=half[:], scale=-0.5)
+        def logs(grp):
+            ln_rest[grp] = two.tile([P, GROUP, WG], F32, name="ln_rest")
+            nc.scalar.activation(out=flat(ln_rest[grp]), in_=flat(th[grp]), func=ACT.Ln, bias=half[:], scale=0.5)
+            if scalar_makes_ln_rho(grp):
+                ln_rho[grp] = two.tile([P, GROUP, WG], F32, name="ln_rho")
+                nc.scalar.activation(out=flat(ln_rho[grp]), in_=flat(th[grp]), func=ACT.Ln, bias=half[:], scale=-0.5)
 
-        def deviation(u):
-            s0, n = first[u], UNIT_SLOTS[u]
-            var = ring("var", [P, n, WG], F32)
-            for s in range(n):
+        def deviation(grp):
+            slots = slice(GROUP * grp, GROUP * (grp + 1))
+            var = three.tile([P, GROUP, WG], F32, name="var")
+            for s in range(GROUP):
                 nc.vector.scalar_tensor_tensor(
                     out=natural(var[:, s, :]),
-                    in0=split(ln_rho2[u][:, s, :]),
+                    in0=split(ln_rest[grp][:, s, :]),
                     scalar=0.5,
-                    in1=state_of(v1, s0 + s),
+                    in1=state_of(v1, GROUP * grp + s),
                     op0=ALU.mult,
                     op1=ALU.add,
                 )
-            nc.sync.dma_start(out=var_v[:, s0 : s0 + n, :], in_=var[:])
+            nc.sync.dma_start(out=var_v[:, slots, :], in_=var[:])
 
-        def sum_transposed(u):
-            n = UNIT_SLOTS[u]
-            sum_t_bank[u] = banks.tile([P, n * P], F32, name="sum_t_bank", tag="bank")
-            for s in range(n):
-                terms = (ln_rho, zz) if u in LN_RHO_ON_SCALAR else (nd, ln_rho2, zz)
-                parts = [t[u][:, s, P * e : P * (e + 1)] for t in terms for e in range(2)]
-                if u in W_ON_SCALAR:
-                    parts.insert(0, base_twice[:, first[u] + s, :])
-                for k, part in enumerate(parts):
+        def sum_transposed(grp):
+            terms = (ln_rho, zz) if scalar_makes_ln_rho(grp) else (nd, ln_rest, zz)
+            sum_t_bank[grp] = banks.tile([P, GROUP_ROWS], F32, name="sum_t_bank", tag="bank")
+            for s in range(GROUP):
+                parts = [term[grp][:, s, P * gauss : P * (gauss + 1)] for term in terms for gauss in range(2)]
+                for position, part in enumerate(parts):
                     nc.tensor.matmul(
-                        out=sum_t_bank[u][:, P * s : P * (s + 1)],
+                        out=sum_t_bank[grp][:, P * s : P * (s + 1)],
                         lhsT=part,
                         rhs=ident[:],
-                        is_transpose=not (k == 0 and s % 2 == 0 and PLAIN_IN_SUMS),
-                        start=(k == 0),
-                        stop=(k == len(parts) - 1),
+                        is_transpose=True,
+                        start=(position == 0),
+                        stop=(position == len(parts) - 1),
                     )
 
-        def sum_copy(u):
-            sum_t[u] = ring("sum_t", [P, UNIT_SLOTS[u] * P], F32)
-            nc.scalar.mul(out=sum_t[u][:], in_=sum_t_bank[u][:], mul=0.5)
+        def sum_copy(grp):
+            sum_t[grp] = two.tile([P, GROUP_ROWS], F32, name="sum_t")
+            nc.scalar.mul(out=sum_t[grp][:], in_=sum_t_bank[grp][:], mul=0.5)
 
-        def sum_back(u):
-            n = UNIT_SLOTS[u]
-            sum_bank[u] = banks.tile([P, n * P], F32, name="sum_bank", tag="bank")
-            for s in range(n):
+        def sum_back(grp):
+            sum_bank[grp] = banks.tile([P, GROUP_ROWS], F32, name="sum_bank", tag="bank")
+            for s in range(GROUP):
                 nc.tensor.transpose(
-                    sum_bank[u][:, P * s : P * (s + 1)], sum_t[u][:, P * s : P * (s + 1)], ident[:]
+                    sum_bank[grp][:, P * s : P * (s + 1)], sum_t[grp][:, P * s : P * (s + 1)], ident[:]
                 )
 
-        def weight_out(u):
-            s0, n = first[u], UNIT_SLOTS[u]
-            weight = ring("weight", [P, n, WG // 2], F32)
-            if u in W_ON_SCALAR:
-                nc.scalar.copy(out=flat(weight), in_=sum_bank[u][:])
-            else:
-              nc.vector.tensor_tensor(
-                out=weight[:].rearrange("p s (i c) -> p s i c", i=NL),
-                in0=sum_bank[u][:].rearrange("p (s i c) -> p s i c", s=n, i=NL),
-                in1=base[:, s0 : s0 + n, :].unsqueeze(2).to_broadcast([P, n, NL, JT]),
+        def weight_out(grp):
+            slots = slice(GROUP * grp, GROUP * (grp + 1))
+            weight = three.tile([P, GROUP, WG // 2], F32, name="weight")
+            nc.vector.tensor_tensor(
+                out=weight[:].rearrange("p s (i u) -> p s i u", i=NL),
+                in0=sum_bank[grp][:].rearrange("p (s i u) -> p s i u", s=GROUP, i=NL),
+                in1=base[:, slots, :].unsqueeze(2).to_broadcast([P, GROUP, NL, JT]),
                 op=ALU.add,
             )
-            nc.sync.dma_start(out=scale_v[:, s0 : s0 + n, :], in_=weight[:])
+            nc.sync.dma_start(out=scale_v[:, slots, :], in_=weight[:])
 
-        stage_of = {
-            "state_base": state_base, "state_exp": state_exp, "state_v": state_v, "state_rest": state_rest,
-            "transpose_x": transpose_x, "quantise_x": quantise_x, "project": project, "differences": differences,
-            "tanh": tanh, "shift": shift, "mean": mean, "logs": logs, "deviation": deviation,
-            "sum_transposed": sum_transposed, "sum_copy": sum_copy, "sum_back": sum_back, "weight_out": weight_out,
-        }
+        spread_over_t(v1, svar_raw)
+        state_exp()
+        transpose_x(0, nc.vector.tensor_copy)
+        quantise_x(0)
+        transpose_x(1, nc.vector.tensor_copy)
+        project(0)
+        quantise_x(1)
+        state_offsets()
+        state_base()
+        differences(0)
+        project(1)
+        transpose_x(2, nc.scalar.copy)
+        tanh(0)
+        differences(1)
+        quantise_x(2)
+        transpose_x(3, nc.scalar.copy)
+        tanh(1)
+        quantise_x(3)
 
-        done = set()
-        for name, u in PROLOGUE:
-            stage_of[name](u)
-            done.add((name, u))
-        for r in range(-3, len(ROUNDS) + 3):
-            for entry in ORDER_EVEN if r % 2 == 0 else ORDER_ODD:
-                name, offset = entry[0], entry[1]
-                if 0 <= r + offset < len(ROUNDS):
-                    units = ROUNDS[r + offset]
-                    if len(entry) > 2:
-                        units = units[entry[2] : entry[2] + 1]
-                    for u in units:
-                        if (name, u) not in done:
-                            stage_of[name](u)
+        def for_pair(pair, stage):
+            if 0 <= pair < N_PAIRS:
+                for grp in range(PAIR * pair, PAIR * (pair + 1)):
+                    stage(grp)
+
+        def transpose_x_by_scalar(grp):
+            transpose_x(grp, nc.scalar.copy)
+
+        for step in range(N_PAIRS + 1):
+            for_pair(step + 1, project)
+            for_pair(step - 1, sum_back)
+            for_pair(step, shift)
+            for_pair(step, mean)
+            for_pair(step + 1, differences)
+            for_pair(step - 1, weight_out)
+            for_pair(step, logs)
+            for_pair(step + 2, transpose_x_by_scalar)
+            for_pair(step + 1, tanh)
+            for_pair(step, sum_transposed)
+            for_pair(step, deviation)
+            for_pair(step, sum_copy)
+            for_pair(step + 2, quantise_x)

@@ -19,9 +19,6 @@ ROWS = 4096
 SLOTS = ROWS // P
 GROUP = 4
 GROUP_ROWS = GROUP * P
-N_GROUPS = SLOTS // GROUP
-PAIR = 2
-N_PAIRS = N_GROUPS // PAIR
 NL = 8
 JTG = 32
 JT = 16
@@ -29,13 +26,23 @@ WG = NL * JTG
 CHUNKS = 2 * WG // P
 LOG_2PI = math.log(2.0 * math.pi)
 
-GPSIMD_SLOTS = (4, 1)
+UNITS = [(4 * i, 4) for i in range(8)]
+XLOADS = UNITS
+ROUNDS = [(0, 1), (2, 3), (4, 5), (6, 7)]
+GSL = 5
+LNRHO = (1, 3, 5, 6, 7)
+XC = {0: "V"}
+BASE_T = False
+BS = "V"
+STE = ""
+WS = "S"
+BUFS = dict(grouped=2, x_codes=2, x_scales=2, a_t=2, dm=3, nd=4, dw=5, th=4, y=2, mu=3, var=3, ln_rest=3, ln_rho=3, sum_t=2, weight=3, zs=2, ls=2)
+ZG = ()
+LG = ()
+START = "i0 v0 e0 X0 Q0 X1 P0 h0 Q1 P1 n0 m0 b0 D0 T0 X2 D1 Q2 T1 X3 Q3"
+STEP = "P:-1 B:1 YZ:0 D:-1 M:0 L:0 X:-2 W:1 T:-1 UV:0 C:0 Q:-2"
 
 FLOPS = 2 * ROWS * K * 2 * WG
-
-
-def scalar_makes_ln_rho(grp):
-    return grp % PAIR == 1 or grp // PAIR == N_PAIRS - 1
 
 
 def tile_chainlveg_pa_t_kernel(
@@ -66,9 +73,11 @@ def tile_chainlveg_pa_t_kernel(
 
     with ExitStack() as stack:
         keep = stack.enter_context(tc.tile_pool(name="keep", bufs=1))
-        two = stack.enter_context(tc.tile_pool(name="two", bufs=PAIR))
-        three = stack.enter_context(tc.tile_pool(name="three", bufs=3))
-        four = stack.enter_context(tc.tile_pool(name="four", bufs=2 * PAIR))
+        pool_of = {}
+        def pools(n):
+            if n not in pool_of:
+                pool_of[n] = stack.enter_context(tc.tile_pool(name=n, bufs=BUFS.get(n, 2)))
+            return pool_of[n]
         banks = stack.enter_context(tc.psum_pool(name="banks", bufs=8))
         stack.enter_context(tc.manual_schedule())
 
@@ -83,54 +92,57 @@ def tile_chainlveg_pa_t_kernel(
         nc.vector.tensor_scalar(
             out=ln_2[:], in0=half[:], scalar1=0.0, scalar2=math.log(2.0), op0=ALU.mult, op1=ALU.add
         )
-
         x_sb = keep.tile([P, SLOTS, K], BF16)
         smu_raw = keep.tile([P, SLOTS, NL * 2], BF16)
         svar_raw = keep.tile([P, SLOTS, NL * 2], BF16)
         sw_raw = keep.tile([P, SLOTS, NL], BF16)
 
-        def load_x(grp):
-            slots = slice(GROUP * grp, GROUP * (grp + 1))
-            nc.sync.dma_start(out=x_sb[:, slots, :], in_=x_v[:, slots, :])
+        def load_x(first, count):
+            nc.sync.dma_start(out=x_sb[:, first : first + count, :], in_=x_v[:, first : first + count, :])
 
-        nc.scalar.dma_start(out=bias_rows[0:2, :], in_=tcm_b.rearrange("(c n) -> c n", c=2))
-        nc.scalar.dma_start(out=bias_rows[2:4, :], in_=tcv_b.rearrange("(c n) -> c n", c=2))
-        load_x(0)
-        nc.scalar.dma_start(out=svar_raw[:], in_=svar_v)
-        nc.scalar.dma_start(out=smu_raw[:], in_=smu_v)
-        nc.sync.dma_start(out=sw_raw[:], in_=sw_v)
-        warm = keep.tile([P, 1], F32)
-        nc.scalar.activation(out=warm[:], in_=half[:], func=ACT.Exp)
-        for which, words in enumerate((tcm_w_words, tcv_w_words)):
+        def load_w(which, words):
             nc.sync.dma_start(
                 out=w_codes[:, WG * which : WG * (which + 1)].bitcast(I32),
                 in_=words[0].rearrange("p n z -> p (n z)").bitcast(I32),
             )
-        load_x(1)
+
+        load_x(*XLOADS[0])
+        nc.scalar.dma_start(out=svar_raw[:], in_=svar_v)
+        load_w(0, tcm_w_words)
+        nc.scalar.dma_start(out=bias_rows[0:2, :], in_=tcm_b.rearrange("(c n) -> c n", c=2))
+        nc.scalar.dma_start(out=bias_rows[2:4, :], in_=tcv_b.rearrange("(c n) -> c n", c=2))
+        load_w(1, tcv_w_words)
+        load_x(*XLOADS[1])
+        nc.scalar.dma_start(out=smu_raw[:], in_=smu_v)
+        warm = keep.tile([P, 1], F32)
+        nc.scalar.activation(out=warm[:], in_=half[:], func=ACT.Exp)
         for which, scales in enumerate((tcm_w_scales, tcv_w_scales)):
             for quad in range(4):
                 nc.sync.dma_start(
                     out=w_scales[32 * quad : 32 * quad + 4, WG * which : WG * (which + 1)].bitcast(I32),
                     in_=scales[0][4 * quad : 4 * quad + 4, :].bitcast(I32),
                 )
-        for grp in range(2, N_GROUPS):
-            load_x(grp)
+        load_x(*XLOADS[2])
+        nc.sync.dma_start(out=sw_raw[:], in_=sw_v)
+        for f, c in XLOADS[3:]:
+            load_x(f, c)
 
         ident = keep.tile([P, P], F32)
         make_identity(nc, ident[:])
-
         bias_f32 = keep.tile([P, P], F32)
-        nc.vector.tensor_copy(out=bias_f32[:], in_=bias_rows[:])
-        bias_bank = banks.tile([P, GROUP_ROWS], F32, name="bias_bank", tag="bank")
-        nc.tensor.transpose(bias_bank[:, 0:P], bias_f32[:], ident[:])
         relu_scale = (-0.5, -0.5, -2.0, -2.0)
         relu_bias = keep.tile([P, CHUNKS], F32)
-        nc.vector.tensor_scalar(
-            out=relu_bias[:, 0:2], in0=bias_bank[:, 0:2], scalar1=-0.5, scalar2=0.5, op0=ALU.mult, op1=ALU.add
-        )
-        nc.vector.tensor_scalar(
-            out=relu_bias[:, 2:4], in0=bias_bank[:, 2:4], scalar1=-2.0, scalar2=2.0, op0=ALU.mult, op1=ALU.add
-        )
+
+        def biases():
+            nc.vector.tensor_copy(out=bias_f32[:], in_=bias_rows[:])
+            bias_bank = banks.tile([P, GROUP_ROWS], F32, name="bias_bank", tag="bank")
+            nc.tensor.transpose(bias_bank[:, 0:P], bias_f32[:], ident[:])
+            nc.vector.tensor_scalar(
+                out=relu_bias[:, 0:2], in0=bias_bank[:, 0:2], scalar1=-0.5, scalar2=0.5, op0=ALU.mult, op1=ALU.add
+            )
+            nc.vector.tensor_scalar(
+                out=relu_bias[:, 2:4], in0=bias_bank[:, 2:4], scalar1=-2.0, scalar2=2.0, op0=ALU.mult, op1=ALU.add
+            )
 
         def natural(ap):
             return ap.rearrange("p (i u g) -> p i u g", i=NL, g=2)
@@ -138,17 +150,18 @@ def tile_chainlveg_pa_t_kernel(
         def split(ap):
             return ap.rearrange("p (g i u) -> p i u g", i=NL, g=2)
 
-        def flat(t):
-            return t[:].rearrange("p s n -> p (s n)")
-
-        def spread_over_t(dst, src):
-            nc.vector.tensor_copy(
-                out=dst[:].rearrange("p s (j t g) -> p (s j) t g", t=2, g=2),
-                in_=src[:].rearrange("p s (j g) -> p (s j) g", g=2).unsqueeze(2).to_broadcast([P, SLOTS * NL, 2, 2]),
-            )
+        def flat(t, n):
+            return t[:, 0:n, :].rearrange("p s n -> p (s n)")
 
         def state_of(tile_, slot):
             return tile_[:, slot, :].rearrange("p (u g) -> p u g", g=2).unsqueeze(1).to_broadcast([P, NL, JT, 2])
+
+        def spread(engine, dst, src, scale, offset):
+            engine.tensor_scalar(
+                out=dst[:].rearrange("p s (j t g) -> p (s j) t g", t=2, g=2),
+                in0=src[:].rearrange("p s (j g) -> p (s j) g", g=2).unsqueeze(2).to_broadcast([P, SLOTS * NL, 2, 2]),
+                scalar1=scale, scalar2=offset, op0=ALU.mult, op1=ALU.add,
+            )
 
         v1 = keep.tile([P, SLOTS, JTG], F32)
         two_less_2v1 = keep.tile([P, SLOTS, JTG], F32)
@@ -158,23 +171,13 @@ def tile_chainlveg_pa_t_kernel(
         v1_sum = keep.tile([P, SLOTS * NL], F32)
         base_j = keep.tile([P, SLOTS * NL], F32)
         base = keep.tile([P, SLOTS, JT], F32)
+        base_i = keep.tile([P, SLOTS, NL * JT], F32, name="base_i") if BASE_T else None
 
         def state_exp():
             nc.scalar.activation(
                 out=two_inv_e1[:].rearrange("p s (g u) -> p s u g", g=2),
                 in_=v1[:].rearrange("p s (u g) -> p s u g", g=2),
-                func=ACT.Exp,
-                scale=-2.0,
-                bias=ln_2[:],
-            )
-
-        def state_offsets():
-            nc.vector.tensor_scalar(
-                out=two_less_2v1[:], in0=v1[:], scalar1=-2.0, scalar2=2.0, op0=ALU.mult, op1=ALU.add
-            )
-            spread_over_t(m1, smu_raw)
-            nc.vector.tensor_scalar(
-                out=half_less_half_m1[:], in0=m1[:], scalar1=-0.5, scalar2=0.5, op0=ALU.mult, op1=ALU.add
+                func=ACT.Exp, scale=-2.0, bias=ln_2[:],
             )
 
         def state_base():
@@ -186,227 +189,239 @@ def tile_chainlveg_pa_t_kernel(
             nc.vector.tensor_scalar(
                 out=base[:].rearrange("p s (j t) -> p (s j) t", t=2),
                 in0=base_j[:].unsqueeze(2).to_broadcast([P, SLOTS * NL, 2]),
-                scalar1=1.0,
-                scalar2=-LOG_2PI,
-                op0=ALU.mult,
-                op1=ALU.add,
+                scalar1=2.0 if BASE_T else 1.0, scalar2=-2 * LOG_2PI if BASE_T else -LOG_2PI, op0=ALU.mult, op1=ALU.add,
             )
 
-        grouped = {}
-        x_codes = {}
-        x_scales = {}
-        a_t = {}
-        dm = {}
-        nd = {}
-        dw = {}
-        th = {}
-        y = {}
-        zz = {}
-        ln_rest = {}
-        ln_rho = {}
-        sum_t_bank = {}
-        sum_t = {}
-        sum_bank = {}
+        def base_spread():
+            BSE = nc.vector if BS == "V" else nc.gpsimd
+            BSE.tensor_scalar(
+                out=base_i[:].rearrange("p s (i u) -> p s i u", i=NL),
+                in0=base[:].unsqueeze(2).to_broadcast([P, SLOTS, NL, JT]),
+                scalar1=1.0, scalar2=0.0, op0=ALU.mult, op1=ALU.add,
+            )
 
-        def transpose_x(grp, copy):
-            grouped[grp] = two.tile([P, GROUP_ROWS, 4], BF16, align_bytes=64, name="grouped")
+        grouped = {}; x_codes = {}; x_scales = {}; a_t = {}; dm = {}; nd = {}; dw = {}; th = {}; y = {}
+        ln_rest = {}; ln_rho = {}; sum_t_bank = {}; sum_t = {}; sum_bank = {}; zs = {}; ls = {}
+
+        def transpose_x(u, copies):
+            s0, n = UNITS[u]
+            grouped[u] = pools("grouped").tile([P, GROUP_ROWS, 4], BF16, align_bytes=64, name="grouped")
             words_out = (
-                grouped[grp][:].rearrange("p r z -> p (r z)").bitcast(F32).rearrange("p (r h) -> p r h", h=2)
+                grouped[u][:].rearrange("p r z -> p (r z)").bitcast(F32).rearrange("p (r h) -> p r h", h=2)
             )
-            x_words = x_sb[:, GROUP * grp : GROUP * (grp + 1), :].bitcast(F32)
-            for first in range(0, GROUP, 2):
+            x_words = x_sb[:, s0 : s0 + n, :].bitcast(F32)
+            for first in range(0, n, 2):
                 xt = banks.tile([P, 2, 2 * P], F32, name="xt", tag="bank")
                 for s in range(2):
                     for h in range(2):
                         nc.tensor.transpose(
                             xt[:, h, P * s : P * (s + 1)], x_words[:, first + s, h : K // 2 : 2], ident[:]
                         )
-                copy(out=words_out[:, P * first : P * (first + 2), :], in_=xt[:].rearrange("p h r -> p r h"))
+                copies[(first // 2) % len(copies)](out=words_out[:, P * first : P * (first + 2), :], in_=xt[:].rearrange("p h r -> p r h"))
 
-        def quantise_x(grp):
-            x_codes[grp] = two.tile([P, GROUP_ROWS], U32, align_bytes=64, name="x_codes")
-            x_scales[grp] = two.tile([P, GROUP_ROWS], U8, align_bytes=64, name="x_scales")
+        def quantise_x(u):
+            n = UNITS[u][1]
+            x_codes[u] = pools("x_codes").tile([P, GROUP_ROWS], U32, align_bytes=64, name="x_codes")
+            x_scales[u] = pools("x_scales").tile([P, GROUP_ROWS], U8, align_bytes=64, name="x_scales")
             nc.vector.quantize_mx(
-                out=x_codes[grp][:].bitcast(FP8X4),
-                scales=x_scales[grp][:],
-                in_=grouped[grp][:].rearrange("p r z -> p (r z)"),
+                out=x_codes[u][:, 0 : P * n].bitcast(FP8X4),
+                scales=x_scales[u][:, 0 : P * n],
+                in_=grouped[u][:, 0 : P * n, :].rearrange("p r z -> p (r z)"),
             )
 
-        def project(grp):
-            a_t[grp] = two.tile([P, CHUNKS, GROUP_ROWS], F32, name="a_t")
+        def project(u):
+            n = UNITS[u][1]
+            a_t[u] = pools("a_t").tile([P, CHUNKS, GROUP_ROWS], F32, name="a_t")
             for c in range(CHUNKS):
                 acc = banks.tile([P, GROUP_ROWS], F32, name="acc", tag="bank")
                 nc.tensor.matmul_mx(
-                    out=acc[:],
+                    out=acc[:, 0 : P * n],
                     lhsT=w_codes[:, P * c : P * (c + 1)].bitcast(FP8X4),
                     lhsT_scale=w_scales[:, P * c : P * (c + 1)],
-                    rhs=x_codes[grp][:].bitcast(FP8X4),
-                    rhs_scale=x_scales[grp][:],
-                    start=True,
-                    stop=True,
+                    rhs=x_codes[u][:, 0 : P * n].bitcast(FP8X4),
+                    rhs_scale=x_scales[u][:, 0 : P * n],
+                    start=True, stop=True,
                 )
                 nc.scalar.activation(
-                    out=a_t[grp][:, c, :], in_=acc[:], func=ACT.Relu, bias=relu_bias[:, c : c + 1], scale=relu_scale[c]
+                    out=a_t[u][:, c, 0 : P * n], in_=acc[:, 0 : P * n], func=ACT.Relu, bias=relu_bias[:, c : c + 1], scale=relu_scale[c]
                 )
 
-        def times_two_inv_e1(engine, grp, first, last):
+        def times_two_inv_e1(engine, u, first, last):
+            s0, n = UNITS[u]
             engine.tensor_tensor(
-                out=dw[grp][:, first:last, :].rearrange("p s (g i u) -> p (s g) i u", g=2, i=NL),
-                in0=dm[grp][:, first:last, :].rearrange("p s (g i u) -> p (s g) i u", g=2, i=NL),
-                in1=two_inv_e1[:, GROUP * grp + first : GROUP * grp + last, :]
+                out=dw[u][:, first:last, :].rearrange("p s (g i u) -> p (s g) i u", g=2, i=NL),
+                in0=dm[u][:, first:last, :].rearrange("p s (g i u) -> p (s g) i u", g=2, i=NL),
+                in1=two_inv_e1[:, s0 + first : s0 + last, :]
                 .rearrange("p s (g u) -> p (s g) u", g=2)
                 .unsqueeze(2)
                 .to_broadcast([P, 2 * (last - first), NL, JT]),
                 op=ALU.mult,
             )
 
-        def differences(grp):
-            dm[grp] = two.tile([P, GROUP, WG], F32, name="dm")
-            nd[grp] = four.tile([P, GROUP, WG], F32, name="nd")
-            dw[grp] = two.tile([P, GROUP, WG], F32, name="dw")
-            for s in range(GROUP):
-                slot = GROUP * grp + s
+        def gp_slots(u):
+            s0, n = UNITS[u]
+            return len([s for s in range(s0, s0 + n) if s % 8 < GSL])
+
+        def differences(u):
+            s0, n = UNITS[u]
+            dm[u] = pools("dm").tile([P, GROUP, WG], F32, name="dm")
+            nd[u] = pools("nd").tile([P, GROUP, WG], F32, name="nd")
+            dw[u] = pools("dw").tile([P, GROUP, WG], F32, name="dw")
+            for s in range(n):
                 a_rows = banks.tile([P, 2 * WG], F32, name="a_rows", tag="bank")
                 for c in range(CHUNKS):
                     nc.tensor.transpose(
-                        a_rows[:, P * c : P * (c + 1)], a_t[grp][:, c, P * s : P * (s + 1)], ident[:]
+                        a_rows[:, P * c : P * (c + 1)], a_t[u][:, c, P * s : P * (s + 1)], ident[:]
                     )
                 for dst, start_col, top, state in (
-                    (dm[grp], 0, 1.0, half_less_half_m1),
-                    (nd[grp], WG, 4.0, two_less_2v1),
+                    (dm[u], 0, 1.0, half_less_half_m1),
+                    (nd[u], WG, 4.0, two_less_2v1),
                 ):
                     nc.vector.scalar_tensor_tensor(
                         out=split(dst[:, s, :]),
                         in0=natural(a_rows[:, start_col : start_col + WG]),
                         scalar=top,
-                        in1=state_of(state, slot),
+                        in1=state_of(state, s0 + s),
                         op0=ALU.min,
                         op1=ALU.subtract,
                     )
-                if s < GPSIMD_SLOTS[grp % PAIR]:
-                    times_two_inv_e1(nc.gpsimd, grp, s, s + 1)
+                if s < gp_slots(u):
+                    times_two_inv_e1(nc.gpsimd, u, s, s + 1)
 
-        def tanh(grp):
-            th[grp] = two.tile([P, GROUP, WG], F32, name="th")
-            nc.scalar.activation(out=flat(th[grp]), in_=flat(nd[grp]), func=ACT.Tanh, scale=-0.5)
+        def tanh(u):
+            n = UNITS[u][1]
+            th[u] = pools("th").tile([P, GROUP, WG], F32, name="th")
+            nc.scalar.activation(out=flat(th[u], n), in_=flat(nd[u], n), func=ACT.Tanh, scale=-0.5)
 
-        def shift(grp):
-            y[grp] = two.tile([P, GROUP, WG], F32, name="y")
-            if GPSIMD_SLOTS[grp % PAIR] < GROUP:
-                times_two_inv_e1(nc.vector, grp, GPSIMD_SLOTS[grp % PAIR], GROUP)
+        def shift(u):
+            n = UNITS[u][1]
+            y[u] = pools("y").tile([P, GROUP, WG], F32, name="y")
+            if gp_slots(u) < n:
+                times_two_inv_e1(nc.vector, u, gp_slots(u), n)
             nc.vector.scalar_tensor_tensor(
-                out=flat(y[grp]), in0=flat(th[grp]), scalar=1.0, in1=flat(dm[grp]), op0=ALU.subtract, op1=ALU.mult
+                out=flat(y[u], n), in0=flat(th[u], n), scalar=1.0, in1=flat(dm[u], n), op0=ALU.subtract, op1=ALU.mult
             )
 
-        def mean(grp):
-            slots = slice(GROUP * grp, GROUP * (grp + 1))
-            mu = three.tile([P, GROUP, WG], F32, name="mu")
-            zz[grp] = two.tile([P, GROUP, WG], F32, name="zz")
-            nc.vector.tensor_tensor(out=flat(zz[grp]), in0=flat(y[grp]), in1=flat(dw[grp]), op=ALU.mult)
+        def product(u):
+            n = UNITS[u][1]
+            nc.vector.tensor_tensor(out=flat(dw[u], n), in0=flat(y[u], n), in1=flat(dw[u], n), op=ALU.mult)
+
+        def sum_zz(u):
+            s0, n = UNITS[u]
+            if u in ZG:
+                zs[u] = pools("zs").tile([P, GROUP, WG // 2], F32, name="zs")
+                nc.gpsimd.tensor_tensor(out=zs[u][:, 0:n, :], in0=dw[u][:, 0:n, 0:P], in1=dw[u][:, 0:n, P : 2 * P], op=ALU.add)
+        def sum_ln(u):
+            s0, n = UNITS[u]
+            if u in LG:
+                ls[u] = pools("ls").tile([P, GROUP, WG // 2], F32, name="ls")
+                nc.gpsimd.tensor_tensor(out=ls[u][:, 0:n, :], in0=ln_rho[u][:, 0:n, 0:P], in1=ln_rho[u][:, 0:n, P : 2 * P], op=ALU.add)
+
+        def mean(u):
+            s0, n = UNITS[u]
+            mu = pools("mu").tile([P, GROUP, WG], F32, name="mu")
             nc.vector.tensor_tensor(
-                out=mu[:].rearrange("p s (i u g) -> p s i u g", i=NL, g=2),
-                in0=y[grp][:].rearrange("p s (g i u) -> p s i u g", i=NL, g=2),
-                in1=m1[:, slots, :].rearrange("p s (u g) -> p s u g", g=2).unsqueeze(2).to_broadcast([P, GROUP, NL, JT, 2]),
+                out=mu[:, 0:n, :].rearrange("p s (i u g) -> p s i u g", i=NL, g=2),
+                in0=y[u][:, 0:n, :].rearrange("p s (g i u) -> p s i u g", i=NL, g=2),
+                in1=m1[:, s0 : s0 + n, :].rearrange("p s (u g) -> p s u g", g=2).unsqueeze(2).to_broadcast([P, n, NL, JT, 2]),
                 op=ALU.add,
             )
-            nc.sync.dma_start(out=mu_v[:, slots, :], in_=mu[:])
+            nc.sync.dma_start(out=mu_v[:, s0 : s0 + n, :], in_=mu[:, 0:n, :])
 
-        def logs(grp):
-            ln_rest[grp] = two.tile([P, GROUP, WG], F32, name="ln_rest")
-            nc.scalar.activation(out=flat(ln_rest[grp]), in_=flat(th[grp]), func=ACT.Ln, bias=half[:], scale=0.5)
-            if scalar_makes_ln_rho(grp):
-                ln_rho[grp] = two.tile([P, GROUP, WG], F32, name="ln_rho")
-                nc.scalar.activation(out=flat(ln_rho[grp]), in_=flat(th[grp]), func=ACT.Ln, bias=half[:], scale=-0.5)
+        def logs(u):
+            n = UNITS[u][1]
+            ln_rest[u] = pools("ln_rest").tile([P, GROUP, WG], F32, name="ln_rest")
+            nc.scalar.activation(out=flat(ln_rest[u], n), in_=flat(th[u], n), func=ACT.Ln, bias=half[:], scale=0.5)
+            if u in LNRHO:
+                ln_rho[u] = pools("ln_rho").tile([P, GROUP, WG], F32, name="ln_rho")
+                nc.scalar.activation(out=flat(ln_rho[u], n), in_=flat(th[u], n), func=ACT.Ln, bias=half[:], scale=-0.5)
 
-        def deviation(grp):
-            slots = slice(GROUP * grp, GROUP * (grp + 1))
-            var = three.tile([P, GROUP, WG], F32, name="var")
-            for s in range(GROUP):
+        def deviation(u):
+            s0, n = UNITS[u]
+            var = pools("var").tile([P, GROUP, WG], F32, name="var")
+            for s in range(n):
                 nc.vector.scalar_tensor_tensor(
                     out=natural(var[:, s, :]),
-                    in0=split(ln_rest[grp][:, s, :]),
+                    in0=split(ln_rest[u][:, s, :]),
                     scalar=0.5,
-                    in1=state_of(v1, GROUP * grp + s),
+                    in1=state_of(v1, s0 + s),
                     op0=ALU.mult,
                     op1=ALU.add,
                 )
-            nc.sync.dma_start(out=var_v[:, slots, :], in_=var[:])
+            nc.sync.dma_start(out=var_v[:, s0 : s0 + n, :], in_=var[:, 0:n, :])
 
-        def sum_transposed(grp):
-            terms = (ln_rho, zz) if scalar_makes_ln_rho(grp) else (nd, ln_rest, zz)
-            sum_t_bank[grp] = banks.tile([P, GROUP_ROWS], F32, name="sum_t_bank", tag="bank")
-            for s in range(GROUP):
-                parts = [term[grp][:, s, P * gauss : P * (gauss + 1)] for term in terms for gauss in range(2)]
+        def sum_transposed(u):
+            s0, n = UNITS[u]
+            terms = (ln_rho[u], dw[u]) if u in LNRHO else (nd[u], ln_rest[u], dw[u])
+            sum_t_bank[u] = banks.tile([P, GROUP_ROWS], F32, name="sum_t_bank", tag="bank")
+            for s in range(n):
+                parts = [term[:, s, P * gauss : P * (gauss + 1)] for term in terms for gauss in range(2)]
+                if u in ZG:
+                    parts = parts[:-2] + [zs[u][:, s, :]]
+                if u in LG:
+                    parts = [ls[u][:, s, :]] + parts[2:]
+                if BASE_T:
+                    parts = [base_i[:, s0 + s, :]] + parts
                 for position, part in enumerate(parts):
                     nc.tensor.matmul(
-                        out=sum_t_bank[grp][:, P * s : P * (s + 1)],
-                        lhsT=part,
-                        rhs=ident[:],
-                        is_transpose=True,
-                        start=(position == 0),
-                        stop=(position == len(parts) - 1),
+                        out=sum_t_bank[u][:, P * s : P * (s + 1)],
+                        lhsT=part, rhs=ident[:], is_transpose=True,
+                        start=(position == 0), stop=(position == len(parts) - 1),
                     )
 
-        def sum_copy(grp):
-            sum_t[grp] = two.tile([P, GROUP_ROWS], F32, name="sum_t")
-            nc.scalar.mul(out=sum_t[grp][:], in_=sum_t_bank[grp][:], mul=0.5)
+        def sum_copy(u):
+            n = UNITS[u][1]
+            sum_t[u] = pools("sum_t").tile([P, GROUP_ROWS], F32, name="sum_t")
+            nc.scalar.mul(out=sum_t[u][:, 0 : P * n], in_=sum_t_bank[u][:, 0 : P * n], mul=0.5)
 
-        def sum_back(grp):
-            sum_bank[grp] = banks.tile([P, GROUP_ROWS], F32, name="sum_bank", tag="bank")
-            for s in range(GROUP):
+        def sum_back(u):
+            n = UNITS[u][1]
+            sum_bank[u] = banks.tile([P, GROUP_ROWS], F32, name="sum_bank", tag="bank")
+            for s in range(n):
                 nc.tensor.transpose(
-                    sum_bank[grp][:, P * s : P * (s + 1)], sum_t[grp][:, P * s : P * (s + 1)], ident[:]
+                    sum_bank[u][:, P * s : P * (s + 1)], sum_t[u][:, P * s : P * (s + 1)], ident[:]
                 )
 
-        def weight_out(grp):
-            slots = slice(GROUP * grp, GROUP * (grp + 1))
-            weight = three.tile([P, GROUP, WG // 2], F32, name="weight")
-            nc.vector.tensor_tensor(
-                out=weight[:].rearrange("p s (i u) -> p s i u", i=NL),
-                in0=sum_bank[grp][:].rearrange("p (s i u) -> p s i u", s=GROUP, i=NL),
-                in1=base[:, slots, :].unsqueeze(2).to_broadcast([P, GROUP, NL, JT]),
-                op=ALU.add,
-            )
-            nc.sync.dma_start(out=scale_v[:, slots, :], in_=weight[:])
+        def weight_out(u):
+            s0, n = UNITS[u]
+            weight = pools("weight").tile([P, GROUP, WG // 2], F32, name="weight")
+            if BASE_T:
+                (nc.scalar.copy if WS == "S" else nc.vector.tensor_copy)(out=flat(weight, n), in_=sum_bank[u][:, 0 : P * n])
+            else:
+                nc.vector.tensor_tensor(
+                    out=weight[:, 0:n, :].rearrange("p s (i u) -> p s i u", i=NL),
+                    in0=sum_bank[u][:, 0 : P * n].rearrange("p (s i u) -> p s i u", s=n, i=NL),
+                    in1=base[:, s0 : s0 + n, :].unsqueeze(2).to_broadcast([P, n, NL, JT]),
+                    op=ALU.add,
+                )
+            nc.sync.dma_start(out=scale_v[:, s0 : s0 + n, :], in_=weight[:, 0:n, :])
 
-        spread_over_t(v1, svar_raw)
-        state_exp()
-        transpose_x(0, nc.vector.tensor_copy)
-        quantise_x(0)
-        transpose_x(1, nc.vector.tensor_copy)
-        project(0)
-        quantise_x(1)
-        state_offsets()
-        state_base()
-        differences(0)
-        project(1)
-        transpose_x(2, nc.scalar.copy)
-        tanh(0)
-        differences(1)
-        quantise_x(2)
-        transpose_x(3, nc.scalar.copy)
-        tanh(1)
-        quantise_x(3)
+        V_, S_ = nc.vector.tensor_copy, nc.scalar.copy
+        STAGES = dict(
+            X=lambda g: transpose_x(g, XC.get(g, "S") == "V" and [V_] or XC.get(g, "S") == "VS" and [V_, S_] or [S_]),
+            Q=quantise_x, P=project, D=differences, T=tanh, Y=shift, Z=lambda g: (product(g), sum_zz(g)), M=mean, L=lambda g: (logs(g), sum_ln(g)), U=sum_transposed,
+            C=sum_copy, B=sum_back, W=weight_out, V=deviation,
+            e=lambda g: state_exp(), v=lambda g: spread(nc.gpsimd if "v" in STE else nc.vector, v1, svar_raw, 1.0, 0.0),
+            n=lambda g: spread(nc.gpsimd if "n" in STE else nc.vector, two_less_2v1, svar_raw, -2.0, 2.0),
+            m=lambda g: spread(nc.gpsimd if "m" in STE else nc.vector, m1, smu_raw, 1.0, 0.0),
+            h=lambda g: spread(nc.gpsimd if "h" in STE else nc.vector, half_less_half_m1, smu_raw, -0.5, 0.5),
+            b=lambda g: state_base(), s=lambda g: base_spread(), i=lambda g: biases(),
+        )
 
-        def for_pair(pair, stage):
-            if 0 <= pair < N_PAIRS:
-                for grp in range(PAIR * pair, PAIR * (pair + 1)):
-                    stage(grp)
+        done = set()
 
-        def transpose_x_by_scalar(grp):
-            transpose_x(grp, nc.scalar.copy)
+        def emit(stage, unit):
+            if (stage, unit) not in done:
+                done.add((stage, unit))
+                STAGES[stage](unit)
 
-        for step in range(N_PAIRS + 1):
-            for_pair(step + 1, project)
-            for_pair(step - 1, sum_back)
-            for_pair(step, shift)
-            for_pair(step, mean)
-            for_pair(step + 1, differences)
-            for_pair(step - 1, weight_out)
-            for_pair(step, logs)
-            for_pair(step + 2, transpose_x_by_scalar)
-            for_pair(step + 1, tanh)
-            for_pair(step, sum_transposed)
-            for_pair(step, deviation)
-            for_pair(step, sum_copy)
-            for_pair(step + 2, quantise_x)
+        for word in START.split():
+            emit(word[0], int(word[1:]))
+
+        for step in range(-4, len(ROUNDS) + 4):
+            for word in STEP.split():
+                stages, lag = word.split(":")
+                if 0 <= step - int(lag) < len(ROUNDS):
+                    for unit in ROUNDS[step - int(lag)]:
+                        for stage in stages:
+                            emit(stage, unit)

@@ -39,8 +39,10 @@ WS = "S"
 BUFS = dict(grouped=2, x_codes=2, x_scales=2, a_t=2, dm=3, nd=4, dw=5, th=4, y=2, mu=3, var=3, ln_rest=3, ln_rho=3, sum_t=2, weight=3, zs=2, ls=2)
 ZG = ()
 LG = ()
-START = "i0 v0 e0 X0 Q0 X1 P0 h0 Q1 P1 n0 m0 b0 D0 T0 X2 D1 Q2 T1 X3 Q3"
-STEP = "P:-1 B:1 YZ:0 D:-1 M:0 L:0 X:-2 W:1 T:-1 UV:0 C:0 Q:-2"
+MMR = 0
+MMO = 0
+START = "X0 Q0 X1 i0 P0 v0 h0 m0 Q1 e0 n0 b0 P1 D0 X2 D1 T0 X3 T1 Q2 Q3"
+STEP = "X:-2 Y:0 Z:0 P:-1 LM:0 D:-1 BW:1 T:-1 U:0 Q:-2 C:0 V:0"
 
 FLOPS = 2 * ROWS * K * 2 * WG
 
@@ -106,25 +108,24 @@ def tile_chainlveg_pa_t_kernel(
                 in_=words[0].rearrange("p n z -> p (n z)").bitcast(I32),
             )
 
-        load_x(*XLOADS[0])
-        nc.scalar.dma_start(out=svar_raw[:], in_=svar_v)
-        load_w(0, tcm_w_words)
         nc.scalar.dma_start(out=bias_rows[0:2, :], in_=tcm_b.rearrange("(c n) -> c n", c=2))
         nc.scalar.dma_start(out=bias_rows[2:4, :], in_=tcv_b.rearrange("(c n) -> c n", c=2))
-        load_w(1, tcv_w_words)
-        load_x(*XLOADS[1])
+        load_x(*XLOADS[0])
+        nc.scalar.dma_start(out=svar_raw[:], in_=svar_v)
         nc.scalar.dma_start(out=smu_raw[:], in_=smu_v)
         warm = keep.tile([P, 1], F32)
         nc.scalar.activation(out=warm[:], in_=half[:], func=ACT.Exp)
+        load_w(0, tcm_w_words)
+        load_w(1, tcv_w_words)
+        load_x(*XLOADS[1])
         for which, scales in enumerate((tcm_w_scales, tcv_w_scales)):
             for quad in range(4):
                 nc.sync.dma_start(
                     out=w_scales[32 * quad : 32 * quad + 4, WG * which : WG * (which + 1)].bitcast(I32),
                     in_=scales[0][4 * quad : 4 * quad + 4, :].bitcast(I32),
                 )
-        load_x(*XLOADS[2])
         nc.sync.dma_start(out=sw_raw[:], in_=sw_v)
-        for f, c in XLOADS[3:]:
+        for f, c in XLOADS[2:]:
             load_x(f, c)
 
         ident = keep.tile([P, P], F32)
@@ -203,6 +204,10 @@ def tile_chainlveg_pa_t_kernel(
         grouped = {}; x_codes = {}; x_scales = {}; a_t = {}; dm = {}; nd = {}; dw = {}; th = {}; y = {}
         ln_rest = {}; ln_rho = {}; sum_t_bank = {}; sum_t = {}; sum_bank = {}; zs = {}; ls = {}
 
+        def turn(index, out, in_, start=True, stop=True):
+            plain = MMR > 0 and index % MMR == MMO
+            nc.tensor.matmul(out=out, lhsT=in_, rhs=ident[:], is_transpose=not plain, start=start, stop=stop)
+
         def transpose_x(u, copies):
             s0, n = UNITS[u]
             grouped[u] = pools("grouped").tile([P, GROUP_ROWS, 4], BF16, align_bytes=64, name="grouped")
@@ -270,9 +275,7 @@ def tile_chainlveg_pa_t_kernel(
             for s in range(n):
                 a_rows = banks.tile([P, 2 * WG], F32, name="a_rows", tag="bank")
                 for c in range(CHUNKS):
-                    nc.tensor.transpose(
-                        a_rows[:, P * c : P * (c + 1)], a_t[u][:, c, P * s : P * (s + 1)], ident[:]
-                    )
+                    turn(4 * s + c, a_rows[:, P * c : P * (c + 1)], a_t[u][:, c, P * s : P * (s + 1)])
                 for dst, start_col, top, state in (
                     (dm[u], 0, 1.0, half_less_half_m1),
                     (nd[u], WG, 4.0, two_less_2v1),
@@ -363,11 +366,7 @@ def tile_chainlveg_pa_t_kernel(
                 if BASE_T:
                     parts = [base_i[:, s0 + s, :]] + parts
                 for position, part in enumerate(parts):
-                    nc.tensor.matmul(
-                        out=sum_t_bank[u][:, P * s : P * (s + 1)],
-                        lhsT=part, rhs=ident[:], is_transpose=True,
-                        start=(position == 0), stop=(position == len(parts) - 1),
-                    )
+                    turn(len(parts) * s + position, sum_t_bank[u][:, P * s : P * (s + 1)], part, position == 0, position == len(parts) - 1)
 
         def sum_copy(u):
             n = UNITS[u][1]
@@ -378,9 +377,7 @@ def tile_chainlveg_pa_t_kernel(
             n = UNITS[u][1]
             sum_bank[u] = banks.tile([P, GROUP_ROWS], F32, name="sum_bank", tag="bank")
             for s in range(n):
-                nc.tensor.transpose(
-                    sum_bank[u][:, P * s : P * (s + 1)], sum_t[u][:, P * s : P * (s + 1)], ident[:]
-                )
+                turn(s, sum_bank[u][:, P * s : P * (s + 1)], sum_t[u][:, P * s : P * (s + 1)])
 
         def weight_out(u):
             s0, n = UNITS[u]

import math
from contextlib import ExitStack

import concourse.mybir as mybir
from concourse.masks import make_identity

F32 = mybir.dt.float32
BF16 = mybir.dt.bfloat16
I32 = mybir.dt.int32
U32 = mybir.dt.uint32
U8 = mybir.dt.uint8
FP8X4 = mybir.dt.float8_e4m3fn_x4
ALU = mybir.AluOpType
ACT = mybir.ActivationFunctionType

P = 128
K = 512
ROWS = 4096
SLOTS = ROWS // P
GROUP = 4
GROUP_ROWS = GROUP * P
NL = 8
JTG = 32
JT = 16
WG = NL * JTG
CHUNKS = 2 * WG // P
LOG_2PI = math.log(2.0 * math.pi)

UNITS = [(4 * i, 4) for i in range(8)]
XLOADS = UNITS
ROUNDS = [(0, 1), (2, 3), (4, 5), (6, 7)]
GSL = 5
LNRHO = (1, 3, 5, 6, 7)
XC = {0: "V"}
BASE_T = False
BS = "V"
STE = ""
WS = "S"
BUFS = dict(grouped=2, x_codes=2, x_scales=2, a_t=2, dm=3, nd=4, dw=5, th=4, y=2, mu=3, var=3, ln_rest=3, ln_rho=3, sum_t=2, weight=3, zs=2, ls=2)
ZG = ()
LG = ()
MMR = 0
MMO = 0
START = "X0 Q0 X1 i0 P0 v0 h0 m0 Q1 e0 n0 b0 P1 D0 X2 D1 T0 X3 T1 Q2 Q3"
STEP = "X:-2 Y:0 Z:0 P:-1 LM:0 D:-1 BW:1 T:-1 U:0 Q:-2 C:0 V:0"

FLOPS = 2 * ROWS * K * 2 * WG


def tile_chainlveg_pa_t_kernel(
    tc,
    x,
    s_weight,
    s_mu,
    s_var,
    tcm_w_words,
    tcm_w_scales,
    tcm_b,
    tcv_w_words,
    tcv_w_scales,
    tcv_b,
    out_0,
    out_1,
    out_2,
):
    nc = tc.nc

    x_v = x.flatten_outer_dims().rearrange("(p s) k -> p s k", s=SLOTS)
    sw_v = s_weight.rearrange("b q j e -> (b q) (j e)").rearrange("(p s) n -> p s n", s=SLOTS)
    smu_v = s_mu.rearrange("b q j e g -> (b q) (j e g)").rearrange("(p s) n -> p s n", s=SLOTS)
    svar_v = s_var.rearrange("b q j e g -> (b q) (j e g)").rearrange("(p s) n -> p s n", s=SLOTS)
    scale_v = out_0.rearrange("b q i j t e -> (b q) (i j t e)").rearrange("(p s) n -> p s n", s=SLOTS)
    mu_v = out_1.rearrange("b q i j t e g -> (b q) (i j t e g)").rearrange("(p s) n -> p s n", s=SLOTS)
    var_v = out_2.rearrange("b q i j t e g -> (b q) (i j t e g)").rearrange("(p s) n -> p s n", s=SLOTS)

    with ExitStack() as stack:
        keep = stack.enter_context(tc.tile_pool(name="keep", bufs=1))
        pool_of = {}
        def pools(n):
            if n not in pool_of:
                pool_of[n] = stack.enter_context(tc.tile_pool(name=n, bufs=BUFS.get(n, 2)))
            return pool_of[n]
        banks = stack.enter_context(tc.psum_pool(name="banks", bufs=8))
        stack.enter_context(tc.manual_schedule())

        w_codes = keep.tile([P, 2 * WG], U32, align_bytes=64)
        w_scales = keep.tile([P, 2 * WG], U8, align_bytes=64)
        bias_rows = keep.tile([P, P], BF16)
        half = keep.tile([P, 1], F32)
        ln_2 = keep.tile([P, 1], F32)
        nc.vector.memset(bias_rows[:], 0.0)
        nc.vector.memset(w_scales[:].bitcast(I32), 0)
        nc.vector.memset(half[:], 0.5)
        nc.vector.tensor_scalar(
            out=ln_2[:], in0=half[:], scalar1=0.0, scalar2=math.log(2.0), op0=ALU.mult, op1=ALU.add
        )
        x_sb = keep.tile([P, SLOTS, K], BF16)
        smu_raw = keep.tile([P, SLOTS, NL * 2], BF16)
        svar_raw = keep.tile([P, SLOTS, NL * 2], BF16)
        sw_raw = keep.tile([P, SLOTS, NL], BF16)

        def load_x(first, count):
            nc.sync.dma_start(out=x_sb[:, first : first + count, :], in_=x_v[:, first : first + count, :])

        def load_w(which, words):
            nc.sync.dma_start(
                out=w_codes[:, WG * which : WG * (which + 1)].bitcast(I32),
                in_=words[0].rearrange("p n z -> p (n z)").bitcast(I32),
            )

        nc.scalar.dma_start(out=bias_rows[0:2, :], in_=tcm_b.rearrange("(c n) -> c n", c=2))
        nc.scalar.dma_start(out=bias_rows[2:4, :], in_=tcv_b.rearrange("(c n) -> c n", c=2))
        load_x(*XLOADS[0])
        nc.scalar.dma_start(out=svar_raw[:], in_=svar_v)
        nc.scalar.dma_start(out=smu_raw[:], in_=smu_v)
        warm = keep.tile([P, 1], F32)
        nc.scalar.activation(out=warm[:], in_=half[:], func=ACT.Exp)
        load_w(0, tcm_w_words)
        load_w(1, tcv_w_words)
        load_x(*XLOADS[1])
        for which, scales in enumerate((tcm_w_scales, tcv_w_scales)):
            for quad in range(4):
                nc.sync.dma_start(
                    out=w_scales[32 * quad : 32 * quad + 4, WG * which : WG * (which + 1)].bitcast(I32),
                    in_=scales[0][4 * quad : 4 * quad + 4, :].bitcast(I32),
                )
        nc.sync.dma_start(out=sw_raw[:], in_=sw_v)
        for f, c in XLOADS[2:]:
            load_x(f, c)

        ident = keep.tile([P, P], F32)
        make_identity(nc, ident[:])
        bias_f32 = keep.tile([P, P], F32)
        relu_scale = (-0.5, -0.5, -2.0, -2.0)
        relu_bias = keep.tile([P, CHUNKS], F32)

        def biases():
            nc.vector.tensor_copy(out=bias_f32[:], in_=bias_rows[:])
            bias_bank = banks.tile([P, GROUP_ROWS], F32, name="bias_bank", tag="bank")
            nc.tensor.transpose(bias_bank[:, 0:P], bias_f32[:], ident[:])
            nc.vector.tensor_scalar(
                out=relu_bias[:, 0:2], in0=bias_bank[:, 0:2], scalar1=-0.5, scalar2=0.5, op0=ALU.mult, op1=ALU.add
            )
            nc.vector.tensor_scalar(
                out=relu_bias[:, 2:4], in0=bias_bank[:, 2:4], scalar1=-2.0, scalar2=2.0, op0=ALU.mult, op1=ALU.add
            )

        def natural(ap):
            return ap.rearrange("p (i u g) -> p i u g", i=NL, g=2)

        def split(ap):
            return ap.rearrange("p (g i u) -> p i u g", i=NL, g=2)

        def flat(t, n):
            return t[:, 0:n, :].rearrange("p s n -> p (s n)")

        def state_of(tile_, slot):
            return tile_[:, slot, :].rearrange("p (u g) -> p u g", g=2).unsqueeze(1).to_broadcast([P, NL, JT, 2])

        def spread(engine, dst, src, scale, offset):
            engine.tensor_scalar(
                out=dst[:].rearrange("p s (j t g) -> p (s j) t g", t=2, g=2),
                in0=src[:].rearrange("p s (j g) -> p (s j) g", g=2).unsqueeze(2).to_broadcast([P, SLOTS * NL, 2, 2]),
                scalar1=scale, scalar2=offset, op0=ALU.mult, op1=ALU.add,
            )

        v1 = keep.tile([P, SLOTS, JTG], F32)
        two_less_2v1 = keep.tile([P, SLOTS, JTG], F32)
        m1 = keep.tile([P, SLOTS, JTG], F32)
        half_less_half_m1 = keep.tile([P, SLOTS, JTG], F32)
        two_inv_e1 = keep.tile([P, SLOTS, JTG], F32)
        v1_sum = keep.tile([P, SLOTS * NL], F32)
        base_j = keep.tile([P, SLOTS * NL], F32)
        base = keep.tile([P, SLOTS, JT], F32)
        base_i = keep.tile([P, SLOTS, NL * JT], F32, name="base_i") if BASE_T else None

        def state_exp():
            nc.scalar.activation(
                out=two_inv_e1[:].rearrange("p s (g u) -> p s u g", g=2),
                in_=v1[:].rearrange("p s (u g) -> p s u g", g=2),
                func=ACT.Exp, scale=-2.0, bias=ln_2[:],
            )

        def state_base():
            svar_pairs = svar_raw[:].rearrange("p s (j g) -> p (s j) g", g=2)
            nc.vector.tensor_tensor(out=v1_sum[:], in0=svar_pairs[:, :, 0], in1=svar_pairs[:, :, 1], op=ALU.add)
            nc.vector.tensor_tensor(
                out=base_j[:], in0=sw_raw[:].rearrange("p s j -> p (s j)"), in1=v1_sum[:], op=ALU.subtract
            )
            nc.vector.tensor_scalar(
                out=base[:].rearrange("p s (j t) -> p (s j) t", t=2),
                in0=base_j[:].unsqueeze(2).to_broadcast([P, SLOTS * NL, 2]),
                scalar1=2.0 if BASE_T else 1.0, scalar2=-2 * LOG_2PI if BASE_T else -LOG_2PI, op0=ALU.mult, op1=ALU.add,
            )

        def base_spread():
            BSE = nc.vector if BS == "V" else nc.gpsimd
            BSE.tensor_scalar(
                out=base_i[:].rearrange("p s (i u) -> p s i u", i=NL),
                in0=base[:].unsqueeze(2).to_broadcast([P, SLOTS, NL, JT]),
                scalar1=1.0, scalar2=0.0, op0=ALU.mult, op1=ALU.add,
            )

        grouped = {}; x_codes = {}; x_scales = {}; a_t = {}; dm = {}; nd = {}; dw = {}; th = {}; y = {}
        ln_rest = {}; ln_rho = {}; sum_t_bank = {}; sum_t = {}; sum_bank = {}; zs = {}; ls = {}

        def turn(index, out, in_, start=True, stop=True):
            plain = MMR > 0 and index % MMR == MMO
            nc.tensor.matmul(out=out, lhsT=in_, rhs=ident[:], is_transpose=not plain, start=start, stop=stop)

        def transpose_x(u, copies):
            s0, n = UNITS[u]
            grouped[u] = pools("grouped").tile([P, GROUP_ROWS, 4], BF16, align_bytes=64, name="grouped")
            words_out = (
                grouped[u][:].rearrange("p r z -> p (r z)").bitcast(F32).rearrange("p (r h) -> p r h", h=2)
            )
            x_words = x_sb[:, s0 : s0 + n, :].bitcast(F32)
            for first in range(0, n, 2):
                xt = banks.tile([P, 2, 2 * P], F32, name="xt", tag="bank")
                for s in range(2):
                    for h in range(2):
                        nc.tensor.transpose(
                            xt[:, h, P * s : P * (s + 1)], x_words[:, first + s, h : K // 2 : 2], ident[:]
                        )
                copies[(first // 2) % len(copies)](out=words_out[:, P * first : P * (first + 2), :], in_=xt[:].rearrange("p h r -> p r h"))

        def quantise_x(u):
            n = UNITS[u][1]
            x_codes[u] = pools("x_codes").tile([P, GROUP_ROWS], U32, align_bytes=64, name="x_codes")
            x_scales[u] = pools("x_scales").tile([P, GROUP_ROWS], U8, align_bytes=64, name="x_scales")
            nc.vector.quantize_mx(
                out=x_codes[u][:, 0 : P * n].bitcast(FP8X4),
                scales=x_scales[u][:, 0 : P * n],
                in_=grouped[u][:, 0 : P * n, :].rearrange("p r z -> p (r z)"),
            )

        def project(u):
            n = UNITS[u][1]
            a_t[u] = pools("a_t").tile([P, CHUNKS, GROUP_ROWS], F32, name="a_t")
            for c in range(CHUNKS):
                acc = banks.tile([P, GROUP_ROWS], F32, name="acc", tag="bank")
                nc.tensor.matmul_mx(
                    out=acc[:, 0 : P * n],
                    lhsT=w_codes[:, P * c : P * (c + 1)].bitcast(FP8X4),
                    lhsT_scale=w_scales[:, P * c : P * (c + 1)],
                    rhs=x_codes[u][:, 0 : P * n].bitcast(FP8X4),
                    rhs_scale=x_scales[u][:, 0 : P * n],
                    start=True, stop=True,
                )
                nc.scalar.activation(
                    out=a_t[u][:, c, 0 : P * n], in_=acc[:, 0 : P * n], func=ACT.Relu, bias=relu_bias[:, c : c + 1], scale=relu_scale[c]
                )

        def times_two_inv_e1(engine, u, first, last):
            s0, n = UNITS[u]
            engine.tensor_tensor(
                out=dw[u][:, first:last, :].rearrange("p s (g i u) -> p (s g) i u", g=2, i=NL),
                in0=dm[u][:, first:last, :].rearrange("p s (g i u) -> p (s g) i u", g=2, i=NL),
                in1=two_inv_e1[:, s0 + first : s0 + last, :]
                .rearrange("p s (g u) -> p (s g) u", g=2)
                .unsqueeze(2)
                .to_broadcast([P, 2 * (last - first), NL, JT]),
                op=ALU.mult,
            )

        def gp_slots(u):
            s0, n = UNITS[u]
            return len([s for s in range(s0, s0 + n) if s % 8 < GSL])

        def differences(u):
            s0, n = UNITS[u]
            dm[u] = pools("dm").tile([P, GROUP, WG], F32, name="dm")
            nd[u] = pools("nd").tile([P, GROUP, WG], F32, name="nd")
            dw[u] = pools("dw").tile([P, GROUP, WG], F32, name="dw")
            for s in range(n):
                a_rows = banks.tile([P, 2 * WG], F32, name="a_rows", tag="bank")
                for c in range(CHUNKS):
                    turn(4 * s + c, a_rows[:, P * c : P * (c + 1)], a_t[u][:, c, P * s : P * (s + 1)])
                for dst, start_col, top, state in (
                    (dm[u], 0, 1.0, half_less_half_m1),
                    (nd[u], WG, 4.0, two_less_2v1),
                ):
                    nc.vector.scalar_tensor_tensor(
                        out=split(dst[:, s, :]),
                        in0=natural(a_rows[:, start_col : start_col + WG]),
                        scalar=top,
                        in1=state_of(state, s0 + s),
                        op0=ALU.min,
                        op1=ALU.subtract,
                    )
                if s < gp_slots(u):
                    times_two_inv_e1(nc.gpsimd, u, s, s + 1)

        def tanh(u):
            n = UNITS[u][1]
            th[u] = pools("th").tile([P, GROUP, WG], F32, name="th")
            nc.scalar.activation(out=flat(th[u], n), in_=flat(nd[u], n), func=ACT.Tanh, scale=-0.5)

        def shift(u):
            n = UNITS[u][1]
            y[u] = pools("y").tile([P, GROUP, WG], F32, name="y")
            if gp_slots(u) < n:
                times_two_inv_e1(nc.vector, u, gp_slots(u), n)
            nc.vector.scalar_tensor_tensor(
                out=flat(y[u], n), in0=flat(th[u], n), scalar=1.0, in1=flat(dm[u], n), op0=ALU.subtract, op1=ALU.mult
            )

        def product(u):
            n = UNITS[u][1]
            nc.vector.tensor_tensor(out=flat(dw[u], n), in0=flat(y[u], n), in1=flat(dw[u], n), op=ALU.mult)

        def sum_zz(u):
            s0, n = UNITS[u]
            if u in ZG:
                zs[u] = pools("zs").tile([P, GROUP, WG // 2], F32, name="zs")
                nc.gpsimd.tensor_tensor(out=zs[u][:, 0:n, :], in0=dw[u][:, 0:n, 0:P], in1=dw[u][:, 0:n, P : 2 * P], op=ALU.add)
        def sum_ln(u):
            s0, n = UNITS[u]
            if u in LG:
                ls[u] = pools("ls").tile([P, GROUP, WG // 2], F32, name="ls")
                nc.gpsimd.tensor_tensor(out=ls[u][:, 0:n, :], in0=ln_rho[u][:, 0:n, 0:P], in1=ln_rho[u][:, 0:n, P : 2 * P], op=ALU.add)

        def mean(u):
            s0, n = UNITS[u]
            mu = pools("mu").tile([P, GROUP, WG], F32, name="mu")
            nc.vector.tensor_tensor(
                out=mu[:, 0:n, :].rearrange("p s (i u g) -> p s i u g", i=NL, g=2),
                in0=y[u][:, 0:n, :].rearrange("p s (g i u) -> p s i u g", i=NL, g=2),
                in1=m1[:, s0 : s0 + n, :].rearrange("p s (u g) -> p s u g", g=2).unsqueeze(2).to_broadcast([P, n, NL, JT, 2]),
                op=ALU.add,
            )
            nc.sync.dma_start(out=mu_v[:, s0 : s0 + n, :], in_=mu[:, 0:n, :])

        def logs(u):
            n = UNITS[u][1]
            ln_rest[u] = pools("ln_rest").tile([P, GROUP, WG], F32, name="ln_rest")
            nc.scalar.activation(out=flat(ln_rest[u], n), in_=flat(th[u], n), func=ACT.Ln, bias=half[:], scale=0.5)
            if u in LNRHO:
                ln_rho[u] = pools("ln_rho").tile([P, GROUP, WG], F32, name="ln_rho")
                nc.scalar.activation(out=flat(ln_rho[u], n), in_=flat(th[u], n), func=ACT.Ln, bias=half[:], scale=-0.5)

        def deviation(u):
            s0, n = UNITS[u]
            var = pools("var").tile([P, GROUP, WG], F32, name="var")
            for s in range(n):
                nc.vector.scalar_tensor_tensor(
                    out=natural(var[:, s, :]),
                    in0=split(ln_rest[u][:, s, :]),
                    scalar=0.5,
                    in1=state_of(v1, s0 + s),
                    op0=ALU.mult,
                    op1=ALU.add,
                )
            nc.sync.dma_start(out=var_v[:, s0 : s0 + n, :], in_=var[:, 0:n, :])

        def sum_transposed(u):
            s0, n = UNITS[u]
            terms = (ln_rho[u], dw[u]) if u in LNRHO else (nd[u], ln_rest[u], dw[u])
            sum_t_bank[u] = banks.tile([P, GROUP_ROWS], F32, name="sum_t_bank", tag="bank")
            for s in range(n):
                parts = [term[:, s, P * gauss : P * (gauss + 1)] for term in terms for gauss in range(2)]
                if u in ZG:
                    parts = parts[:-2] + [zs[u][:, s, :]]
                if u in LG:
                    parts = [ls[u][:, s, :]] + parts[2:]
                if BASE_T:
                    parts = [base_i[:, s0 + s, :]] + parts
                for position, part in enumerate(parts):
                    turn(len(parts) * s + position, sum_t_bank[u][:, P * s : P * (s + 1)], part, position == 0, position == len(parts) - 1)

        def sum_copy(u):
            n = UNITS[u][1]
            sum_t[u] = pools("sum_t").tile([P, GROUP_ROWS], F32, name="sum_t")
            nc.scalar.mul(out=sum_t[u][:, 0 : P * n], in_=sum_t_bank[u][:, 0 : P * n], mul=0.5)

        def sum_back(u):
            n = UNITS[u][1]
            sum_bank[u] = banks.tile([P, GROUP_ROWS], F32, name="sum_bank", tag="bank")
            for s in range(n):
                turn(s, sum_bank[u][:, P * s : P * (s + 1)], sum_t[u][:, P * s : P * (s + 1)])

        def weight_out(u):
            s0, n = UNITS[u]
            weight = pools("weight").tile([P, GROUP, WG // 2], F32, name="weight")
            if BASE_T:
                (nc.scalar.copy if WS == "S" else nc.vector.tensor_copy)(out=flat(weight, n), in_=sum_bank[u][:, 0 : P * n])
            else:
                nc.vector.tensor_tensor(
                    out=weight[:, 0:n, :].rearrange("p s (i u) -> p s i u", i=NL),
                    in0=sum_bank[u][:, 0 : P * n].rearrange("p (s i u) -> p s i u", s=n, i=NL),
                    in1=base[:, s0 : s0 + n, :].unsqueeze(2).to_broadcast([P, n, NL, JT]),
                    op=ALU.add,
                )
            nc.sync.dma_start(out=scale_v[:, s0 : s0 + n, :], in_=weight[:, 0:n, :])

        V_, S_ = nc.vector.tensor_copy, nc.scalar.copy
        STAGES = dict(
            X=lambda g: transpose_x(g, XC.get(g, "S") == "V" and [V_] or XC.get(g, "S") == "VS" and [V_, S_] or [S_]),
            Q=quantise_x, P=project, D=differences, T=tanh, Y=shift, Z=lambda g: (product(g), sum_zz(g)), M=mean, L=lambda g: (logs(g), sum_ln(g)), U=sum_transposed,
            C=sum_copy, B=sum_back, W=weight_out, V=deviation,
            e=lambda g: state_exp(), v=lambda g: spread(nc.gpsimd if "v" in STE else nc.vector, v1, svar_raw, 1.0, 0.0),
            n=lambda g: spread(nc.gpsimd if "n" in STE else nc.vector, two_less_2v1, svar_raw, -2.0, 2.0),
            m=lambda g: spread(nc.gpsimd if "m" in STE else nc.vector, m1, smu_raw, 1.0, 0.0),
            h=lambda g: spread(nc.gpsimd if "h" in STE else nc.vector, half_less_half_m1, smu_raw, -0.5, 0.5),
            b=lambda g: state_base(), s=lambda g: base_spread(), i=lambda g: biases(),
        )

        done = set()

        def emit(stage, unit):
            if (stage, unit) not in done:
                done.add((stage, unit))
                STAGES[stage](unit)

        for word in START.split():
            emit(word[0], int(word[1:]))

        for step in range(-4, len(ROUNDS) + 4):
            for word in STEP.split():
                stages, lag = word.split(":")
                if 0 <= step - int(lag) < len(ROUNDS):
                    for unit in ROUNDS[step - int(lag)]:
                        for stage in stages:
                            emit(stage, unit)
